import numpy as np
import ml_dtypes


def mxq(x, axis, fmt="e4m3"):
    dtype, down = {"e4m3": (ml_dtypes.float8_e4m3fn, 7), "e5m2": (ml_dtypes.float8_e5m2, 14)}[fmt]
    v = np.moveaxis(np.asarray(x, np.float32).astype(ml_dtypes.bfloat16).astype(np.float64), axis, -1)
    blocks = v.reshape(v.shape[:-1] + (-1, 32))
    amax = np.abs(blocks).max(-1, keepdims=True)
    byte = np.maximum(np.where(amax > 0, np.frexp(amax)[1] - 1 + 127, 0) - down, 1)
    scale = np.exp2(byte - 127.0)
    codes = (blocks / scale).astype(np.float32).astype(dtype).astype(np.float64)
    return np.moveaxis((codes * scale).reshape(v.shape), -1, axis)


WIDE = False


def mx_kscale(k):
    if not WIDE:
        return np.ones(k)
    levels = np.array([10, -10, 5, -5, 0])
    a = np.random.permutation(np.resize(levels, k // 512 * 4)).reshape(k // 512, 4)
    idx = np.arange(k)
    return np.exp2(a[idx // 512, idx % 128 // 32])


BF16 = ml_dtypes.bfloat16


def bf(x):
    return np.asarray(x, np.float32).astype(BF16)


def f64(x):
    return np.asarray(x).astype(np.float64)


B, H, S, D, P = 2, 8, 1024, 128, 3


def setup_inputs():
    s = mx_kscale(S)
    g = np.exp2(np.round(np.log2(np.mean(s))))
    sign = np.where(np.random.standard_normal((H, 1)) < 0.0, -1.0, 1.0)
    q = np.random.standard_normal((B, H, S, D)) * 1.5
    k = np.random.standard_normal((B, H, S, D))
    v = np.random.standard_normal((B, H, S, D)) * 2.0
    q[..., 0] = 1.0
    k[..., 0] += np.log(s) * np.sqrt(D)
    v = v / s[:, None] * g
    return {
        "q": bf(q),
        "k": bf(k),
        "v": bf(v),
        "qs_s": bf(np.random.uniform(0.0, 1.0, (B, S, P))),
        "ks_s": bf(np.random.uniform(0.0, 1.0, (B, S, P))),
        "alpha": bf(sign * (1.5 + np.random.uniform(0.0, 1.0, (H, 1)))),
        "beta": bf(1.5 + 0.5 * np.random.standard_normal((H, 1))),
    }


def reference(q, k, v, qs_s, ks_s, alpha, beta):
    scale = 1.0 / np.sqrt(D)
    scores = (f64(q) @ f64(k).transpose(0, 1, 3, 2)) * scale
    d_sq = np.sum(np.square(f64(qs_s)[:, :, None, :] - f64(ks_s)[:, None, :, :]), axis=-1)
    a = f64(alpha)[:, 0][None, :, None, None]
    bexp = f64(beta)[:, 0][None, :, None, None]
    bias = a * np.exp(-bexp * d_sq[:, None, :, :])
    z = scores + bias
    e = np.exp(z - z.max(-1, keepdims=True))
    return (mxq(e, 3, "e4m3") @ mxq(f64(v), 2, "e4m3")) / e.sum(-1, keepdims=True)

@@ -1,0 +1,460 @@
+import math
+from contextlib import ExitStack
+
+import concourse.masks as masks
+import concourse.mybir as mybir
+
+FLOPS = 2 * 2 * 16 * 1024 * 1024 * 128
+
+F32 = mybir.dt.float32
+BF16 = mybir.dt.bfloat16
+U32 = mybir.dt.uint32
+U8 = mybir.dt.uint8
+I32 = mybir.dt.int32
+FP8X4 = mybir.dt.float8_e4m3fn_x4
+ALU = mybir.AluOpType
+ACTF = mybir.ActivationFunctionType
+AX = mybir.AxisListType
+
+P = 128
+B = 2
+H = 8
+S = 1024
+D = 128
+NT = 8
+NHEAD = B * H
+NTILES = NHEAD * NT
+RAWB = 4
+PIN = True
+ACT_C_EVERY = 4
+
+
+def tile_rbfbias_kernel(tc, q, k, v, qs_s, ks_s, alpha, beta, out):
+    nc = tc.nc
+    scale = 1.0 / math.sqrt(D)
+    with ExitStack() as ctx:
+        const = ctx.enter_context(tc.tile_pool(name="const", bufs=1))
+        small = ctx.enter_context(tc.tile_pool(name="small", bufs=3))
+        raw = ctx.enter_context(tc.tile_pool(name="raw", bufs=RAWB))
+        work2 = ctx.enter_context(tc.tile_pool(name="work2", bufs=2))
+        work3 = ctx.enter_context(tc.tile_pool(name="work3", bufs=3))
+        upool = ctx.enter_context(tc.tile_pool(name="upool", bufs=4))
+        ps_w = ctx.enter_context(tc.psum_pool(name="ps_w", bufs=4))
+        ps_t = ctx.enter_context(tc.psum_pool(name="ps_t", bufs=3))
+        ps_o = ctx.enter_context(tc.psum_pool(name="ps_o", bufs=1))
+        if PIN:
+            ctx.enter_context(tc.manual_schedule())
+
+        pos = const.tile([P, 4, 32], BF16, name="pos")
+        for b in range(B):
+            nc.sync.dma_start(
+                out=pos[:, b, 0:24].rearrange("p (t f) -> p t f", f=3),
+                in_=qs_s[b].rearrange("(p t) f -> p t f", t=NT),
+            )
+            nc.sync.dma_start(
+                out=pos[:, 2 + b, 0:24].rearrange("p (g j f) -> p g j f", g=2, f=3),
+                in_=ks_s[b].rearrange("(g p j) f -> p g j f", g=2, j=4),
+            )
+        yraw = const.tile([P, 1536], BF16, name="yraw")
+        al_bf = const.tile([P, H], BF16, name="al_bf")
+        be_bf = const.tile([P, H], BF16, name="be_bf")
+        nc.sync.dma_start(out=al_bf[:], in_=alpha.rearrange("h o -> (h o)").partition_broadcast(P))
+        nc.sync.dma_start(out=be_bf[:], in_=beta.rearrange("h o -> (h o)").partition_broadcast(P))
+
+        nc.sync.dma_start(out=yraw[:], in_=ks_s[1, 512:1024, :].rearrange("k f -> (k f)").partition_broadcast(P))
+
+        qr = {}
+        kr = {}
+        vr = {}
+
+        def load(bh):
+            b, h = bh // H, bh % H
+            qr[bh] = raw.tile([P, NT, D], BF16, name="qr", tag="qr")
+            nc.sync.dma_start(out=qr[bh][:], in_=q[b, h].rearrange("(p t) d -> p t d", t=NT))
+            kr[bh] = raw.tile([P, 2, 4, D], BF16, name="kr", tag="kr")
+            nc.sync.dma_start(out=kr[bh][:], in_=k[b, h].rearrange("(g p j) d -> p g j d", g=2, j=4))
+            vr[bh] = raw.tile([P, 2, 4, D], BF16, name="vr", tag="vr")
+            nc.sync.dma_start(out=vr[bh][:], in_=v[b, h].rearrange("(g p j) d -> p g j d", g=2, j=4))
+
+        for bh in range(RAWB):
+            load(bh)
+
+        ident_bf = const.tile([P, P], BF16, name="ident_bf")
+        masks.make_identity(nc, ident_bf[:])
+        ident_f = const.tile([P, P], F32, name="ident_f")
+        masks.make_identity(nc, ident_f[:])
+
+        feat = const.tile([P, 4, NT, P], BF16, name="feat")
+        nc.vector.memset(feat[:], 0.0)
+
+        al = const.tile([P, H], F32, name="al")
+        nc.vector.tensor_copy(out=al[:], in_=al_bf[:])
+        sgn = const.tile([P, H], F32, name="sgn")
+        nc.vector.tensor_scalar(out=sgn[:], in0=al[:], scalar1=0.0, scalar2=2.0, op0=ALU.is_ge, op1=ALU.mult)
+        nc.vector.tensor_scalar(out=sgn[:], in0=sgn[:], scalar1=-1.0, scalar2=None, op0=ALU.add)
+        absa = const.tile([P, H], F32, name="absa")
+        nc.vector.tensor_tensor(out=absa[:], in0=al[:], in1=sgn[:], op=ALU.mult)
+        nc.vector.tensor_scalar(
+            out=absa[:], in0=absa[:], scalar1=math.sqrt(D), scalar2=2.0 ** -60, op0=ALU.mult, op1=ALU.max
+        )
+        lna = const.tile([P, H], F32, name="lna")
+        nc.scalar.activation(out=lna[:], in_=absa[:], func=ACTF.Ln)
+        nbeta = const.tile([P, H], F32, name="nbeta")
+        nc.vector.tensor_scalar(out=nbeta[:], in0=be_bf[:], scalar1=-1.0, scalar2=None, op0=ALU.mult)
+        scpos = const.tile([P, H], F32, name="scpos")
+        nc.vector.tensor_scalar(out=scpos[:], in0=sgn[:], scalar1=scale, scalar2=None, op0=ALU.mult)
+        scneg = const.tile([P, H], F32, name="scneg")
+        nc.vector.tensor_scalar(out=scneg[:], in0=sgn[:], scalar1=-scale, scalar2=None, op0=ALU.mult)
+
+        xf = const.tile([P, 4, 24], F32, name="xf")
+        nc.vector.tensor_copy(out=xf[:], in_=pos[:, :, 0:24])
+        sq = const.tile([P, 4, 24], F32, name="sq")
+        nc.vector.tensor_tensor(out=sq[:], in0=xf[:], in1=xf[:], op=ALU.mult)
+        s2 = const.tile([P, 4, NT], F32, name="s2")
+        nc.vector.tensor_reduce(
+            out=s2[:], in_=sq[:].rearrange("p w (t f) -> p w t f", f=3), axis=AX.X, op=ALU.add
+        )
+        rem = s2
+        m2x = const.tile([P, 24], F32, name="m2x")
+        nc.vector.tensor_scalar(out=m2x[:], in0=xf[:, 1, :], scalar1=-2.0, scalar2=None, op0=ALU.mult)
+        nc.vector.tensor_scalar(
+            out=feat[:, 0:2, :, 0:3],
+            in0=xf[:, 0:2, :].rearrange("p w (t f) -> p w t f", f=3),
+            scalar1=-2.0,
+            scalar2=None,
+            op0=ALU.mult,
+        )
+        nc.vector.tensor_copy(out=feat[:, 2:4, :, 0:3], in_=xf[:, 2:4, :].rearrange("p w (t f) -> p w t f", f=3))
+        nc.vector.memset(feat[:, 0:2, :, 6:9], 1.0)
+        nc.vector.memset(feat[:, 2:4, :, 3:6], 1.0)
+        for i in range(3):
+            part = const.tile([P, 4, NT], BF16, name="part%d" % i)
+            nc.vector.tensor_copy(out=part[:], in_=rem[:])
+            nc.vector.tensor_copy(out=feat[:, 0:2, :, 3 + i], in_=part[:, 0:2, :])
+            nc.vector.tensor_copy(out=feat[:, 2:4, :, 6 + i], in_=part[:, 2:4, :])
+            if i < 2:
+                nxt = const.tile([P, 4, NT], F32, name="rem%d" % (i + 1))
+                nc.vector.tensor_tensor(out=nxt[:], in0=rem[:], in1=part[:], op=ALU.subtract)
+                rem = nxt
+
+        featT = []
+        for w in (0, 2, 1, 3):
+            tp = ps_t.tile([P, NT, P], BF16, name="tp", tag="t")
+            for t in range(NT):
+                nc.tensor.transpose(out=tp[:, t, :], in_=feat[:, w, t, :], identity=ident_bf[:])
+            ft = const.tile([P, NT * P], BF16, name="featT%d" % w)
+            if w < 2:
+                nc.vector.tensor_copy(out=ft[:], in_=tp[:].rearrange("p t c -> p (t c)"))
+            else:
+                nc.scalar.copy(out=ft[:], in_=tp[:].rearrange("p t c -> p (t c)"))
+            featT.append((w, ft))
+        featT = dict(featT)
+
+        dT = [const.tile([P, NT, S], F32, name="dT%d" % b) for b in range(B)]
+
+        def dist_tile(b, half, c, pool, tag, on_act):
+            dps = pool.tile([P, 512], F32, name="dps", tag=tag)
+            nc.tensor.matmul(
+                out=dps[:],
+                lhsT=featT[2 + b][:, c * P : (c + 1) * P],
+                rhs=featT[b][:, half * 512 : (half + 1) * 512],
+                start=True,
+                stop=True,
+            )
+            dst = dT[b][:, c, half * 512 : (half + 1) * 512]
+            if on_act:
+                nc.scalar.copy(out=dst, in_=dps[:])
+            else:
+                nc.vector.tensor_copy(out=dst, in_=dps[:])
+
+        for c in range(NT):
+            dist_tile(0, 0, c, ps_w, "w", c % 2 == 1)
+
+        yv = yraw[:].rearrange("x (p j f) -> x f j p", j=4, f=3)
+        uu = {}
+
+        def u_tile(t):
+            uu[t] = upool.tile([P, 3, 512], F32, name="uu", tag="uu")
+            for f in range(3):
+                nc.gpsimd.tensor_scalar(
+                    out=uu[t][:, f, :].rearrange("x (j p) -> x j p", j=4),
+                    in0=yv[:, f],
+                    scalar1=m2x[:, t * 3 + f : t * 3 + f + 1],
+                    scalar2=(s2[:, 1, t : t + 1] if f == 0 else 0.0),
+                    op0=ALU.mult,
+                    op1=ALU.add,
+                )
+
+        def dist_tile_sp(half, c):
+            dps = ps_t.tile([P, 512], F32, name="dps", tag="t")
+            for tq in range(4):
+                for f in range(3):
+                    nc.tensor.matmul(
+                        out=dps[:, tq * P : (tq + 1) * P],
+                        lhsT=uu[half * 4 + tq][:, f, (c - 4) * P : (c - 3) * P],
+                        rhs=ident_f[:],
+                        is_transpose=True,
+                        start=(tq == 0 and f == 0),
+                        stop=(tq == 3 and f == 2),
+                    )
+            nc.vector.tensor_scalar(
+                out=dT[1][:, c, half * 512 : (half + 1) * 512],
+                in0=dps[:],
+                scalar1=s2[:, 3, c : c + 1],
+                scalar2=None,
+                op0=ALU.add,
+            )
+
+        for t in range(4):
+            u_tile(t)
+
+        qT = {}
+        kT = {}
+        vc = {}
+        vs = {}
+        vg = {}
+        et = {}
+        wt = {}
+        nb = {}
+        nb0 = {}
+        ee = {}
+        eT = {}
+        gr = {}
+        ec = {}
+        es = {}
+        rs = {}
+        rinv = {}
+        rsum = {}
+        osb = {}
+
+        def trans_q(bh):
+            h = bh % H
+            tp = ps_t.tile([P, NT, P], BF16, name="tp", tag="t")
+            for t in range(NT):
+                nc.tensor.transpose(out=tp[:, t, :], in_=qr[bh][:, t, :], identity=ident_bf[:])
+            qT[bh] = work2.tile([P, NT * P], BF16, name="qT", tag="qT")
+            nc.scalar.activation(
+                out=qT[bh][:], in_=tp[:].rearrange("p t c -> p (t c)"), func=ACTF.Copy, scale=sgn[:, h : h + 1]
+            )
+
+        def trans_k(bh):
+            tp = ps_t.tile([P, NT, P], BF16, name="tp", tag="t")
+            for c in range(NT):
+                nc.tensor.transpose(out=tp[:, c, :], in_=kr[bh][:, c // 4, c % 4, :], identity=ident_bf[:])
+            kT[bh] = work2.tile([P, NT * P], BF16, name="kT", tag="kT")
+            nc.vector.tensor_copy(out=kT[bh][:], in_=tp[:].rearrange("p t c -> p (t c)"))
+
+        def v_group(bh):
+            vg[bh] = work2.tile([P, 2, D, 4], BF16, name="vg", tag="vg", align_bytes=64)
+            nc.gpsimd.tensor_scalar(
+                out=vg[bh][:],
+                in0=vr[bh][:].rearrange("p g j d -> p g d j"),
+                scalar1=1.0,
+                scalar2=0.0,
+                op0=ALU.mult,
+                op1=ALU.add,
+            )
+
+        def v_quant(bh):
+            vc[bh] = work2.tile([P, 2 * D], U32, name="vc", tag="vc", align_bytes=64)
+            vs[bh] = work2.tile([P, 2 * D], U8, name="vs", tag="vs", align_bytes=64)
+            nc.vector.quantize_mx(
+                out=vc[bh][:].bitcast(FP8X4), scales=vs[bh][:], in_=vg[bh][:].rearrange("p g d j -> p (g d j)")
+            )
+
+        def x1(tau):
+            bh, t = tau // NT, tau % NT
+            b, h = bh // H, bh % H
+            et[tau] = work3.tile([P, NT, P], F32, name="et", tag="et")
+            nc.scalar.activation(
+                out=et[tau][:],
+                in_=dT[b][:, :, t * P : (t + 1) * P],
+                func=ACTF.Exp,
+                scale=nbeta[:, h : h + 1],
+                bias=lna[:, h : h + 1],
+            )
+
+        def wmm(tau):
+            bh, t = tau // NT, tau % NT
+            wt[tau] = []
+            for g in range(2):
+                wg = ps_w.tile([P, 512], F32, name="wg", tag="w")
+                nc.tensor.matmul(
+                    out=wg[:],
+                    lhsT=qT[bh][:, t * P : (t + 1) * P],
+                    rhs=kT[bh][:, g * 512 : (g + 1) * 512],
+                    start=True,
+                    stop=False,
+                )
+                for j in range(4):
+                    nc.tensor.matmul(
+                        out=wg[:, j * P : (j + 1) * P],
+                        lhsT=et[tau][:, g * 4 + j, :],
+                        rhs=ident_f[:],
+                        is_transpose=True,
+                        start=False,
+                        stop=(j == 3),
+                    )
+                wt[tau].append(wg)
+
+        def m_half(tau, g):
+            h = (tau // NT) % H
+            junk = work2.tile([P, 512], BF16, name="junk", tag="junk")
+            if g == 0:
+                nb0[tau] = small.tile([P, 1], F32, name="nb0", tag="nb0")
+                nc.vector.tensor_scalar(
+                    out=junk[:],
+                    in0=wt[tau][0][:],
+                    scalar1=scneg[:, h : h + 1],
+                    scalar2=None,
+                    op0=ALU.mult,
+                    op1=ALU.min,
+                    accum_out=nb0[tau][:],
+                )
+            else:
+                nb[tau] = small.tile([P, 1], F32, name="nb", tag="nb")
+                nc.vector.tensor_scalar(
+                    out=junk[:],
+                    in0=wt[tau][1][:],
+                    scalar1=scneg[:, h : h + 1],
+                    scalar2=nb0[tau][:],
+                    op0=ALU.mult,
+                    op1=ALU.min,
+                    accum_out=nb[tau][:],
+                )
+
+        def x2(tau):
+            bh, t = tau // NT, tau % NT
+            h = bh % H
+            if t == 0:
+                rs[bh] = work2.tile([P, NT, 2], F32, name="rs", tag="rs")
+            ee[tau] = work3.tile([P, S], BF16, name="ee", tag="ee")
+            for g in range(2):
+                nc.scalar.activation(
+                    out=ee[tau][:, g * 512 : (g + 1) * 512],
+                    in_=wt[tau][g][:],
+                    func=ACTF.Exp,
+                    scale=scpos[:, h : h + 1],
+                    bias=nb[tau][:],
+                    accum_out=rs[bh][:, t, g : g + 1],
+                )
+
+        def te(tau):
+            eT[tau] = ps_t.tile([P, NT, P], BF16, name="eT", tag="t")
+            for c in range(NT):
+                nc.tensor.transpose(out=eT[tau][:, c, :], in_=ee[tau][:, c * P : (c + 1) * P], identity=ident_bf[:])
+
+        def regroup(tau):
+            gr[tau] = work2.tile([P, 2, P, 4], BF16, name="gr", tag="gr", align_bytes=64)
+            src = eT[tau][:].rearrange("p (g j) c -> p g c j", j=4)
+            if tau % ACT_C_EVERY == ACT_C_EVERY - 1:
+                nc.scalar.copy(out=gr[tau][:], in_=src)
+            else:
+                nc.vector.tensor_copy(out=gr[tau][:], in_=src)
+
+        def quant(tau):
+            u, i = tau // 4, tau % 4
+            if i == 0:
+                ec[u] = work2.tile([P, 4, 2 * P], U32, name="ec", tag="ec", align_bytes=64)
+                es[u] = work2.tile([P, 4, 2 * P], U8, name="es", tag="es", align_bytes=64)
+            nc.vector.quantize_mx(
+                out=ec[u][:, i, :].bitcast(FP8X4),
+                scales=es[u][:, i, :],
+                in_=gr[tau][:].rearrange("p g c j -> p (g c j)"),
+            )
+
+        def r_sum(u):
+            bh, uu = u // 2, u % 2
+            rsum[u] = small.tile([P, 4], F32, name="rsum", tag="rsum")
+            nc.vector.tensor_reduce(out=rsum[u][:], in_=rs[bh][:, uu * 4 : uu * 4 + 4, :], axis=AX.X, op=ALU.add)
+
+        def r_inv(u):
+            rinv[u] = small.tile([P, 4], F32, name="rinv", tag="rinv")
+            nc.vector.reciprocal(out=rinv[u][:], in_=rsum[u][:])
+
+        ob = {}
+
+        def mxg(u):
+            bh = u // 2
+            ob[u] = ps_o.tile([P, 4, D], F32, name="ob", tag="o")
+            for i in range(4):
+                for g in range(2):
+                    nc.tensor.matmul_mx(
+                        out=ob[u][:, i, :],
+                        lhsT=ec[u][:, i, g * P : (g + 1) * P].bitcast(FP8X4),
+                        lhsT_scale=es[u][:, i, g * P : (g + 1) * P],
+                        rhs=vc[bh][:, g * D : (g + 1) * D].bitcast(FP8X4),
+                        rhs_scale=vs[bh][:, g * D : (g + 1) * D],
+                        start=(g == 0),
+                        stop=(g == 1),
+                    )
+
+        def norm(u):
+            bh, uu = u // 2, u % 2
+            b, h = bh // H, bh % H
+            if uu == 0:
+                osb[bh] = work2.tile([P, NT, D], F32, name="osb", tag="osb")
+            dst = osb[bh][:, uu * 4 : uu * 4 + 4, :]
+            nc.vector.tensor_tensor(
+                out=dst, in0=ob[u][:], in1=rinv[u][:].unsqueeze(2).to_broadcast([P, 4, D]), op=ALU.mult
+            )
+            nc.sync.dma_start(
+                out=out[b, h].rearrange("(p t) d -> p t d", t=NT)[:, uu * 4 : uu * 4 + 4, :], in_=dst
+            )
+
+        trans_q(0)
+        trans_k(0)
+        v_group(0)
+
+        def ok(tau):
+            return 0 <= tau < NTILES
+
+        for n in range(-3, NTILES + 6):
+            if ok(n):
+                x2(n)
+            if ok(n - 1):
+                te(n - 1)
+            if (n - 5) % 4 == 0 and 0 <= (n - 5) // 4 < NTILES // 4:
+                mxg((n - 5) // 4)
+            if ok(n + 1):
+                m_half(n + 1, 0)
+            if (n - 4) % 4 == 0 and 0 <= (n - 4) // 4 < NTILES // 4:
+                r_sum((n - 4) // 4)
+            if ok(n - 1):
+                regroup(n - 1)
+            if ok(n + 3):
+                x1(n + 3)
+            if (n + 4) % NT == 0 and 1 <= (n + 4) // NT < NHEAD:
+                trans_q((n + 4) // NT)
+            if (n + 3) % NT == 0 and 1 <= (n + 3) // NT < NHEAD:
+                trans_k((n + 3) // NT)
+            if ok(n + 2):
+                wmm(n + 2)
+            if (n + 2) % NT == 0 and 1 <= (n + 2) // NT < NHEAD:
+                v_group((n + 2) // NT)
+            if ok(n + 1):
+                m_half(n + 1, 1)
+            if (n - 4) % 4 == 0 and 0 <= (n - 4) // 4 < NTILES // 4:
+                r_inv((n - 4) // 4)
+            if ok(n - 1):
+                quant(n - 1)
+            if n % NT == 0 and 0 <= n // NT < NHEAD:
+                v_quant(n // NT)
+            if (n - 5) % 4 == 0 and 0 <= (n - 5) // 4 < NTILES // 4:
+                norm((n - 5) // 4)
+            if (n + 1) % NT == 0 and 0 <= (n + 1) // NT and (n + 1) // NT + RAWB < NHEAD:
+                load((n + 1) // NT + RAWB)
+            if n == -3 or n == -2:
+                for c in range(4):
+                    dist_tile(0, 1, (n + 3) * 4 + c, ps_t, "t", False)
+            if -1 <= n <= 2:
+                for rep in range(2):
+                    i = (n + 1) * 2 + rep
+                    dist_tile(1, i // 4, i % 4, ps_t, "t", False)
+            if 3 <= n <= 6:
+                for rep in range(2):
+                    i = (n - 3) * 2 + rep
+                    dist_tile_sp(i // 4, 4 + i % 4)
+            if n == 4:
+                for t in range(4, 8):
+                    u_tile(t)

@@ -26,6 +26,7 @@ NHEAD = B * H
 NTILES = NHEAD * NT
 RAWB = 4
 PIN = True
+N_IDLE = 1
 ACT_C_EVERY = 4
 
 
@@ -83,6 +84,23 @@ def tile_rbfbias_kernel(tc, q, k, v, qs_s, ks_s, alpha, beta, out):
         masks.make_identity(nc, ident_bf[:])
         ident_f = const.tile([P, P], F32, name="ident_f")
         masks.make_identity(nc, ident_f[:])
+
+        dsrc = const.tile([P, 2048], BF16, name="dsrc", align_bytes=64)
+        nc.vector.memset(dsrc[:], 1.0)
+        dcode = const.tile([P, 512], U32, name="dcode", align_bytes=64)
+        dscl = const.tile([P, 512], U8, name="dscl", align_bytes=64)
+        nc.vector.quantize_mx(out=dcode[:].bitcast(FP8X4), scales=dscl[:], in_=dsrc[:])
+
+        def idle_pass(bank):
+            nc.tensor.matmul_mx(
+                out=bank,
+                lhsT=dcode[:, 0:P].bitcast(FP8X4),
+                lhsT_scale=dscl[:, 0:P],
+                rhs=dcode[:].bitcast(FP8X4),
+                rhs_scale=dscl[:],
+                start=True,
+                stop=True,
+            )
 
         feat = const.tile([P, 4, NT, P], BF16, name="feat")
         nc.vector.memset(feat[:], 0.0)
@@ -279,6 +297,8 @@ def tile_rbfbias_kernel(tc, q, k, v, qs_s, ks_s, alpha, beta, out):
             wt[tau] = []
             for g in range(2):
                 wg = ps_w.tile([P, 512], F32, name="wg", tag="w")
+                if g < N_IDLE:
+                    idle_pass(wg[:])
                 nc.tensor.matmul(
                     out=wg[:],
                     lhsT=qT[bh][:, t * P : (t + 1) * P],

@@ -26,8 +26,7 @@ NHEAD = B * H
 NTILES = NHEAD * NT
 RAWB = 4
 PIN = True
-N_IDLE = 1
-ACT_C_EVERY = 4
+ACT_C_EVERY = 3
 
 
 def tile_rbfbias_kernel(tc, q, k, v, qs_s, ks_s, alpha, beta, out):
@@ -40,8 +39,10 @@ def tile_rbfbias_kernel(tc, q, k, v, qs_s, ks_s, alpha, beta, out):
         work2 = ctx.enter_context(tc.tile_pool(name="work2", bufs=2))
         work3 = ctx.enter_context(tc.tile_pool(name="work3", bufs=3))
         upool = ctx.enter_context(tc.tile_pool(name="upool", bufs=4))
-        ps_w = ctx.enter_context(tc.psum_pool(name="ps_w", bufs=4))
+        work4 = ctx.enter_context(tc.tile_pool(name="work4", bufs=4))
+        ps_w = ctx.enter_context(tc.psum_pool(name="ps_w", bufs=3))
         ps_t = ctx.enter_context(tc.psum_pool(name="ps_t", bufs=3))
+        ps_q = ctx.enter_context(tc.psum_pool(name="ps_q", bufs=1))
         ps_o = ctx.enter_context(tc.psum_pool(name="ps_o", bufs=1))
         if PIN:
             ctx.enter_context(tc.manual_schedule())
@@ -85,23 +86,6 @@ def tile_rbfbias_kernel(tc, q, k, v, qs_s, ks_s, alpha, beta, out):
         ident_f = const.tile([P, P], F32, name="ident_f")
         masks.make_identity(nc, ident_f[:])
 
-        dsrc = const.tile([P, 2048], BF16, name="dsrc", align_bytes=64)
-        nc.vector.memset(dsrc[:], 1.0)
-        dcode = const.tile([P, 512], U32, name="dcode", align_bytes=64)
-        dscl = const.tile([P, 512], U8, name="dscl", align_bytes=64)
-        nc.vector.quantize_mx(out=dcode[:].bitcast(FP8X4), scales=dscl[:], in_=dsrc[:])
-
-        def idle_pass(bank):
-            nc.tensor.matmul_mx(
-                out=bank,
-                lhsT=dcode[:, 0:P].bitcast(FP8X4),
-                lhsT_scale=dscl[:, 0:P],
-                rhs=dcode[:].bitcast(FP8X4),
-                rhs_scale=dscl[:],
-                start=True,
-                stop=True,
-            )
-
         feat = const.tile([P, 4, NT, P], BF16, name="feat")
         nc.vector.memset(feat[:], 0.0)
 
@@ -119,8 +103,6 @@ def tile_rbfbias_kernel(tc, q, k, v, qs_s, ks_s, alpha, beta, out):
         nc.scalar.activation(out=lna[:], in_=absa[:], func=ACTF.Ln)
         nbeta = const.tile([P, H], F32, name="nbeta")
         nc.vector.tensor_scalar(out=nbeta[:], in0=be_bf[:], scalar1=-1.0, scalar2=None, op0=ALU.mult)
-        scpos = const.tile([P, H], F32, name="scpos")
-        nc.vector.tensor_scalar(out=scpos[:], in0=sgn[:], scalar1=scale, scalar2=None, op0=ALU.mult)
         scneg = const.tile([P, H], F32, name="scneg")
         nc.vector.tensor_scalar(out=scneg[:], in0=sgn[:], scalar1=-scale, scalar2=None, op0=ALU.mult)
 
@@ -204,7 +186,7 @@ def tile_rbfbias_kernel(tc, q, k, v, qs_s, ks_s, alpha, beta, out):
                 )
 
         def dist_tile_sp(half, c):
-            dps = ps_t.tile([P, 512], F32, name="dps", tag="t")
+            dps = ps_o.tile([P, 512], F32, name="dps", tag="o")
             for tq in range(4):
                 for f in range(3):
                     nc.tensor.matmul(
@@ -235,6 +217,7 @@ def tile_rbfbias_kernel(tc, q, k, v, qs_s, ks_s, alpha, beta, out):
         wt = {}
         nb = {}
         nb0 = {}
+        zt = {}
         ee = {}
         eT = {}
         gr = {}
@@ -242,12 +225,11 @@ def tile_rbfbias_kernel(tc, q, k, v, qs_s, ks_s, alpha, beta, out):
         es = {}
         rs = {}
         rinv = {}
-        rsum = {}
         osb = {}
 
         def trans_q(bh):
             h = bh % H
-            tp = ps_t.tile([P, NT, P], BF16, name="tp", tag="t")
+            tp = ps_q.tile([P, NT, P], BF16, name="tq", tag="tq")
             for t in range(NT):
                 nc.tensor.transpose(out=tp[:, t, :], in_=qr[bh][:, t, :], identity=ident_bf[:])
             qT[bh] = work2.tile([P, NT * P], BF16, name="qT", tag="qT")
@@ -256,7 +238,7 @@ def tile_rbfbias_kernel(tc, q, k, v, qs_s, ks_s, alpha, beta, out):
             )
 
         def trans_k(bh):
-            tp = ps_t.tile([P, NT, P], BF16, name="tp", tag="t")
+            tp = ps_q.tile([P, NT, P], BF16, name="tq", tag="tq")
             for c in range(NT):
                 nc.tensor.transpose(out=tp[:, c, :], in_=kr[bh][:, c // 4, c % 4, :], identity=ident_bf[:])
             kT[bh] = work2.tile([P, NT * P], BF16, name="kT", tag="kT")
@@ -297,8 +279,6 @@ def tile_rbfbias_kernel(tc, q, k, v, qs_s, ks_s, alpha, beta, out):
             wt[tau] = []
             for g in range(2):
                 wg = ps_w.tile([P, 512], F32, name="wg", tag="w")
-                if g < N_IDLE:
-                    idle_pass(wg[:])
                 nc.tensor.matmul(
                     out=wg[:],
                     lhsT=qT[bh][:, t * P : (t + 1) * P],
@@ -319,11 +299,11 @@ def tile_rbfbias_kernel(tc, q, k, v, qs_s, ks_s, alpha, beta, out):
 
         def m_half(tau, g):
             h = (tau // NT) % H
-            junk = work2.tile([P, 512], BF16, name="junk", tag="junk")
             if g == 0:
+                zt[tau] = work4.tile([P, S], F32, name="zt", tag="zt")
                 nb0[tau] = small.tile([P, 1], F32, name="nb0", tag="nb0")
                 nc.vector.tensor_scalar(
-                    out=junk[:],
+                    out=zt[tau][:, 0:512],
                     in0=wt[tau][0][:],
                     scalar1=scneg[:, h : h + 1],
                     scalar2=None,
@@ -332,9 +312,9 @@ def tile_rbfbias_kernel(tc, q, k, v, qs_s, ks_s, alpha, beta, out):
                     accum_out=nb0[tau][:],
                 )
             else:
-                nb[tau] = small.tile([P, 1], F32, name="nb", tag="nb")
+                nb[tau] = work4.tile([P, 1], F32, name="nb", tag="nb")
                 nc.vector.tensor_scalar(
-                    out=junk[:],
+                    out=zt[tau][:, 512:1024],
                     in0=wt[tau][1][:],
                     scalar1=scneg[:, h : h + 1],
                     scalar2=nb0[tau][:],
@@ -345,19 +325,17 @@ def tile_rbfbias_kernel(tc, q, k, v, qs_s, ks_s, alpha, beta, out):
 
         def x2(tau):
             bh, t = tau // NT, tau % NT
-            h = bh % H
             if t == 0:
-                rs[bh] = work2.tile([P, NT, 2], F32, name="rs", tag="rs")
+                rs[bh] = work2.tile([P, NT], F32, name="rs", tag="rs")
             ee[tau] = work3.tile([P, S], BF16, name="ee", tag="ee")
-            for g in range(2):
-                nc.scalar.activation(
-                    out=ee[tau][:, g * 512 : (g + 1) * 512],
-                    in_=wt[tau][g][:],
-                    func=ACTF.Exp,
-                    scale=scpos[:, h : h + 1],
-                    bias=nb[tau][:],
-                    accum_out=rs[bh][:, t, g : g + 1],
-                )
+            nc.scalar.activation(
+                out=ee[tau][:],
+                in_=zt[tau][:],
+                func=ACTF.Exp,
+                scale=-1.0,
+                bias=nb[tau][:],
+                accum_out=rs[bh][:, t : t + 1],
+            )
 
         def te(tau):
             eT[tau] = ps_t.tile([P, NT, P], BF16, name="eT", tag="t")
@@ -365,9 +343,9 @@ def tile_rbfbias_kernel(tc, q, k, v, qs_s, ks_s, alpha, beta, out):
                 nc.tensor.transpose(out=eT[tau][:, c, :], in_=ee[tau][:, c * P : (c + 1) * P], identity=ident_bf[:])
 
         def regroup(tau):
-            gr[tau] = work2.tile([P, 2, P, 4], BF16, name="gr", tag="gr", align_bytes=64)
+            gr[tau] = work3.tile([P, 2, P, 4], BF16, name="gr", tag="gr", align_bytes=64)
             src = eT[tau][:].rearrange("p (g j) c -> p g c j", j=4)
-            if tau % ACT_C_EVERY == ACT_C_EVERY - 1:
+            if tau % ACT_C_EVERY == 1:
                 nc.scalar.copy(out=gr[tau][:], in_=src)
             else:
                 nc.vector.tensor_copy(out=gr[tau][:], in_=src)
@@ -375,22 +353,18 @@ def tile_rbfbias_kernel(tc, q, k, v, qs_s, ks_s, alpha, beta, out):
         def quant(tau):
             u, i = tau // 4, tau % 4
             if i == 0:
-                ec[u] = work2.tile([P, 4, 2 * P], U32, name="ec", tag="ec", align_bytes=64)
-                es[u] = work2.tile([P, 4, 2 * P], U8, name="es", tag="es", align_bytes=64)
+                ec[u] = work3.tile([P, 4, 2 * P], U32, name="ec", tag="ec", align_bytes=64)
+                es[u] = work3.tile([P, 4, 2 * P], U8, name="es", tag="es", align_bytes=64)
             nc.vector.quantize_mx(
                 out=ec[u][:, i, :].bitcast(FP8X4),
                 scales=es[u][:, i, :],
                 in_=gr[tau][:].rearrange("p g c j -> p (g c j)"),
             )
 
-        def r_sum(u):
-            bh, uu = u // 2, u % 2
-            rsum[u] = small.tile([P, 4], F32, name="rsum", tag="rsum")
-            nc.vector.tensor_reduce(out=rsum[u][:], in_=rs[bh][:, uu * 4 : uu * 4 + 4, :], axis=AX.X, op=ALU.add)
-
         def r_inv(u):
+            bh, uu = u // 2, u % 2
             rinv[u] = small.tile([P, 4], F32, name="rinv", tag="rinv")
-            nc.vector.reciprocal(out=rinv[u][:], in_=rsum[u][:])
+            nc.vector.reciprocal(out=rinv[u][:], in_=rs[bh][:, uu * 4 : uu * 4 + 4])
 
         ob = {}
 
@@ -429,52 +403,60 @@ def tile_rbfbias_kernel(tc, q, k, v, qs_s, ks_s, alpha, beta, out):
         def ok(tau):
             return 0 <= tau < NTILES
 
-        for n in range(-3, NTILES + 6):
+        def grp(x):
+            return x // 4 if (x % 4 == 3 and 0 <= x < NTILES) else -1
+
+        def head(x):
+            return x // NT if (x % NT == 0 and NT <= x < NTILES) else -1
+
+        d1_todo = (
+            [(1, 0, c) for c in range(4, 8)]
+            + [(0, half, c) for half in range(2) for c in range(4)]
+            + [(1, 1, c) for c in range(4, 8)]
+        )
+
+        for n in range(-4, NTILES + 8):
             if ok(n):
                 x2(n)
             if ok(n - 1):
                 te(n - 1)
-            if (n - 5) % 4 == 0 and 0 <= (n - 5) // 4 < NTILES // 4:
-                mxg((n - 5) // 4)
-            if ok(n + 1):
-                m_half(n + 1, 0)
-            if (n - 4) % 4 == 0 and 0 <= (n - 4) // 4 < NTILES // 4:
-                r_sum((n - 4) // 4)
-            if ok(n - 1):
-                regroup(n - 1)
-            if ok(n + 3):
-                x1(n + 3)
-            if (n + 4) % NT == 0 and 1 <= (n + 4) // NT < NHEAD:
-                trans_q((n + 4) // NT)
-            if (n + 3) % NT == 0 and 1 <= (n + 3) // NT < NHEAD:
-                trans_k((n + 3) // NT)
+            if grp(n - 4) >= 0:
+                mxg(grp(n - 4))
             if ok(n + 2):
-                wmm(n + 2)
-            if (n + 2) % NT == 0 and 1 <= (n + 2) // NT < NHEAD:
-                v_group((n + 2) // NT)
-            if ok(n + 1):
-                m_half(n + 1, 1)
-            if (n - 4) % 4 == 0 and 0 <= (n - 4) // 4 < NTILES // 4:
-                r_inv((n - 4) // 4)
-            if ok(n - 1):
-                quant(n - 1)
-            if n % NT == 0 and 0 <= n // NT < NHEAD:
-                v_quant(n // NT)
-            if (n - 5) % 4 == 0 and 0 <= (n - 5) // 4 < NTILES // 4:
-                norm((n - 5) // 4)
+                m_half(n + 2, 0)
+            if ok(n - 3):
+                quant(n - 3)
+            if ok(n + 4):
+                x1(n + 4)
+            if head(n + 5) >= 0:
+                trans_q(head(n + 5))
+            if head(n + 4) >= 0:
+                trans_k(head(n + 4))
+            if ok(n + 3):
+                wmm(n + 3)
+            if head(n + 2) >= 0:
+                v_group(head(n + 2))
+            if ok(n + 2):
+                m_half(n + 2, 1)
+            if grp(n - 2) >= 0:
+                r_inv(grp(n - 2))
+            if ok(n - 2):
+                regroup(n - 2)
+            if n == 2 or head(n - 2) >= 0:
+                v_quant((n - 2) // NT)
+            if grp(n - 4) >= 0:
+                norm(grp(n - 4))
             if (n + 1) % NT == 0 and 0 <= (n + 1) // NT and (n + 1) // NT + RAWB < NHEAD:
                 load((n + 1) // NT + RAWB)
-            if n == -3 or n == -2:
+            if n == -4 or n == -3:
                 for c in range(4):
-                    dist_tile(0, 1, (n + 3) * 4 + c, ps_t, "t", False)
-            if -1 <= n <= 2:
-                for rep in range(2):
-                    i = (n + 1) * 2 + rep
-                    dist_tile(1, i // 4, i % 4, ps_t, "t", False)
-            if 3 <= n <= 6:
-                for rep in range(2):
-                    i = (n - 3) * 2 + rep
-                    dist_tile_sp(i // 4, 4 + i % 4)
+                    dist_tile(0, 1, (n + 4) * 4 + c, ps_t, "t", False)
+            if 1 <= n <= 16:
+                kind, half, c = d1_todo[n - 1]
+                if kind == 0:
+                    dist_tile(1, half, c, ps_o, "o", False)
+                else:
+                    dist_tile_sp(half, c)
             if n == 4:
                 for t in range(4, 8):
                     u_tile(t)

@@ -26,7 +26,7 @@ NHEAD = B * H
 NTILES = NHEAD * NT
 RAWB = 4
 PIN = True
-ACT_C_EVERY = 3
+ACT_C1_INDEX = 2
 
 
 def tile_rbfbias_kernel(tc, q, k, v, qs_s, ks_s, alpha, beta, out):
@@ -185,8 +185,8 @@ def tile_rbfbias_kernel(tc, q, k, v, qs_s, ks_s, alpha, beta, out):
                     op1=ALU.add,
                 )
 
-        def dist_tile_sp(half, c):
-            dps = ps_o.tile([P, 512], F32, name="dps", tag="o")
+        def dist_tile_sp(half, c, pool, tag):
+            dps = pool.tile([P, 512], F32, name="dps", tag=tag)
             for tq in range(4):
                 for f in range(3):
                     nc.tensor.matmul(
@@ -227,22 +227,28 @@ def tile_rbfbias_kernel(tc, q, k, v, qs_s, ks_s, alpha, beta, out):
         rinv = {}
         osb = {}
 
-        def trans_q(bh):
-            h = bh % H
-            tp = ps_q.tile([P, NT, P], BF16, name="tq", tag="tq")
+        tps = {}
+
+        def trans_q_pe(bh):
+            tps[bh] = ps_q.tile([P, NT, P], BF16, name="tq", tag="tq")
             for t in range(NT):
-                nc.tensor.transpose(out=tp[:, t, :], in_=qr[bh][:, t, :], identity=ident_bf[:])
+                nc.tensor.transpose(out=tps[bh][:, t, :], in_=qr[bh][:, t, :], identity=ident_bf[:])
+
+        def trans_q_cp(bh):
+            h = bh % H
             qT[bh] = work2.tile([P, NT * P], BF16, name="qT", tag="qT")
             nc.scalar.activation(
-                out=qT[bh][:], in_=tp[:].rearrange("p t c -> p (t c)"), func=ACTF.Copy, scale=sgn[:, h : h + 1]
+                out=qT[bh][:], in_=tps[bh][:].rearrange("p t c -> p (t c)"), func=ACTF.Copy, scale=sgn[:, h : h + 1]
             )
 
-        def trans_k(bh):
-            tp = ps_q.tile([P, NT, P], BF16, name="tq", tag="tq")
+        def trans_k_pe(bh):
+            tps[bh] = ps_q.tile([P, NT, P], BF16, name="tq", tag="tq")
             for c in range(NT):
-                nc.tensor.transpose(out=tp[:, c, :], in_=kr[bh][:, c // 4, c % 4, :], identity=ident_bf[:])
+                nc.tensor.transpose(out=tps[bh][:, c, :], in_=kr[bh][:, c // 4, c % 4, :], identity=ident_bf[:])
+
+        def trans_k_cp(bh):
             kT[bh] = work2.tile([P, NT * P], BF16, name="kT", tag="kT")
-            nc.vector.tensor_copy(out=kT[bh][:], in_=tp[:].rearrange("p t c -> p (t c)"))
+            nc.vector.tensor_copy(out=kT[bh][:], in_=tps[bh][:].rearrange("p t c -> p (t c)"))
 
         def v_group(bh):
             vg[bh] = work2.tile([P, 2, D, 4], BF16, name="vg", tag="vg", align_bytes=64)
@@ -342,23 +348,37 @@ def tile_rbfbias_kernel(tc, q, k, v, qs_s, ks_s, alpha, beta, out):
             for c in range(NT):
                 nc.tensor.transpose(out=eT[tau][:, c, :], in_=ee[tau][:, c * P : (c + 1) * P], identity=ident_bf[:])
 
-        def regroup(tau):
-            gr[tau] = work3.tile([P, 2, P, 4], BF16, name="gr", tag="gr", align_bytes=64)
-            src = eT[tau][:].rearrange("p (g j) c -> p g c j", j=4)
-            if tau % ACT_C_EVERY == 1:
-                nc.scalar.copy(out=gr[tau][:], in_=src)
-            else:
-                nc.vector.tensor_copy(out=gr[tau][:], in_=src)
+        es1 = {}
+        g4 = {}
 
-        def quant(tau):
+        def c1(tau):
+            es1[tau] = work3.tile([P, NT * P], BF16, name="es1", tag="es1")
+            src = eT[tau][:].rearrange("p c q -> p (c q)")
+            if tau % 4 == ACT_C1_INDEX:
+                nc.scalar.copy(out=es1[tau][:], in_=src)
+            else:
+                nc.vector.tensor_copy(out=es1[tau][:], in_=src)
+
+        def c2(tau):
             u, i = tau // 4, tau % 4
             if i == 0:
-                ec[u] = work3.tile([P, 4, 2 * P], U32, name="ec", tag="ec", align_bytes=64)
-                es[u] = work3.tile([P, 4, 2 * P], U8, name="es", tag="es", align_bytes=64)
+                g4[u] = work2.tile([P, 4, 2, P, 4], BF16, name="g4", tag="g4", align_bytes=64)
+            nc.gpsimd.tensor_scalar(
+                out=g4[u][:, i],
+                in0=es1[tau][:].rearrange("p (g j c) -> p g c j", g=2, j=4),
+                scalar1=1.0,
+                scalar2=0.0,
+                op0=ALU.mult,
+                op1=ALU.add,
+            )
+
+        def q4(u):
+            ec[u] = work2.tile([P, 4, 2 * P], U32, name="ec", tag="ec", align_bytes=64)
+            es[u] = work2.tile([P, 4, 2 * P], U8, name="es", tag="es", align_bytes=64)
             nc.vector.quantize_mx(
-                out=ec[u][:, i, :].bitcast(FP8X4),
-                scales=es[u][:, i, :],
-                in_=gr[tau][:].rearrange("p g c j -> p (g c j)"),
+                out=ec[u][:].rearrange("p i w -> p (i w)").bitcast(FP8X4),
+                scales=es[u][:].rearrange("p i w -> p (i w)"),
+                in_=g4[u][:].rearrange("p i g c j -> p (i g c j)"),
             )
 
         def r_inv(u):
@@ -383,21 +403,28 @@ def tile_rbfbias_kernel(tc, q, k, v, qs_s, ks_s, alpha, beta, out):
                         stop=(g == 1),
                     )
 
-        def norm(u):
+        def norm_half(u, hh):
             bh, uu = u // 2, u % 2
             b, h = bh // H, bh % H
-            if uu == 0:
+            if uu == 0 and hh == 0:
                 osb[bh] = work2.tile([P, NT, D], F32, name="osb", tag="osb")
-            dst = osb[bh][:, uu * 4 : uu * 4 + 4, :]
+            t0 = uu * 4 + hh * 2
             nc.vector.tensor_tensor(
-                out=dst, in0=ob[u][:], in1=rinv[u][:].unsqueeze(2).to_broadcast([P, 4, D]), op=ALU.mult
+                out=osb[bh][:, t0 : t0 + 2, :],
+                in0=ob[u][:, hh * 2 : hh * 2 + 2, :],
+                in1=rinv[u][:, hh * 2 : hh * 2 + 2].unsqueeze(2).to_broadcast([P, 2, D]),
+                op=ALU.mult,
             )
-            nc.sync.dma_start(
-                out=out[b, h].rearrange("(p t) d -> p t d", t=NT)[:, uu * 4 : uu * 4 + 4, :], in_=dst
-            )
+            if hh == 1:
+                nc.sync.dma_start(
+                    out=out[b, h].rearrange("(p t) d -> p t d", t=NT)[:, uu * 4 : uu * 4 + 4, :],
+                    in_=osb[bh][:, uu * 4 : uu * 4 + 4, :],
+                )
 
-        trans_q(0)
-        trans_k(0)
+        trans_q_pe(0)
+        trans_q_cp(0)
+        trans_k_pe(0)
+        trans_k_cp(0)
         v_group(0)
 
         def ok(tau):
@@ -409,54 +436,69 @@ def tile_rbfbias_kernel(tc, q, k, v, qs_s, ks_s, alpha, beta, out):
         def head(x):
             return x // NT if (x % NT == 0 and NT <= x < NTILES) else -1
 
-        d1_todo = (
-            [(1, 0, c) for c in range(4, 8)]
-            + [(0, half, c) for half in range(2) for c in range(4)]
-            + [(1, 1, c) for c in range(4, 8)]
-        )
+        d1_todo = [(0, half, c) for half in range(2) for c in range(4)] + [(1, 1, c) for c in range(4, 8)]
+        d1_done = 0
 
-        for n in range(-4, NTILES + 8):
+        for n in range(-4, NTILES + 10):
+            i = (n - 2) % 4
             if ok(n):
                 x2(n)
             if ok(n - 1):
                 te(n - 1)
-            if grp(n - 4) >= 0:
-                mxg(grp(n - 4))
+            if grp(n - 6) >= 0:
+                mxg(grp(n - 6))
+            if head(n + 7) >= 0:
+                trans_q_pe(head(n + 7))
+            if head(n + 5) >= 0:
+                trans_k_pe(head(n + 5))
             if ok(n + 2):
                 m_half(n + 2, 0)
-            if ok(n - 3):
-                quant(n - 3)
+            if grp(n - 7) >= 0:
+                norm_half(grp(n - 7), 0)
+            if grp(n - 9) >= 0:
+                norm_half(grp(n - 9), 1)
+            if (i == 1 or i == 3) and ok(n - 2):
+                c1(n - 2)
+                c2(n - 2)
             if ok(n + 4):
                 x1(n + 4)
-            if head(n + 5) >= 0:
-                trans_q(head(n + 5))
-            if head(n + 4) >= 0:
-                trans_k(head(n + 4))
+            if i == 2 and ok(n - 2):
+                c1(n - 2)
+                c2(n - 2)
+            if head(n + 6) >= 0:
+                trans_q_cp(head(n + 6))
             if ok(n + 3):
                 wmm(n + 3)
-            if head(n + 2) >= 0:
-                v_group(head(n + 2))
             if ok(n + 2):
                 m_half(n + 2, 1)
             if grp(n - 2) >= 0:
                 r_inv(grp(n - 2))
-            if ok(n - 2):
-                regroup(n - 2)
             if n == 2 or head(n - 2) >= 0:
                 v_quant((n - 2) // NT)
-            if grp(n - 4) >= 0:
-                norm(grp(n - 4))
-            if (n + 1) % NT == 0 and 0 <= (n + 1) // NT and (n + 1) // NT + RAWB < NHEAD:
-                load((n + 1) // NT + RAWB)
+            if grp(n - 3) >= 0:
+                q4(grp(n - 3))
+            if i == 0 and ok(n - 2):
+                c1(n - 2)
+                c2(n - 2)
+            if head(n + 1) >= 0:
+                v_group(head(n + 1))
+            if head(n + 4) >= 0:
+                trans_k_cp(head(n + 4))
+            if n % NT == 0 and 0 <= n // NT and n // NT + RAWB < NHEAD:
+                load(n // NT + RAWB)
             if n == -4 or n == -3:
                 for c in range(4):
                     dist_tile(0, 1, (n + 4) * 4 + c, ps_t, "t", False)
-            if 1 <= n <= 16:
-                kind, half, c = d1_todo[n - 1]
-                if kind == 0:
-                    dist_tile(1, half, c, ps_o, "o", False)
-                else:
-                    dist_tile_sp(half, c)
-            if n == 4:
+            if n == -1 or n == 0:
+                for rep in range(2):
+                    dist_tile_sp(0, 4 + (n + 1) * 2 + rep, ps_t, "t")
+            if n == 0:
                 for t in range(4, 8):
                     u_tile(t)
+            if n >= 5 and n % NT in (5, 6, 7, 0) and d1_done < 12:
+                kind, half, c = d1_todo[d1_done]
+                d1_done += 1
+                if kind == 0:
+                    dist_tile(1, half, c, ps_q, "tq", False)
+                else:
+                    dist_tile_sp(half, c, ps_q, "tq")

@@ -237,8 +237,12 @@ def tile_rbfbias_kernel(tc, q, k, v, qs_s, ks_s, alpha, beta, out):
         def trans_q_cp(bh):
             h = bh % H
             qT[bh] = work2.tile([P, NT * P], BF16, name="qT", tag="qT")
-            nc.scalar.activation(
-                out=qT[bh][:], in_=tps[bh][:].rearrange("p t c -> p (t c)"), func=ACTF.Copy, scale=sgn[:, h : h + 1]
+            nc.vector.tensor_scalar(
+                out=qT[bh][:],
+                in0=tps[bh][:].rearrange("p t c -> p (t c)"),
+                scalar1=sgn[:, h : h + 1],
+                scalar2=None,
+                op0=ALU.mult,
             )
 
         def trans_k_pe(bh):
@@ -268,13 +272,14 @@ def tile_rbfbias_kernel(tc, q, k, v, qs_s, ks_s, alpha, beta, out):
                 out=vc[bh][:].bitcast(FP8X4), scales=vs[bh][:], in_=vg[bh][:].rearrange("p g d j -> p (g d j)")
             )
 
-        def x1(tau):
+        def x1(pair):
+            tau = pair * 2
             bh, t = tau // NT, tau % NT
             b, h = bh // H, bh % H
-            et[tau] = work3.tile([P, NT, P], F32, name="et", tag="et")
+            et[pair] = work2.tile([P, NT, 2 * P], F32, name="et", tag="et")
             nc.scalar.activation(
-                out=et[tau][:],
-                in_=dT[b][:, :, t * P : (t + 1) * P],
+                out=et[pair][:],
+                in_=dT[b][:, :, t * P : (t + 2) * P],
                 func=ACTF.Exp,
                 scale=nbeta[:, h : h + 1],
                 bias=lna[:, h : h + 1],
@@ -295,7 +300,7 @@ def tile_rbfbias_kernel(tc, q, k, v, qs_s, ks_s, alpha, beta, out):
                 for j in range(4):
                     nc.tensor.matmul(
                         out=wg[:, j * P : (j + 1) * P],
-                        lhsT=et[tau][:, g * 4 + j, :],
+                        lhsT=et[tau // 2][:, g * 4 + j, (tau % 2) * P : (tau % 2 + 1) * P],
                         rhs=ident_f[:],
                         is_transpose=True,
                         start=False,
@@ -460,8 +465,8 @@ def tile_rbfbias_kernel(tc, q, k, v, qs_s, ks_s, alpha, beta, out):
             if (i == 1 or i == 3) and ok(n - 2):
                 c1(n - 2)
                 c2(n - 2)
-            if ok(n + 4):
-                x1(n + 4)
+            if ok(n + 4) and n % 2 == 0:
+                x1((n + 4) // 2)
             if i == 2 and ok(n - 2):
                 c1(n - 2)
                 c2(n - 2)

@@ -40,10 +40,8 @@ def tile_rbfbias_kernel(tc, q, k, v, qs_s, ks_s, alpha, beta, out):
         work3 = ctx.enter_context(tc.tile_pool(name="work3", bufs=3))
         upool = ctx.enter_context(tc.tile_pool(name="upool", bufs=4))
         work4 = ctx.enter_context(tc.tile_pool(name="work4", bufs=4))
-        ps_w = ctx.enter_context(tc.psum_pool(name="ps_w", bufs=3))
-        ps_t = ctx.enter_context(tc.psum_pool(name="ps_t", bufs=3))
-        ps_q = ctx.enter_context(tc.psum_pool(name="ps_q", bufs=1))
-        ps_o = ctx.enter_context(tc.psum_pool(name="ps_o", bufs=1))
+        ps_w = ctx.enter_context(tc.psum_pool(name="ps_w", bufs=4))
+        ps_t = ctx.enter_context(tc.psum_pool(name="ps_t", bufs=4))
         if PIN:
             ctx.enter_context(tc.manual_schedule())
 
@@ -230,7 +228,7 @@ def tile_rbfbias_kernel(tc, q, k, v, qs_s, ks_s, alpha, beta, out):
         tps = {}
 
         def trans_q_pe(bh):
-            tps[bh] = ps_q.tile([P, NT, P], BF16, name="tq", tag="tq")
+            tps[bh] = ps_t.tile([P, NT, P], BF16, name="tq", tag="t")
             for t in range(NT):
                 nc.tensor.transpose(out=tps[bh][:, t, :], in_=qr[bh][:, t, :], identity=ident_bf[:])
 
@@ -246,7 +244,7 @@ def tile_rbfbias_kernel(tc, q, k, v, qs_s, ks_s, alpha, beta, out):
             )
 
         def trans_k_pe(bh):
-            tps[bh] = ps_q.tile([P, NT, P], BF16, name="tq", tag="tq")
+            tps[bh] = ps_t.tile([P, NT, P], BF16, name="tq", tag="t")
             for c in range(NT):
                 nc.tensor.transpose(out=tps[bh][:, c, :], in_=kr[bh][:, c // 4, c % 4, :], identity=ident_bf[:])
 
@@ -395,7 +393,7 @@ def tile_rbfbias_kernel(tc, q, k, v, qs_s, ks_s, alpha, beta, out):
 
         def mxg(u):
             bh = u // 2
-            ob[u] = ps_o.tile([P, 4, D], F32, name="ob", tag="o")
+            ob[u] = ps_t.tile([P, 4, D], F32, name="ob", tag="t")
             for i in range(4):
                 for g in range(2):
                     nc.tensor.matmul_mx(
@@ -450,18 +448,18 @@ def tile_rbfbias_kernel(tc, q, k, v, qs_s, ks_s, alpha, beta, out):
                 x2(n)
             if ok(n - 1):
                 te(n - 1)
-            if grp(n - 6) >= 0:
-                mxg(grp(n - 6))
-            if head(n + 7) >= 0:
-                trans_q_pe(head(n + 7))
-            if head(n + 5) >= 0:
-                trans_k_pe(head(n + 5))
+            if grp(n - 5) >= 0:
+                mxg(grp(n - 5))
             if ok(n + 2):
                 m_half(n + 2, 0)
+            if grp(n - 6) >= 0:
+                norm_half(grp(n - 6), 0)
             if grp(n - 7) >= 0:
-                norm_half(grp(n - 7), 0)
-            if grp(n - 9) >= 0:
-                norm_half(grp(n - 9), 1)
+                norm_half(grp(n - 7), 1)
+            if grp(n - 5) >= 0:
+                r_inv(grp(n - 5))
+            if head(n + 4) >= 0:
+                trans_k_cp(head(n + 4))
             if (i == 1 or i == 3) and ok(n - 2):
                 c1(n - 2)
                 c2(n - 2)
@@ -476,8 +474,6 @@ def tile_rbfbias_kernel(tc, q, k, v, qs_s, ks_s, alpha, beta, out):
                 wmm(n + 3)
             if ok(n + 2):
                 m_half(n + 2, 1)
-            if grp(n - 2) >= 0:
-                r_inv(grp(n - 2))
             if n == 2 or head(n - 2) >= 0:
                 v_quant((n - 2) // NT)
             if grp(n - 3) >= 0:
@@ -487,8 +483,10 @@ def tile_rbfbias_kernel(tc, q, k, v, qs_s, ks_s, alpha, beta, out):
                 c2(n - 2)
             if head(n + 1) >= 0:
                 v_group(head(n + 1))
-            if head(n + 4) >= 0:
-                trans_k_cp(head(n + 4))
+            if head(n + 7) >= 0:
+                trans_q_pe(head(n + 7))
+            if head(n + 5) >= 0:
+                trans_k_pe(head(n + 5))
             if n % NT == 0 and 0 <= n // NT and n // NT + RAWB < NHEAD:
                 load(n // NT + RAWB)
             if n == -4 or n == -3:
@@ -500,10 +498,10 @@ def tile_rbfbias_kernel(tc, q, k, v, qs_s, ks_s, alpha, beta, out):
             if n == 0:
                 for t in range(4, 8):
                     u_tile(t)
-            if n >= 5 and n % NT in (5, 6, 7, 0) and d1_done < 12:
+            if n >= 5 and n % NT in (2, 5, 6, 7) and d1_done < 12:
                 kind, half, c = d1_todo[d1_done]
                 d1_done += 1
                 if kind == 0:
-                    dist_tile(1, half, c, ps_q, "tq", False)
+                    dist_tile(1, half, c, ps_t, "t", False)
                 else:
-                    dist_tile_sp(half, c, ps_q, "tq")
+                    dist_tile_sp(half, c, ps_t, "t")

@@ -87,23 +87,6 @@ def tile_rbfbias_kernel(tc, q, k, v, qs_s, ks_s, alpha, beta, out):
         feat = const.tile([P, 4, NT, P], BF16, name="feat")
         nc.vector.memset(feat[:], 0.0)
 
-        al = const.tile([P, H], F32, name="al")
-        nc.vector.tensor_copy(out=al[:], in_=al_bf[:])
-        sgn = const.tile([P, H], F32, name="sgn")
-        nc.vector.tensor_scalar(out=sgn[:], in0=al[:], scalar1=0.0, scalar2=2.0, op0=ALU.is_ge, op1=ALU.mult)
-        nc.vector.tensor_scalar(out=sgn[:], in0=sgn[:], scalar1=-1.0, scalar2=None, op0=ALU.add)
-        absa = const.tile([P, H], F32, name="absa")
-        nc.vector.tensor_tensor(out=absa[:], in0=al[:], in1=sgn[:], op=ALU.mult)
-        nc.vector.tensor_scalar(
-            out=absa[:], in0=absa[:], scalar1=math.sqrt(D), scalar2=2.0 ** -60, op0=ALU.mult, op1=ALU.max
-        )
-        lna = const.tile([P, H], F32, name="lna")
-        nc.scalar.activation(out=lna[:], in_=absa[:], func=ACTF.Ln)
-        nbeta = const.tile([P, H], F32, name="nbeta")
-        nc.vector.tensor_scalar(out=nbeta[:], in0=be_bf[:], scalar1=-1.0, scalar2=None, op0=ALU.mult)
-        scneg = const.tile([P, H], F32, name="scneg")
-        nc.vector.tensor_scalar(out=scneg[:], in0=sgn[:], scalar1=-scale, scalar2=None, op0=ALU.mult)
-
         xf = const.tile([P, 4, 24], F32, name="xf")
         nc.vector.tensor_copy(out=xf[:], in_=pos[:, :, 0:24])
         sq = const.tile([P, 4, 24], F32, name="sq")
@@ -134,6 +117,23 @@ def tile_rbfbias_kernel(tc, q, k, v, qs_s, ks_s, alpha, beta, out):
                 nxt = const.tile([P, 4, NT], F32, name="rem%d" % (i + 1))
                 nc.vector.tensor_tensor(out=nxt[:], in0=rem[:], in1=part[:], op=ALU.subtract)
                 rem = nxt
+
+        al = const.tile([P, H], F32, name="al")
+        nc.vector.tensor_copy(out=al[:], in_=al_bf[:])
+        sgn = const.tile([P, H], F32, name="sgn")
+        nc.vector.tensor_scalar(out=sgn[:], in0=al[:], scalar1=0.0, scalar2=2.0, op0=ALU.is_ge, op1=ALU.mult)
+        nc.vector.tensor_scalar(out=sgn[:], in0=sgn[:], scalar1=-1.0, scalar2=None, op0=ALU.add)
+        absa = const.tile([P, H], F32, name="absa")
+        nc.vector.tensor_tensor(out=absa[:], in0=al[:], in1=sgn[:], op=ALU.mult)
+        nc.vector.tensor_scalar(
+            out=absa[:], in0=absa[:], scalar1=math.sqrt(D), scalar2=2.0 ** -60, op0=ALU.mult, op1=ALU.max
+        )
+        lna = const.tile([P, H], F32, name="lna")
+        nc.scalar.activation(out=lna[:], in_=absa[:], func=ACTF.Ln)
+        nbeta = const.tile([P, H], F32, name="nbeta")
+        nc.vector.tensor_scalar(out=nbeta[:], in0=be_bf[:], scalar1=-1.0, scalar2=None, op0=ALU.mult)
+        scneg = const.tile([P, H], F32, name="scneg")
+        nc.vector.tensor_scalar(out=scneg[:], in0=sgn[:], scalar1=-scale, scalar2=None, op0=ALU.mult)
 
         featT = []
         for w in (0, 2, 1, 3):
@@ -275,13 +275,16 @@ def tile_rbfbias_kernel(tc, q, k, v, qs_s, ks_s, alpha, beta, out):
             bh, t = tau // NT, tau % NT
             b, h = bh // H, bh % H
             et[pair] = work2.tile([P, NT, 2 * P], F32, name="et", tag="et")
-            nc.scalar.activation(
-                out=et[pair][:],
-                in_=dT[b][:, :, t * P : (t + 2) * P],
-                func=ACTF.Exp,
-                scale=nbeta[:, h : h + 1],
-                bias=lna[:, h : h + 1],
-            )
+            pieces = 2 if pair == 0 else 1
+            wid = 2 * P // pieces
+            for k2 in range(pieces):
+                nc.scalar.activation(
+                    out=et[pair][:, :, k2 * wid : (k2 + 1) * wid],
+                    in_=dT[b][:, :, t * P + k2 * wid : t * P + (k2 + 1) * wid],
+                    func=ACTF.Exp,
+                    scale=nbeta[:, h : h + 1],
+                    bias=lna[:, h : h + 1],
+                )
 
         def wmm(tau):
             bh, t = tau // NT, tau % NT
@@ -295,16 +298,17 @@ def tile_rbfbias_kernel(tc, q, k, v, qs_s, ks_s, alpha, beta, out):
                     start=True,
                     stop=False,
                 )
+                wt[tau].append(wg)
+            for g in range(2):
                 for j in range(4):
                     nc.tensor.matmul(
-                        out=wg[:, j * P : (j + 1) * P],
+                        out=wt[tau][g][:, j * P : (j + 1) * P],
                         lhsT=et[tau // 2][:, g * 4 + j, (tau % 2) * P : (tau % 2 + 1) * P],
                         rhs=ident_f[:],
                         is_transpose=True,
                         start=False,
                         stop=(j == 3),
                     )
-                wt[tau].append(wg)
 
         def m_half(tau, g):
             h = (tau // NT) % H
@@ -384,6 +388,25 @@ def tile_rbfbias_kernel(tc, q, k, v, qs_s, ks_s, alpha, beta, out):
                 in_=g4[u][:].rearrange("p i g c j -> p (i g c j)"),
             )
 
+        def c_direct(tau, on_act):
+            u, i = tau // 4, tau % 4
+            src = eT[tau][:].rearrange("p (g j) c -> p g c j", j=4)
+            if on_act:
+                nc.scalar.copy(out=g4[u][:, i], in_=src)
+            else:
+                nc.vector.tensor_copy(out=g4[u][:, i], in_=src)
+
+        def q1(tau):
+            u, i = tau // 4, tau % 4
+            if i == 0:
+                ec[u] = work2.tile([P, 4, 2 * P], U32, name="ec", tag="ec", align_bytes=64)
+                es[u] = work2.tile([P, 4, 2 * P], U8, name="es", tag="es", align_bytes=64)
+            nc.vector.quantize_mx(
+                out=ec[u][:, i, :].bitcast(FP8X4),
+                scales=es[u][:, i, :],
+                in_=g4[u][:, i].rearrange("p g c j -> p (g c j)"),
+            )
+
         def r_inv(u):
             bh, uu = u // 2, u % 2
             rinv[u] = small.tile([P, 4], F32, name="rinv", tag="rinv")
@@ -391,20 +414,25 @@ def tile_rbfbias_kernel(tc, q, k, v, qs_s, ks_s, alpha, beta, out):
 
         ob = {}
 
-        def mxg(u):
+        def mx1(tau):
+            u, i = tau // 4, tau % 4
             bh = u // 2
-            ob[u] = ps_t.tile([P, 4, D], F32, name="ob", tag="t")
+            if i == 0:
+                ob[u] = ps_t.tile([P, 4, D], F32, name="ob", tag="t")
+            for g in range(2):
+                nc.tensor.matmul_mx(
+                    out=ob[u][:, i, :],
+                    lhsT=ec[u][:, i, g * P : (g + 1) * P].bitcast(FP8X4),
+                    lhsT_scale=es[u][:, i, g * P : (g + 1) * P],
+                    rhs=vc[bh][:, g * D : (g + 1) * D].bitcast(FP8X4),
+                    rhs_scale=vs[bh][:, g * D : (g + 1) * D],
+                    start=(g == 0),
+                    stop=(g == 1),
+                )
+
+        def mxg(u):
             for i in range(4):
-                for g in range(2):
-                    nc.tensor.matmul_mx(
-                        out=ob[u][:, i, :],
-                        lhsT=ec[u][:, i, g * P : (g + 1) * P].bitcast(FP8X4),
-                        lhsT_scale=es[u][:, i, g * P : (g + 1) * P],
-                        rhs=vc[bh][:, g * D : (g + 1) * D].bitcast(FP8X4),
-                        rhs_scale=vs[bh][:, g * D : (g + 1) * D],
-                        start=(g == 0),
-                        stop=(g == 1),
-                    )
+                mx1(u * 4 + i)
 
         def norm_half(u, hh):
             bh, uu = u // 2, u % 2
@@ -418,11 +446,11 @@ def tile_rbfbias_kernel(tc, q, k, v, qs_s, ks_s, alpha, beta, out):
                 in1=rinv[u][:, hh * 2 : hh * 2 + 2].unsqueeze(2).to_broadcast([P, 2, D]),
                 op=ALU.mult,
             )
-            if hh == 1:
-                nc.sync.dma_start(
-                    out=out[b, h].rearrange("(p t) d -> p t d", t=NT)[:, uu * 4 : uu * 4 + 4, :],
-                    in_=osb[bh][:, uu * 4 : uu * 4 + 4, :],
-                )
+            dram = out[b, h].rearrange("(p t) d -> p t d", t=NT)
+            if u == NTILES // 4 - 1:
+                nc.sync.dma_start(out=dram[:, t0 : t0 + 2, :], in_=osb[bh][:, t0 : t0 + 2, :])
+            elif hh == 1:
+                nc.sync.dma_start(out=dram[:, uu * 4 : uu * 4 + 4, :], in_=osb[bh][:, uu * 4 : uu * 4 + 4, :])
 
         trans_q_pe(0)
         trans_q_cp(0)
@@ -442,7 +470,7 @@ def tile_rbfbias_kernel(tc, q, k, v, qs_s, ks_s, alpha, beta, out):
         d1_todo = [(0, half, c) for half in range(2) for c in range(4)] + [(1, 1, c) for c in range(4, 8)]
         d1_done = 0
 
-        for n in range(-4, NTILES + 10):
+        for n in range(-4, NTILES + 1):
             i = (n - 2) % 4
             if ok(n):
                 x2(n)
@@ -465,7 +493,7 @@ def tile_rbfbias_kernel(tc, q, k, v, qs_s, ks_s, alpha, beta, out):
                 c2(n - 2)
             if ok(n + 4) and n % 2 == 0:
                 x1((n + 4) // 2)
-            if i == 2 and ok(n - 2):
+            if i == 2 and ok(n - 2) and n - 2 < NTILES - 2:
                 c1(n - 2)
                 c2(n - 2)
             if head(n + 6) >= 0:
@@ -505,3 +533,21 @@ def tile_rbfbias_kernel(tc, q, k, v, qs_s, ks_s, alpha, beta, out):
                     dist_tile(1, half, c, ps_t, "t", False)
                 else:
                     dist_tile_sp(half, c, ps_t, "t")
+            if n == NTILES - 1:
+                q1(NTILES - 4)
+                mx1(NTILES - 4)
+            if n == NTILES:
+                c_direct(NTILES - 2, True)
+                q1(NTILES - 3)
+                mx1(NTILES - 3)
+                r_inv(NTILES // 4 - 1)
+
+        c_direct(NTILES - 1, False)
+        q1(NTILES - 2)
+        q1(NTILES - 1)
+        mx1(NTILES - 2)
+        mx1(NTILES - 1)
+        norm_half(NTILES // 4 - 2, 0)
+        norm_half(NTILES // 4 - 2, 1)
+        norm_half(NTILES // 4 - 1, 0)
+        norm_half(NTILES // 4 - 1, 1)

@@ -10,7 +10,6 @@ F32 = mybir.dt.float32
 BF16 = mybir.dt.bfloat16
 U32 = mybir.dt.uint32
 U8 = mybir.dt.uint8
-I32 = mybir.dt.int32
 FP8X4 = mybir.dt.float8_e4m3fn_x4
 ALU = mybir.AluOpType
 ACTF = mybir.ActivationFunctionType
@@ -21,12 +20,20 @@ B = 2
 H = 8
 S = 1024
 D = 128
+NF = 3
 NT = 8
+BANK = 512
+PACK = 4
+PASSES = 2
+GROUP = 4
+GROUPS_PER_HEAD = NT // GROUP
+TILES_PER_BANK = BANK // P
 NHEAD = B * H
 NTILES = NHEAD * NT
+NGROUPS = NTILES // GROUP
+FIRST_SUMMED_CHUNK = 4
 RAWB = 4
-PIN = True
-ACT_C1_INDEX = 2
+SCALAR_RANK = 2
 
 
 def tile_rbfbias_kernel(tc, q, k, v, qs_s, ks_s, alpha, beta, out):
@@ -42,39 +49,43 @@ def tile_rbfbias_kernel(tc, q, k, v, qs_s, ks_s, alpha, beta, out):
         work4 = ctx.enter_context(tc.tile_pool(name="work4", bufs=4))
         ps_w = ctx.enter_context(tc.psum_pool(name="ps_w", bufs=4))
         ps_t = ctx.enter_context(tc.psum_pool(name="ps_t", bufs=4))
-        if PIN:
-            ctx.enter_context(tc.manual_schedule())
+        ctx.enter_context(tc.manual_schedule())
 
         pos = const.tile([P, 4, 32], BF16, name="pos")
         for b in range(B):
             nc.sync.dma_start(
-                out=pos[:, b, 0:24].rearrange("p (t f) -> p t f", f=3),
+                out=pos[:, b, 0 : NT * NF].rearrange("p (t f) -> p t f", f=NF),
                 in_=qs_s[b].rearrange("(p t) f -> p t f", t=NT),
             )
             nc.sync.dma_start(
-                out=pos[:, 2 + b, 0:24].rearrange("p (g j f) -> p g j f", g=2, f=3),
-                in_=ks_s[b].rearrange("(g p j) f -> p g j f", g=2, j=4),
+                out=pos[:, 2 + b, 0 : NT * NF].rearrange("p (g j f) -> p g j f", g=PASSES, f=NF),
+                in_=ks_s[b].rearrange("(g p j) f -> p g j f", g=PASSES, j=PACK),
             )
-        yraw = const.tile([P, 1536], BF16, name="yraw")
-        al_bf = const.tile([P, H], BF16, name="al_bf")
-        be_bf = const.tile([P, H], BF16, name="be_bf")
-        nc.sync.dma_start(out=al_bf[:], in_=alpha.rearrange("h o -> (h o)").partition_broadcast(P))
-        nc.sync.dma_start(out=be_bf[:], in_=beta.rearrange("h o -> (h o)").partition_broadcast(P))
+        key_row = const.tile([P, BANK * NF], BF16, name="yraw")
+        alpha_bf = const.tile([P, H], BF16, name="al_bf")
+        beta_bf = const.tile([P, H], BF16, name="be_bf")
+        nc.sync.dma_start(out=alpha_bf[:], in_=alpha.rearrange("h o -> (h o)").partition_broadcast(P))
+        nc.sync.dma_start(out=beta_bf[:], in_=beta.rearrange("h o -> (h o)").partition_broadcast(P))
+        nc.sync.dma_start(
+            out=key_row[:], in_=ks_s[1, BANK:S, :].rearrange("k f -> (k f)").partition_broadcast(P)
+        )
 
-        nc.sync.dma_start(out=yraw[:], in_=ks_s[1, 512:1024, :].rearrange("k f -> (k f)").partition_broadcast(P))
-
-        qr = {}
-        kr = {}
-        vr = {}
+        q_raw = {}
+        k_raw = {}
+        v_raw = {}
 
         def load(bh):
             b, h = bh // H, bh % H
-            qr[bh] = raw.tile([P, NT, D], BF16, name="qr", tag="qr")
-            nc.sync.dma_start(out=qr[bh][:], in_=q[b, h].rearrange("(p t) d -> p t d", t=NT))
-            kr[bh] = raw.tile([P, 2, 4, D], BF16, name="kr", tag="kr")
-            nc.sync.dma_start(out=kr[bh][:], in_=k[b, h].rearrange("(g p j) d -> p g j d", g=2, j=4))
-            vr[bh] = raw.tile([P, 2, 4, D], BF16, name="vr", tag="vr")
-            nc.sync.dma_start(out=vr[bh][:], in_=v[b, h].rearrange("(g p j) d -> p g j d", g=2, j=4))
+            q_raw[bh] = raw.tile([P, NT, D], BF16, name="qr", tag="qr")
+            nc.sync.dma_start(out=q_raw[bh][:], in_=q[b, h].rearrange("(p t) d -> p t d", t=NT))
+            k_raw[bh] = raw.tile([P, PASSES, PACK, D], BF16, name="kr", tag="kr")
+            nc.sync.dma_start(
+                out=k_raw[bh][:], in_=k[b, h].rearrange("(g p j) d -> p g j d", g=PASSES, j=PACK)
+            )
+            v_raw[bh] = raw.tile([P, PASSES, PACK, D], BF16, name="vr", tag="vr")
+            nc.sync.dma_start(
+                out=v_raw[bh][:], in_=v[b, h].rearrange("(g p j) d -> p g j d", g=PASSES, j=PACK)
+            )
 
         for bh in range(RAWB):
             load(bh)
@@ -86,468 +97,468 @@ def tile_rbfbias_kernel(tc, q, k, v, qs_s, ks_s, alpha, beta, out):
 
         feat = const.tile([P, 4, NT, P], BF16, name="feat")
         nc.vector.memset(feat[:], 0.0)
-
-        xf = const.tile([P, 4, 24], F32, name="xf")
-        nc.vector.tensor_copy(out=xf[:], in_=pos[:, :, 0:24])
-        sq = const.tile([P, 4, 24], F32, name="sq")
-        nc.vector.tensor_tensor(out=sq[:], in0=xf[:], in1=xf[:], op=ALU.mult)
-        s2 = const.tile([P, 4, NT], F32, name="s2")
-        nc.vector.tensor_reduce(
-            out=s2[:], in_=sq[:].rearrange("p w (t f) -> p w t f", f=3), axis=AX.X, op=ALU.add
-        )
-        rem = s2
-        m2x = const.tile([P, 24], F32, name="m2x")
-        nc.vector.tensor_scalar(out=m2x[:], in0=xf[:, 1, :], scalar1=-2.0, scalar2=None, op0=ALU.mult)
+        nc.vector.memset(feat[:, 0:2, :, 9:15], 1.0)
+        nc.vector.memset(feat[:, 2:4, :, 3:9], 1.0)
+        pos_v = pos[:, :, 0 : NT * NF].rearrange("p w (t f) -> p w t f", f=NF)
+        squares = const.tile([P, 4, NT, NF], F32, name="sq")
+        nc.vector.tensor_tensor(out=squares[:], in0=pos_v, in1=pos_v, op=ALU.mult)
+        nc.vector.tensor_copy(out=feat[:, 0:2, :, 3:6], in_=squares[:, 0:2])
+        nc.vector.tensor_copy(out=feat[:, 2:4, :, 9:12], in_=squares[:, 2:4])
         nc.vector.tensor_scalar(
-            out=feat[:, 0:2, :, 0:3],
-            in0=xf[:, 0:2, :].rearrange("p w (t f) -> p w t f", f=3),
-            scalar1=-2.0,
-            scalar2=None,
-            op0=ALU.mult,
+            out=feat[:, 0:2, :, 0:3], in0=pos_v[:, 0:2], scalar1=-2.0, scalar2=None, op0=ALU.mult
         )
-        nc.vector.tensor_copy(out=feat[:, 2:4, :, 0:3], in_=xf[:, 2:4, :].rearrange("p w (t f) -> p w t f", f=3))
-        nc.vector.memset(feat[:, 0:2, :, 6:9], 1.0)
-        nc.vector.memset(feat[:, 2:4, :, 3:6], 1.0)
-        for i in range(3):
-            part = const.tile([P, 4, NT], BF16, name="part%d" % i)
-            nc.vector.tensor_copy(out=part[:], in_=rem[:])
-            nc.vector.tensor_copy(out=feat[:, 0:2, :, 3 + i], in_=part[:, 0:2, :])
-            nc.vector.tensor_copy(out=feat[:, 2:4, :, 6 + i], in_=part[:, 2:4, :])
-            if i < 2:
-                nxt = const.tile([P, 4, NT], F32, name="rem%d" % (i + 1))
-                nc.vector.tensor_tensor(out=nxt[:], in0=rem[:], in1=part[:], op=ALU.subtract)
-                rem = nxt
+        nc.vector.tensor_copy(out=feat[:, 2:4, :, 0:3], in_=pos_v[:, 2:4])
+        nc.vector.tensor_tensor(
+            out=feat[:, 0:2, :, 6:9], in0=squares[:, 0:2], in1=feat[:, 0:2, :, 3:6], op=ALU.subtract
+        )
+        nc.vector.tensor_tensor(
+            out=feat[:, 2:4, :, 12:15], in0=squares[:, 2:4], in1=feat[:, 2:4, :, 9:12], op=ALU.subtract
+        )
 
-        al = const.tile([P, H], F32, name="al")
-        nc.vector.tensor_copy(out=al[:], in_=al_bf[:])
-        sgn = const.tile([P, H], F32, name="sgn")
-        nc.vector.tensor_scalar(out=sgn[:], in0=al[:], scalar1=0.0, scalar2=2.0, op0=ALU.is_ge, op1=ALU.mult)
-        nc.vector.tensor_scalar(out=sgn[:], in0=sgn[:], scalar1=-1.0, scalar2=None, op0=ALU.add)
-        absa = const.tile([P, H], F32, name="absa")
-        nc.vector.tensor_tensor(out=absa[:], in0=al[:], in1=sgn[:], op=ALU.mult)
+        alpha_f = const.tile([P, H], F32, name="al")
+        nc.vector.tensor_copy(out=alpha_f[:], in_=alpha_bf[:])
+        sign = const.tile([P, H], F32, name="sgn")
         nc.vector.tensor_scalar(
-            out=absa[:], in0=absa[:], scalar1=math.sqrt(D), scalar2=2.0 ** -60, op0=ALU.mult, op1=ALU.max
+            out=sign[:], in0=alpha_f[:], scalar1=0.0, scalar2=2.0, op0=ALU.is_ge, op1=ALU.mult
         )
-        lna = const.tile([P, H], F32, name="lna")
-        nc.scalar.activation(out=lna[:], in_=absa[:], func=ACTF.Ln)
-        nbeta = const.tile([P, H], F32, name="nbeta")
-        nc.vector.tensor_scalar(out=nbeta[:], in0=be_bf[:], scalar1=-1.0, scalar2=None, op0=ALU.mult)
-        scneg = const.tile([P, H], F32, name="scneg")
-        nc.vector.tensor_scalar(out=scneg[:], in0=sgn[:], scalar1=-scale, scalar2=None, op0=ALU.mult)
+        nc.vector.tensor_scalar(out=sign[:], in0=sign[:], scalar1=-1.0, scalar2=None, op0=ALU.add)
+        height = const.tile([P, H], F32, name="absa")
+        nc.vector.tensor_tensor(out=height[:], in0=alpha_f[:], in1=sign[:], op=ALU.mult)
+        nc.vector.tensor_scalar(
+            out=height[:], in0=height[:], scalar1=math.sqrt(D), scalar2=2.0 ** -60, op0=ALU.mult, op1=ALU.max
+        )
+        ln_height = const.tile([P, H], F32, name="lna")
+        nc.scalar.activation(out=ln_height[:], in_=height[:], func=ACTF.Ln)
+        minus_beta = const.tile([P, H], F32, name="nbeta")
+        nc.vector.tensor_scalar(out=minus_beta[:], in0=beta_bf[:], scalar1=-1.0, scalar2=None, op0=ALU.mult)
+        to_minus_z = const.tile([P, H], F32, name="scneg")
+        nc.vector.tensor_scalar(out=to_minus_z[:], in0=sign[:], scalar1=-scale, scalar2=None, op0=ALU.mult)
 
-        featT = []
-        for w in (0, 2, 1, 3):
-            tp = ps_t.tile([P, NT, P], BF16, name="tp", tag="t")
+        norm2 = const.tile([P, 4, NT], F32, name="s2")
+        nc.vector.tensor_reduce(out=norm2[:], in_=squares[:], axis=AX.X, op=ALU.add)
+        minus_2x = const.tile([P, NT * NF], F32, name="m2x")
+        nc.vector.tensor_scalar(
+            out=minus_2x[:], in0=pos[:, 1, 0 : NT * NF], scalar1=-2.0, scalar2=None, op0=ALU.mult
+        )
+
+        featT = {}
+        for slot in (0, 2, 1, 3):
+            bank = ps_t.tile([P, NT, P], BF16, name="tp", tag="t")
             for t in range(NT):
-                nc.tensor.transpose(out=tp[:, t, :], in_=feat[:, w, t, :], identity=ident_bf[:])
-            ft = const.tile([P, NT * P], BF16, name="featT%d" % w)
-            if w < 2:
-                nc.vector.tensor_copy(out=ft[:], in_=tp[:].rearrange("p t c -> p (t c)"))
+                nc.tensor.transpose(out=bank[:, t, :], in_=feat[:, slot, t, :], identity=ident_bf[:])
+            featT[slot] = const.tile([P, NT * P], BF16, name="featT%d" % slot)
+            if slot < 2:
+                nc.vector.tensor_copy(out=featT[slot][:], in_=bank[:].rearrange("p t c -> p (t c)"))
             else:
-                nc.scalar.copy(out=ft[:], in_=tp[:].rearrange("p t c -> p (t c)"))
-            featT.append((w, ft))
-        featT = dict(featT)
+                nc.scalar.copy(out=featT[slot][:], in_=bank[:].rearrange("p t c -> p (t c)"))
 
-        dT = [const.tile([P, NT, S], F32, name="dT%d" % b) for b in range(B)]
+        dist = [const.tile([P, NT, S], F32, name="dT%d" % b) for b in range(B)]
 
-        def dist_tile(b, half, c, pool, tag, on_act):
-            dps = pool.tile([P, 512], F32, name="dps", tag=tag)
+        def dist_by_matmul(b, q_half, c, pool, tag, on_scalar):
+            bank = pool.tile([P, BANK], F32, name="dps", tag=tag)
             nc.tensor.matmul(
-                out=dps[:],
+                out=bank[:],
                 lhsT=featT[2 + b][:, c * P : (c + 1) * P],
-                rhs=featT[b][:, half * 512 : (half + 1) * 512],
+                rhs=featT[b][:, q_half * BANK : (q_half + 1) * BANK],
                 start=True,
                 stop=True,
             )
-            dst = dT[b][:, c, half * 512 : (half + 1) * 512]
-            if on_act:
-                nc.scalar.copy(out=dst, in_=dps[:])
+            dst = dist[b][:, c, q_half * BANK : (q_half + 1) * BANK]
+            if on_scalar:
+                nc.scalar.copy(out=dst, in_=bank[:])
             else:
-                nc.vector.tensor_copy(out=dst, in_=dps[:])
+                nc.vector.tensor_copy(out=dst, in_=bank[:])
 
         for c in range(NT):
-            dist_tile(0, 0, c, ps_w, "w", c % 2 == 1)
+            dist_by_matmul(0, 0, c, ps_w, "w", c % 2 == 1)
 
-        yv = yraw[:].rearrange("x (p j f) -> x f j p", j=4, f=3)
-        uu = {}
+        key_feature = key_row[:].rearrange("x (p j f) -> x f j p", j=PACK, f=NF)
+        products = {}
 
-        def u_tile(t):
-            uu[t] = upool.tile([P, 3, 512], F32, name="uu", tag="uu")
-            for f in range(3):
+        def product_tile(t):
+            products[t] = upool.tile([P, NF, BANK], F32, name="uu", tag="uu")
+            for f in range(NF):
                 nc.gpsimd.tensor_scalar(
-                    out=uu[t][:, f, :].rearrange("x (j p) -> x j p", j=4),
-                    in0=yv[:, f],
-                    scalar1=m2x[:, t * 3 + f : t * 3 + f + 1],
-                    scalar2=(s2[:, 1, t : t + 1] if f == 0 else 0.0),
+                    out=products[t][:, f, :].rearrange("x (j p) -> x j p", j=PACK),
+                    in0=key_feature[:, f],
+                    scalar1=minus_2x[:, t * NF + f : t * NF + f + 1],
+                    scalar2=(norm2[:, 1, t : t + 1] if f == 0 else 0.0),
                     op0=ALU.mult,
                     op1=ALU.add,
                 )
 
-        def dist_tile_sp(half, c, pool, tag):
-            dps = pool.tile([P, 512], F32, name="dps", tag=tag)
-            for tq in range(4):
-                for f in range(3):
+        def dist_by_transposes(q_half, c):
+            bank = ps_t.tile([P, BANK], F32, name="dps", tag="t")
+            col = c - FIRST_SUMMED_CHUNK
+            for tq in range(TILES_PER_BANK):
+                for f in range(NF):
                     nc.tensor.matmul(
-                        out=dps[:, tq * P : (tq + 1) * P],
-                        lhsT=uu[half * 4 + tq][:, f, (c - 4) * P : (c - 3) * P],
+                        out=bank[:, tq * P : (tq + 1) * P],
+                        lhsT=products[q_half * TILES_PER_BANK + tq][:, f, col * P : (col + 1) * P],
                         rhs=ident_f[:],
                         is_transpose=True,
                         start=(tq == 0 and f == 0),
-                        stop=(tq == 3 and f == 2),
+                        stop=(tq == TILES_PER_BANK - 1 and f == NF - 1),
                     )
             nc.vector.tensor_scalar(
-                out=dT[1][:, c, half * 512 : (half + 1) * 512],
-                in0=dps[:],
-                scalar1=s2[:, 3, c : c + 1],
+                out=dist[1][:, c, q_half * BANK : (q_half + 1) * BANK],
+                in0=bank[:],
+                scalar1=norm2[:, 3, c : c + 1],
                 scalar2=None,
                 op0=ALU.add,
             )
 
-        for t in range(4):
-            u_tile(t)
+        for t in range(TILES_PER_BANK):
+            product_tile(t)
 
+        t_bank = {}
         qT = {}
         kT = {}
-        vc = {}
-        vs = {}
-        vg = {}
-        et = {}
-        wt = {}
-        nb = {}
-        nb0 = {}
-        zt = {}
-        ee = {}
-        eT = {}
-        gr = {}
-        ec = {}
-        es = {}
-        rs = {}
-        rinv = {}
-        osb = {}
+        v_grouped = {}
+        v_codes = {}
+        v_scales = {}
+        bias = {}
+        w_banks = {}
+        minus_z = {}
+        minus_max_half = {}
+        minus_max = {}
+        row_sums = {}
+        e_sb = {}
+        eT_bank = {}
+        eT_sb = {}
+        e_grouped = {}
+        e_codes = {}
+        e_scales = {}
+        inv_sums = {}
+        o_bank = {}
+        o_sb = {}
 
-        tps = {}
-
-        def trans_q_pe(bh):
-            tps[bh] = ps_t.tile([P, NT, P], BF16, name="tq", tag="t")
+        def transpose_q(bh):
+            t_bank[bh] = ps_t.tile([P, NT, P], BF16, name="tq", tag="t")
             for t in range(NT):
-                nc.tensor.transpose(out=tps[bh][:, t, :], in_=qr[bh][:, t, :], identity=ident_bf[:])
+                nc.tensor.transpose(out=t_bank[bh][:, t, :], in_=q_raw[bh][:, t, :], identity=ident_bf[:])
 
-        def trans_q_cp(bh):
+        def copy_qT(bh):
             h = bh % H
             qT[bh] = work2.tile([P, NT * P], BF16, name="qT", tag="qT")
             nc.vector.tensor_scalar(
                 out=qT[bh][:],
-                in0=tps[bh][:].rearrange("p t c -> p (t c)"),
-                scalar1=sgn[:, h : h + 1],
+                in0=t_bank[bh][:].rearrange("p t c -> p (t c)"),
+                scalar1=sign[:, h : h + 1],
                 scalar2=None,
                 op0=ALU.mult,
             )
 
-        def trans_k_pe(bh):
-            tps[bh] = ps_t.tile([P, NT, P], BF16, name="tq", tag="t")
+        def transpose_k(bh):
+            t_bank[bh] = ps_t.tile([P, NT, P], BF16, name="tq", tag="t")
             for c in range(NT):
-                nc.tensor.transpose(out=tps[bh][:, c, :], in_=kr[bh][:, c // 4, c % 4, :], identity=ident_bf[:])
+                nc.tensor.transpose(
+                    out=t_bank[bh][:, c, :], in_=k_raw[bh][:, c // PACK, c % PACK, :], identity=ident_bf[:]
+                )
 
-        def trans_k_cp(bh):
+        def copy_kT(bh):
             kT[bh] = work2.tile([P, NT * P], BF16, name="kT", tag="kT")
-            nc.vector.tensor_copy(out=kT[bh][:], in_=tps[bh][:].rearrange("p t c -> p (t c)"))
+            nc.vector.tensor_copy(out=kT[bh][:], in_=t_bank[bh][:].rearrange("p t c -> p (t c)"))
 
-        def v_group(bh):
-            vg[bh] = work2.tile([P, 2, D, 4], BF16, name="vg", tag="vg", align_bytes=64)
+        def group_v(bh):
+            v_grouped[bh] = work2.tile([P, PASSES, D, PACK], BF16, name="vg", tag="vg", align_bytes=64)
             nc.gpsimd.tensor_scalar(
-                out=vg[bh][:],
-                in0=vr[bh][:].rearrange("p g j d -> p g d j"),
+                out=v_grouped[bh][:],
+                in0=v_raw[bh][:].rearrange("p g j d -> p g d j"),
                 scalar1=1.0,
                 scalar2=0.0,
                 op0=ALU.mult,
                 op1=ALU.add,
             )
 
-        def v_quant(bh):
-            vc[bh] = work2.tile([P, 2 * D], U32, name="vc", tag="vc", align_bytes=64)
-            vs[bh] = work2.tile([P, 2 * D], U8, name="vs", tag="vs", align_bytes=64)
+        def quantise_v(bh):
+            v_codes[bh] = work2.tile([P, PASSES * D], U32, name="vc", tag="vc", align_bytes=64)
+            v_scales[bh] = work2.tile([P, PASSES * D], U8, name="vs", tag="vs", align_bytes=64)
             nc.vector.quantize_mx(
-                out=vc[bh][:].bitcast(FP8X4), scales=vs[bh][:], in_=vg[bh][:].rearrange("p g d j -> p (g d j)")
+                out=v_codes[bh][:].bitcast(FP8X4),
+                scales=v_scales[bh][:],
+                in_=v_grouped[bh][:].rearrange("p g d j -> p (g d j)"),
             )
 
-        def x1(pair):
-            tau = pair * 2
-            bh, t = tau // NT, tau % NT
+        def bias_exp(pair):
+            tile = pair * 2
+            bh, t = tile // NT, tile % NT
             b, h = bh // H, bh % H
-            et[pair] = work2.tile([P, NT, 2 * P], F32, name="et", tag="et")
-            pieces = 2 if pair == 0 else 1
-            wid = 2 * P // pieces
-            for k2 in range(pieces):
+            bias[pair] = work2.tile([P, NT, 2 * P], F32, name="et", tag="et")
+            cuts = 2 if pair == 0 else 1
+            width = 2 * P // cuts
+            for cut in range(cuts):
                 nc.scalar.activation(
-                    out=et[pair][:, :, k2 * wid : (k2 + 1) * wid],
-                    in_=dT[b][:, :, t * P + k2 * wid : t * P + (k2 + 1) * wid],
+                    out=bias[pair][:, :, cut * width : (cut + 1) * width],
+                    in_=dist[b][:, :, t * P + cut * width : t * P + (cut + 1) * width],
                     func=ACTF.Exp,
-                    scale=nbeta[:, h : h + 1],
-                    bias=lna[:, h : h + 1],
+                    scale=minus_beta[:, h : h + 1],
+                    bias=ln_height[:, h : h + 1],
                 )
 
-        def wmm(tau):
-            bh, t = tau // NT, tau % NT
-            wt[tau] = []
-            for g in range(2):
-                wg = ps_w.tile([P, 512], F32, name="wg", tag="w")
+        def scores(tile):
+            bh, t = tile // NT, tile % NT
+            w_banks[tile] = []
+            for g in range(PASSES):
+                bank = ps_w.tile([P, BANK], F32, name="wg", tag="w")
                 nc.tensor.matmul(
-                    out=wg[:],
+                    out=bank[:],
                     lhsT=qT[bh][:, t * P : (t + 1) * P],
-                    rhs=kT[bh][:, g * 512 : (g + 1) * 512],
+                    rhs=kT[bh][:, g * BANK : (g + 1) * BANK],
                     start=True,
                     stop=False,
                 )
-                wt[tau].append(wg)
-            for g in range(2):
-                for j in range(4):
+                w_banks[tile].append(bank)
+            for g in range(PASSES):
+                for j in range(PACK):
                     nc.tensor.matmul(
-                        out=wt[tau][g][:, j * P : (j + 1) * P],
-                        lhsT=et[tau // 2][:, g * 4 + j, (tau % 2) * P : (tau % 2 + 1) * P],
+                        out=w_banks[tile][g][:, j * P : (j + 1) * P],
+                        lhsT=bias[tile // 2][:, g * PACK + j, (tile % 2) * P : (tile % 2 + 1) * P],
                         rhs=ident_f[:],
                         is_transpose=True,
                         start=False,
-                        stop=(j == 3),
+                        stop=(j == PACK - 1),
                     )
 
-        def m_half(tau, g):
-            h = (tau // NT) % H
+        def row_max(tile, g):
+            h = (tile // NT) % H
             if g == 0:
-                zt[tau] = work4.tile([P, S], F32, name="zt", tag="zt")
-                nb0[tau] = small.tile([P, 1], F32, name="nb0", tag="nb0")
+                minus_z[tile] = work4.tile([P, S], F32, name="zt", tag="zt")
+                minus_max_half[tile] = small.tile([P, 1], F32, name="nb0", tag="nb0")
                 nc.vector.tensor_scalar(
-                    out=zt[tau][:, 0:512],
-                    in0=wt[tau][0][:],
-                    scalar1=scneg[:, h : h + 1],
+                    out=minus_z[tile][:, 0:BANK],
+                    in0=w_banks[tile][0][:],
+                    scalar1=to_minus_z[:, h : h + 1],
                     scalar2=None,
                     op0=ALU.mult,
                     op1=ALU.min,
-                    accum_out=nb0[tau][:],
+                    accum_out=minus_max_half[tile][:],
                 )
             else:
-                nb[tau] = work4.tile([P, 1], F32, name="nb", tag="nb")
+                minus_max[tile] = work4.tile([P, 1], F32, name="nb", tag="nb")
                 nc.vector.tensor_scalar(
-                    out=zt[tau][:, 512:1024],
-                    in0=wt[tau][1][:],
-                    scalar1=scneg[:, h : h + 1],
-                    scalar2=nb0[tau][:],
+                    out=minus_z[tile][:, BANK:S],
+                    in0=w_banks[tile][1][:],
+                    scalar1=to_minus_z[:, h : h + 1],
+                    scalar2=minus_max_half[tile][:],
                     op0=ALU.mult,
                     op1=ALU.min,
-                    accum_out=nb[tau][:],
+                    accum_out=minus_max[tile][:],
                 )
 
-        def x2(tau):
-            bh, t = tau // NT, tau % NT
+        def softmax_exp(tile):
+            bh, t = tile // NT, tile % NT
             if t == 0:
-                rs[bh] = work2.tile([P, NT], F32, name="rs", tag="rs")
-            ee[tau] = work3.tile([P, S], BF16, name="ee", tag="ee")
+                row_sums[bh] = work2.tile([P, NT], F32, name="rs", tag="rs")
+            e_sb[tile] = work3.tile([P, S], BF16, name="ee", tag="ee")
             nc.scalar.activation(
-                out=ee[tau][:],
-                in_=zt[tau][:],
+                out=e_sb[tile][:],
+                in_=minus_z[tile][:],
                 func=ACTF.Exp,
                 scale=-1.0,
-                bias=nb[tau][:],
-                accum_out=rs[bh][:, t : t + 1],
+                bias=minus_max[tile][:],
+                accum_out=row_sums[bh][:, t : t + 1],
             )
 
-        def te(tau):
-            eT[tau] = ps_t.tile([P, NT, P], BF16, name="eT", tag="t")
+        def transpose_e(tile):
+            eT_bank[tile] = ps_t.tile([P, NT, P], BF16, name="eT", tag="t")
             for c in range(NT):
-                nc.tensor.transpose(out=eT[tau][:, c, :], in_=ee[tau][:, c * P : (c + 1) * P], identity=ident_bf[:])
+                nc.tensor.transpose(
+                    out=eT_bank[tile][:, c, :], in_=e_sb[tile][:, c * P : (c + 1) * P], identity=ident_bf[:]
+                )
 
-        es1 = {}
-        g4 = {}
-
-        def c1(tau):
-            es1[tau] = work3.tile([P, NT * P], BF16, name="es1", tag="es1")
-            src = eT[tau][:].rearrange("p c q -> p (c q)")
-            if tau % 4 == ACT_C1_INDEX:
-                nc.scalar.copy(out=es1[tau][:], in_=src)
+        def copy_eT(tile):
+            eT_sb[tile] = work3.tile([P, NT * P], BF16, name="es1", tag="es1")
+            src = eT_bank[tile][:].rearrange("p c q -> p (c q)")
+            if tile % GROUP == SCALAR_RANK:
+                nc.scalar.copy(out=eT_sb[tile][:], in_=src)
             else:
-                nc.vector.tensor_copy(out=es1[tau][:], in_=src)
+                nc.vector.tensor_copy(out=eT_sb[tile][:], in_=src)
 
-        def c2(tau):
-            u, i = tau // 4, tau % 4
-            if i == 0:
-                g4[u] = work2.tile([P, 4, 2, P, 4], BF16, name="g4", tag="g4", align_bytes=64)
+        def group_e(tile):
+            u, rank = tile // GROUP, tile % GROUP
+            if rank == 0:
+                e_grouped[u] = work2.tile([P, GROUP, PASSES, P, PACK], BF16, name="g4", tag="g4", align_bytes=64)
             nc.gpsimd.tensor_scalar(
-                out=g4[u][:, i],
-                in0=es1[tau][:].rearrange("p (g j c) -> p g c j", g=2, j=4),
+                out=e_grouped[u][:, rank],
+                in0=eT_sb[tile][:].rearrange("p (g j c) -> p g c j", g=PASSES, j=PACK),
                 scalar1=1.0,
                 scalar2=0.0,
                 op0=ALU.mult,
                 op1=ALU.add,
             )
 
-        def q4(u):
-            ec[u] = work2.tile([P, 4, 2 * P], U32, name="ec", tag="ec", align_bytes=64)
-            es[u] = work2.tile([P, 4, 2 * P], U8, name="es", tag="es", align_bytes=64)
+        def quantise_group(u):
+            e_codes[u] = work2.tile([P, GROUP, PASSES * P], U32, name="ec", tag="ec", align_bytes=64)
+            e_scales[u] = work2.tile([P, GROUP, PASSES * P], U8, name="es", tag="es", align_bytes=64)
             nc.vector.quantize_mx(
-                out=ec[u][:].rearrange("p i w -> p (i w)").bitcast(FP8X4),
-                scales=es[u][:].rearrange("p i w -> p (i w)"),
-                in_=g4[u][:].rearrange("p i g c j -> p (i g c j)"),
+                out=e_codes[u][:].rearrange("p i w -> p (i w)").bitcast(FP8X4),
+                scales=e_scales[u][:].rearrange("p i w -> p (i w)"),
+                in_=e_grouped[u][:].rearrange("p i g c j -> p (i g c j)"),
             )
 
-        def c_direct(tau, on_act):
-            u, i = tau // 4, tau % 4
-            src = eT[tau][:].rearrange("p (g j) c -> p g c j", j=4)
-            if on_act:
-                nc.scalar.copy(out=g4[u][:, i], in_=src)
+        def group_e_from_psum(tile, on_scalar):
+            u, rank = tile // GROUP, tile % GROUP
+            src = eT_bank[tile][:].rearrange("p (g j) c -> p g c j", j=PACK)
+            if on_scalar:
+                nc.scalar.copy(out=e_grouped[u][:, rank], in_=src)
             else:
-                nc.vector.tensor_copy(out=g4[u][:, i], in_=src)
+                nc.vector.tensor_copy(out=e_grouped[u][:, rank], in_=src)
 
-        def q1(tau):
-            u, i = tau // 4, tau % 4
-            if i == 0:
-                ec[u] = work2.tile([P, 4, 2 * P], U32, name="ec", tag="ec", align_bytes=64)
-                es[u] = work2.tile([P, 4, 2 * P], U8, name="es", tag="es", align_bytes=64)
+        def quantise_tile(tile):
+            u, rank = tile // GROUP, tile % GROUP
+            if rank == 0:
+                e_codes[u] = work2.tile([P, GROUP, PASSES * P], U32, name="ec", tag="ec", align_bytes=64)
+                e_scales[u] = work2.tile([P, GROUP, PASSES * P], U8, name="es", tag="es", align_bytes=64)
             nc.vector.quantize_mx(
-                out=ec[u][:, i, :].bitcast(FP8X4),
-                scales=es[u][:, i, :],
-                in_=g4[u][:, i].rearrange("p g c j -> p (g c j)"),
+                out=e_codes[u][:, rank, :].bitcast(FP8X4),
+                scales=e_scales[u][:, rank, :],
+                in_=e_grouped[u][:, rank].rearrange("p g c j -> p (g c j)"),
             )
 
-        def r_inv(u):
-            bh, uu = u // 2, u % 2
-            rinv[u] = small.tile([P, 4], F32, name="rinv", tag="rinv")
-            nc.vector.reciprocal(out=rinv[u][:], in_=rs[bh][:, uu * 4 : uu * 4 + 4])
+        def invert_sums(u):
+            bh, first = u // GROUPS_PER_HEAD, (u % GROUPS_PER_HEAD) * GROUP
+            inv_sums[u] = small.tile([P, GROUP], F32, name="rinv", tag="rinv")
+            nc.vector.reciprocal(out=inv_sums[u][:], in_=row_sums[bh][:, first : first + GROUP])
 
-        ob = {}
-
-        def mx1(tau):
-            u, i = tau // 4, tau % 4
-            bh = u // 2
-            if i == 0:
-                ob[u] = ps_t.tile([P, 4, D], F32, name="ob", tag="t")
-            for g in range(2):
+        def multiply_tile(tile):
+            u, rank = tile // GROUP, tile % GROUP
+            bh = u // GROUPS_PER_HEAD
+            if rank == 0:
+                o_bank[u] = ps_t.tile([P, GROUP, D], F32, name="ob", tag="t")
+            for g in range(PASSES):
                 nc.tensor.matmul_mx(
-                    out=ob[u][:, i, :],
-                    lhsT=ec[u][:, i, g * P : (g + 1) * P].bitcast(FP8X4),
-                    lhsT_scale=es[u][:, i, g * P : (g + 1) * P],
-                    rhs=vc[bh][:, g * D : (g + 1) * D].bitcast(FP8X4),
-                    rhs_scale=vs[bh][:, g * D : (g + 1) * D],
+                    out=o_bank[u][:, rank, :],
+                    lhsT=e_codes[u][:, rank, g * P : (g + 1) * P].bitcast(FP8X4),
+                    lhsT_scale=e_scales[u][:, rank, g * P : (g + 1) * P],
+                    rhs=v_codes[bh][:, g * D : (g + 1) * D].bitcast(FP8X4),
+                    rhs_scale=v_scales[bh][:, g * D : (g + 1) * D],
                     start=(g == 0),
-                    stop=(g == 1),
+                    stop=(g == PASSES - 1),
                 )
 
-        def mxg(u):
-            for i in range(4):
-                mx1(u * 4 + i)
+        def multiply_group(u):
+            for rank in range(GROUP):
+                multiply_tile(u * GROUP + rank)
 
-        def norm_half(u, hh):
-            bh, uu = u // 2, u % 2
+        def normalise(u, g_half):
+            bh, first = u // GROUPS_PER_HEAD, (u % GROUPS_PER_HEAD) * GROUP
             b, h = bh // H, bh % H
-            if uu == 0 and hh == 0:
-                osb[bh] = work2.tile([P, NT, D], F32, name="osb", tag="osb")
-            t0 = uu * 4 + hh * 2
+            if first == 0 and g_half == 0:
+                o_sb[bh] = work2.tile([P, NT, D], F32, name="osb", tag="osb")
+            t0 = first + g_half * 2
             nc.vector.tensor_tensor(
-                out=osb[bh][:, t0 : t0 + 2, :],
-                in0=ob[u][:, hh * 2 : hh * 2 + 2, :],
-                in1=rinv[u][:, hh * 2 : hh * 2 + 2].unsqueeze(2).to_broadcast([P, 2, D]),
+                out=o_sb[bh][:, t0 : t0 + 2, :],
+                in0=o_bank[u][:, g_half * 2 : g_half * 2 + 2, :],
+                in1=inv_sums[u][:, g_half * 2 : g_half * 2 + 2].unsqueeze(2).to_broadcast([P, 2, D]),
                 op=ALU.mult,
             )
             dram = out[b, h].rearrange("(p t) d -> p t d", t=NT)
-            if u == NTILES // 4 - 1:
-                nc.sync.dma_start(out=dram[:, t0 : t0 + 2, :], in_=osb[bh][:, t0 : t0 + 2, :])
-            elif hh == 1:
-                nc.sync.dma_start(out=dram[:, uu * 4 : uu * 4 + 4, :], in_=osb[bh][:, uu * 4 : uu * 4 + 4, :])
+            if u == NGROUPS - 1:
+                nc.sync.dma_start(out=dram[:, t0 : t0 + 2, :], in_=o_sb[bh][:, t0 : t0 + 2, :])
+            elif g_half == 1:
+                nc.sync.dma_start(
+                    out=dram[:, first : first + GROUP, :], in_=o_sb[bh][:, first : first + GROUP, :]
+                )
 
-        trans_q_pe(0)
-        trans_q_cp(0)
-        trans_k_pe(0)
-        trans_k_cp(0)
-        v_group(0)
+        transpose_q(0)
+        copy_qT(0)
+        transpose_k(0)
+        copy_kT(0)
+        group_v(0)
 
-        def ok(tau):
-            return 0 <= tau < NTILES
+        def is_tile(x):
+            return 0 <= x < NTILES
 
-        def grp(x):
-            return x // 4 if (x % 4 == 3 and 0 <= x < NTILES) else -1
+        def group_ending_at(x):
+            return x // GROUP if (x % GROUP == GROUP - 1 and is_tile(x)) else -1
 
-        def head(x):
+        def head_starting_at(x):
             return x // NT if (x % NT == 0 and NT <= x < NTILES) else -1
 
-        d1_todo = [(0, half, c) for half in range(2) for c in range(4)] + [(1, 1, c) for c in range(4, 8)]
-        d1_done = 0
+        later_dist = [(False, q_half, c) for q_half in range(2) for c in range(FIRST_SUMMED_CHUNK)] + [
+            (c < NT - 1, 1, c) for c in range(FIRST_SUMMED_CHUNK, NT)
+        ]
+        later_done = 0
 
         for n in range(-4, NTILES + 1):
-            i = (n - 2) % 4
-            if ok(n):
-                x2(n)
-            if ok(n - 1):
-                te(n - 1)
-            if grp(n - 5) >= 0:
-                mxg(grp(n - 5))
-            if ok(n + 2):
-                m_half(n + 2, 0)
-            if grp(n - 6) >= 0:
-                norm_half(grp(n - 6), 0)
-            if grp(n - 7) >= 0:
-                norm_half(grp(n - 7), 1)
-            if grp(n - 5) >= 0:
-                r_inv(grp(n - 5))
-            if head(n + 4) >= 0:
-                trans_k_cp(head(n + 4))
-            if (i == 1 or i == 3) and ok(n - 2):
-                c1(n - 2)
-                c2(n - 2)
-            if ok(n + 4) and n % 2 == 0:
-                x1((n + 4) // 2)
-            if i == 2 and ok(n - 2) and n - 2 < NTILES - 2:
-                c1(n - 2)
-                c2(n - 2)
-            if head(n + 6) >= 0:
-                trans_q_cp(head(n + 6))
-            if ok(n + 3):
-                wmm(n + 3)
-            if ok(n + 2):
-                m_half(n + 2, 1)
-            if n == 2 or head(n - 2) >= 0:
-                v_quant((n - 2) // NT)
-            if grp(n - 3) >= 0:
-                q4(grp(n - 3))
-            if i == 0 and ok(n - 2):
-                c1(n - 2)
-                c2(n - 2)
-            if head(n + 1) >= 0:
-                v_group(head(n + 1))
-            if head(n + 7) >= 0:
-                trans_q_pe(head(n + 7))
-            if head(n + 5) >= 0:
-                trans_k_pe(head(n + 5))
-            if n % NT == 0 and 0 <= n // NT and n // NT + RAWB < NHEAD:
+            rank = (n - 2) % GROUP
+            if is_tile(n):
+                softmax_exp(n)
+            if is_tile(n - 1):
+                transpose_e(n - 1)
+            if group_ending_at(n - 5) >= 0:
+                multiply_group(group_ending_at(n - 5))
+            if is_tile(n + 2):
+                row_max(n + 2, 0)
+            if group_ending_at(n - 6) >= 0:
+                normalise(group_ending_at(n - 6), 0)
+            if group_ending_at(n - 7) >= 0:
+                normalise(group_ending_at(n - 7), 1)
+            if group_ending_at(n - 5) >= 0:
+                invert_sums(group_ending_at(n - 5))
+            if head_starting_at(n + 4) >= 0:
+                copy_kT(head_starting_at(n + 4))
+            if (rank == 1 or rank == 3) and is_tile(n - 2):
+                copy_eT(n - 2)
+                group_e(n - 2)
+            if is_tile(n + 4) and n % 2 == 0:
+                bias_exp((n + 4) // 2)
+            if rank == SCALAR_RANK and is_tile(n - 2) and n - 2 < NTILES - 2:
+                copy_eT(n - 2)
+                group_e(n - 2)
+            if head_starting_at(n + 6) >= 0:
+                copy_qT(head_starting_at(n + 6))
+            if is_tile(n + 3):
+                scores(n + 3)
+            if is_tile(n + 2):
+                row_max(n + 2, 1)
+            if n == 2 or head_starting_at(n - 2) >= 0:
+                quantise_v((n - 2) // NT)
+            if group_ending_at(n - 3) >= 0:
+                quantise_group(group_ending_at(n - 3))
+            if rank == 0 and is_tile(n - 2):
+                copy_eT(n - 2)
+                group_e(n - 2)
+            if head_starting_at(n + 1) >= 0:
+                group_v(head_starting_at(n + 1))
+            if head_starting_at(n + 7) >= 0:
+                transpose_q(head_starting_at(n + 7))
+            if head_starting_at(n + 5) >= 0:
+                transpose_k(head_starting_at(n + 5))
+            if n % NT == 0 and n // NT + RAWB < NHEAD:
                 load(n // NT + RAWB)
             if n == -4 or n == -3:
-                for c in range(4):
-                    dist_tile(0, 1, (n + 4) * 4 + c, ps_t, "t", False)
+                for step in range(4):
+                    dist_by_matmul(0, 1, (n + 4) * 4 + step, ps_t, "t", False)
             if n == -1 or n == 0:
-                for rep in range(2):
-                    dist_tile_sp(0, 4 + (n + 1) * 2 + rep, ps_t, "t")
+                for step in range(2):
+                    dist_by_transposes(0, FIRST_SUMMED_CHUNK + (n + 1) * 2 + step)
             if n == 0:
-                for t in range(4, 8):
-                    u_tile(t)
-            if n >= 5 and n % NT in (2, 5, 6, 7) and d1_done < 12:
-                kind, half, c = d1_todo[d1_done]
-                d1_done += 1
-                if kind == 0:
-                    dist_tile(1, half, c, ps_t, "t", False)
+                for t in range(TILES_PER_BANK, NT):
+                    product_tile(t)
+            if n >= 5 and n % NT in (2, 5, 6, 7) and later_done < len(later_dist):
+                by_transposes, q_half, c = later_dist[later_done]
+                later_done += 1
+                if by_transposes:
+                    dist_by_transposes(q_half, c)
                 else:
-                    dist_tile_sp(half, c, ps_t, "t")
+                    dist_by_matmul(1, q_half, c, ps_t, "t", False)
             if n == NTILES - 1:
-                q1(NTILES - 4)
-                mx1(NTILES - 4)
+                quantise_tile(NTILES - 4)
+                multiply_tile(NTILES - 4)
             if n == NTILES:
-                c_direct(NTILES - 2, True)
-                q1(NTILES - 3)
-                mx1(NTILES - 3)
-                r_inv(NTILES // 4 - 1)
+                group_e_from_psum(NTILES - 2, True)
+                quantise_tile(NTILES - 3)
+                multiply_tile(NTILES - 3)
+                invert_sums(NGROUPS - 1)
 
-        c_direct(NTILES - 1, False)
-        q1(NTILES - 2)
-        q1(NTILES - 1)
-        mx1(NTILES - 2)
-        mx1(NTILES - 1)
-        norm_half(NTILES // 4 - 2, 0)
-        norm_half(NTILES // 4 - 2, 1)
-        norm_half(NTILES // 4 - 1, 0)
-        norm_half(NTILES // 4 - 1, 1)
+        group_e_from_psum(NTILES - 1, False)
+        quantise_tile(NTILES - 2)
+        quantise_tile(NTILES - 1)
+        multiply_tile(NTILES - 2)
+        multiply_tile(NTILES - 1)
+        normalise(NGROUPS - 2, 0)
+        normalise(NGROUPS - 2, 1)
+        normalise(NGROUPS - 1, 0)
+        normalise(NGROUPS - 1, 1)

@@ -25,6 +25,7 @@ NT = 8
 BANK = 512
 PACK = 4
 PASSES = 2
+WORD_BLOCKS = 4
 GROUP = 4
 GROUPS_PER_HEAD = NT // GROUP
 TILES_PER_BANK = BANK // P
@@ -225,7 +226,6 @@ def tile_rbfbias_kernel(tc, q, k, v, qs_s, ks_s, alpha, beta, out):
         row_sums = {}
         e_sb = {}
         eT_bank = {}
-        eT_sb = {}
         e_grouped = {}
         e_codes = {}
         e_scales = {}
@@ -352,8 +352,8 @@ def tile_rbfbias_kernel(tc, q, k, v, qs_s, ks_s, alpha, beta, out):
                 row_sums[bh] = work2.tile([P, NT], F32, name="rs", tag="rs")
             e_sb[tile] = work3.tile([P, S], BF16, name="ee", tag="ee")
             nc.scalar.activation(
-                out=e_sb[tile][:],
-                in_=minus_z[tile][:],
+                out=e_sb[tile][:].rearrange("q (a p e) -> q a p e", a=WORD_BLOCKS, e=2),
+                in_=minus_z[tile][:].rearrange("q (a e p) -> q a p e", a=WORD_BLOCKS, e=2),
                 func=ACTF.Exp,
                 scale=-1.0,
                 bias=minus_max[tile][:],
@@ -361,32 +361,23 @@ def tile_rbfbias_kernel(tc, q, k, v, qs_s, ks_s, alpha, beta, out):
             )
 
         def transpose_e(tile):
-            eT_bank[tile] = ps_t.tile([P, NT, P], BF16, name="eT", tag="t")
-            for c in range(NT):
+            eT_bank[tile] = ps_t.tile([P, WORD_BLOCKS, P], F32, name="eT", tag="t")
+            words = e_sb[tile][:].bitcast(F32)
+            for a in range(WORD_BLOCKS):
                 nc.tensor.transpose(
-                    out=eT_bank[tile][:, c, :], in_=e_sb[tile][:, c * P : (c + 1) * P], identity=ident_bf[:]
+                    out=eT_bank[tile][:, a, :], in_=words[:, a * P : (a + 1) * P], identity=ident_f[:]
                 )
 
-        def copy_eT(tile):
-            eT_sb[tile] = work3.tile([P, NT * P], BF16, name="es1", tag="es1")
-            src = eT_bank[tile][:].rearrange("p c q -> p (c q)")
-            if tile % GROUP == SCALAR_RANK:
-                nc.scalar.copy(out=eT_sb[tile][:], in_=src)
-            else:
-                nc.vector.tensor_copy(out=eT_sb[tile][:], in_=src)
-
-        def group_e(tile):
+        def group_e(tile, on_scalar):
             u, rank = tile // GROUP, tile % GROUP
             if rank == 0:
                 e_grouped[u] = work2.tile([P, GROUP, PASSES, P, PACK], BF16, name="g4", tag="g4", align_bytes=64)
-            nc.gpsimd.tensor_scalar(
-                out=e_grouped[u][:, rank],
-                in0=eT_sb[tile][:].rearrange("p (g j c) -> p g c j", g=PASSES, j=PACK),
-                scalar1=1.0,
-                scalar2=0.0,
-                op0=ALU.mult,
-                op1=ALU.add,
-            )
+            dst = e_grouped[u][:, rank].bitcast(F32)
+            src = eT_bank[tile][:].rearrange("p (g u) q -> p g q u", u=2)
+            if on_scalar:
+                nc.scalar.copy(out=dst, in_=src)
+            else:
+                nc.vector.tensor_copy(out=dst, in_=src)
 
         def quantise_group(u):
             e_codes[u] = work2.tile([P, GROUP, PASSES * P], U32, name="ec", tag="ec", align_bytes=64)
@@ -396,14 +387,6 @@ def tile_rbfbias_kernel(tc, q, k, v, qs_s, ks_s, alpha, beta, out):
                 scales=e_scales[u][:].rearrange("p i w -> p (i w)"),
                 in_=e_grouped[u][:].rearrange("p i g c j -> p (i g c j)"),
             )
-
-        def group_e_from_psum(tile, on_scalar):
-            u, rank = tile // GROUP, tile % GROUP
-            src = eT_bank[tile][:].rearrange("p (g j) c -> p g c j", j=PACK)
-            if on_scalar:
-                nc.scalar.copy(out=e_grouped[u][:, rank], in_=src)
-            else:
-                nc.vector.tensor_copy(out=e_grouped[u][:, rank], in_=src)
 
         def quantise_tile(tile):
             u, rank = tile // GROUP, tile % GROUP
@@ -500,13 +483,11 @@ def tile_rbfbias_kernel(tc, q, k, v, qs_s, ks_s, alpha, beta, out):
             if head_starting_at(n + 4) >= 0:
                 copy_kT(head_starting_at(n + 4))
             if (rank == 1 or rank == 3) and is_tile(n - 2):
-                copy_eT(n - 2)
-                group_e(n - 2)
+                group_e(n - 2, False)
             if is_tile(n + 4) and n % 2 == 0:
                 bias_exp((n + 4) // 2)
             if rank == SCALAR_RANK and is_tile(n - 2) and n - 2 < NTILES - 2:
-                copy_eT(n - 2)
-                group_e(n - 2)
+                group_e(n - 2, True)
             if head_starting_at(n + 6) >= 0:
                 copy_qT(head_starting_at(n + 6))
             if is_tile(n + 3):
@@ -518,8 +499,7 @@ def tile_rbfbias_kernel(tc, q, k, v, qs_s, ks_s, alpha, beta, out):
             if group_ending_at(n - 3) >= 0:
                 quantise_group(group_ending_at(n - 3))
             if rank == 0 and is_tile(n - 2):
-                copy_eT(n - 2)
-                group_e(n - 2)
+                group_e(n - 2, False)
             if head_starting_at(n + 1) >= 0:
                 group_v(head_starting_at(n + 1))
             if head_starting_at(n + 7) >= 0:
@@ -548,12 +528,12 @@ def tile_rbfbias_kernel(tc, q, k, v, qs_s, ks_s, alpha, beta, out):
                 quantise_tile(NTILES - 4)
                 multiply_tile(NTILES - 4)
             if n == NTILES:
-                group_e_from_psum(NTILES - 2, True)
+                group_e(NTILES - 2, True)
                 quantise_tile(NTILES - 3)
                 multiply_tile(NTILES - 3)
                 invert_sums(NGROUPS - 1)
 
-        group_e_from_psum(NTILES - 1, False)
+        group_e(NTILES - 1, False)
         quantise_tile(NTILES - 2)
         quantise_tile(NTILES - 1)
         multiply_tile(NTILES - 2)

@@ -34,7 +34,7 @@ NTILES = NHEAD * NT
 NGROUPS = NTILES // GROUP
 FIRST_SUMMED_CHUNK = 4
 RAWB = 4
-SCALAR_RANK = 2
+SCALAR_TILES = (2,)
 
 
 def tile_rbfbias_kernel(tc, q, k, v, qs_s, ks_s, alpha, beta, out):
@@ -482,11 +482,11 @@ def tile_rbfbias_kernel(tc, q, k, v, qs_s, ks_s, alpha, beta, out):
                 invert_sums(group_ending_at(n - 5))
             if head_starting_at(n + 4) >= 0:
                 copy_kT(head_starting_at(n + 4))
-            if (rank == 1 or rank == 3) and is_tile(n - 2):
+            if rank != 0 and is_tile(n - 2) and n - 2 < NTILES - 2 and (n - 2) % NT not in SCALAR_TILES:
                 group_e(n - 2, False)
             if is_tile(n + 4) and n % 2 == 0:
                 bias_exp((n + 4) // 2)
-            if rank == SCALAR_RANK and is_tile(n - 2) and n - 2 < NTILES - 2:
+            if is_tile(n - 2) and n - 2 < NTILES - 2 and (n - 2) % NT in SCALAR_TILES:
                 group_e(n - 2, True)
             if head_starting_at(n + 6) >= 0:
                 copy_qT(head_starting_at(n + 6))
@@ -498,7 +498,7 @@ def tile_rbfbias_kernel(tc, q, k, v, qs_s, ks_s, alpha, beta, out):
                 quantise_v((n - 2) // NT)
             if group_ending_at(n - 3) >= 0:
                 quantise_group(group_ending_at(n - 3))
-            if rank == 0 and is_tile(n - 2):
+            if rank == 0 and is_tile(n - 2) and (n - 2) % NT not in SCALAR_TILES:
                 group_e(n - 2, False)
             if head_starting_at(n + 1) >= 0:
                 group_v(head_starting_at(n + 1))

@@ -34,7 +34,7 @@ NTILES = NHEAD * NT
 NGROUPS = NTILES // GROUP
 FIRST_SUMMED_CHUNK = 4
 RAWB = 4
-SCALAR_TILES = (2,)
+SCALAR_TILES = (0, 4)
 
 
 def tile_rbfbias_kernel(tc, q, k, v, qs_s, ks_s, alpha, beta, out):
@@ -67,9 +67,6 @@ def tile_rbfbias_kernel(tc, q, k, v, qs_s, ks_s, alpha, beta, out):
         beta_bf = const.tile([P, H], BF16, name="be_bf")
         nc.sync.dma_start(out=alpha_bf[:], in_=alpha.rearrange("h o -> (h o)").partition_broadcast(P))
         nc.sync.dma_start(out=beta_bf[:], in_=beta.rearrange("h o -> (h o)").partition_broadcast(P))
-        nc.sync.dma_start(
-            out=key_row[:], in_=ks_s[1, BANK:S, :].rearrange("k f -> (k f)").partition_broadcast(P)
-        )
 
         q_raw = {}
         k_raw = {}
@@ -88,7 +85,11 @@ def tile_rbfbias_kernel(tc, q, k, v, qs_s, ks_s, alpha, beta, out):
                 out=v_raw[bh][:], in_=v[b, h].rearrange("(g p j) d -> p g j d", g=PASSES, j=PACK)
             )
 
-        for bh in range(RAWB):
+        load(0)
+        nc.sync.dma_start(
+            out=key_row[:], in_=ks_s[1, BANK:S, :].rearrange("k f -> (k f)").partition_broadcast(P)
+        )
+        for bh in range(1, RAWB):
             load(bh)
 
         ident_bf = const.tile([P, P], BF16, name="ident_bf")
@@ -130,6 +131,8 @@ def tile_rbfbias_kernel(tc, q, k, v, qs_s, ks_s, alpha, beta, out):
         )
         ln_height = const.tile([P, H], F32, name="lna")
         nc.scalar.activation(out=ln_height[:], in_=height[:], func=ACTF.Ln)
+        table_change = const.tile([P, 1], F32, name="warm")
+        nc.scalar.activation(out=table_change[:], in_=ln_height[:, 0:1], func=ACTF.Exp)
         minus_beta = const.tile([P, H], F32, name="nbeta")
         nc.vector.tensor_scalar(out=minus_beta[:], in0=beta_bf[:], scalar1=-1.0, scalar2=None, op0=ALU.mult)
         to_minus_z = const.tile([P, H], F32, name="scneg")
@@ -143,15 +146,18 @@ def tile_rbfbias_kernel(tc, q, k, v, qs_s, ks_s, alpha, beta, out):
         )
 
         featT = {}
-        for slot in (0, 2, 1, 3):
-            bank = ps_t.tile([P, NT, P], BF16, name="tp", tag="t")
-            for t in range(NT):
-                nc.tensor.transpose(out=bank[:, t, :], in_=feat[:, slot, t, :], identity=ident_bf[:])
+        for slot in range(4):
             featT[slot] = const.tile([P, NT * P], BF16, name="featT%d" % slot)
-            if slot < 2:
-                nc.vector.tensor_copy(out=featT[slot][:], in_=bank[:].rearrange("p t c -> p (t c)"))
+
+        def transpose_feat(slot, first, last, on_scalar):
+            bank = ps_t.tile([P, NT, P], BF16, name="tp", tag="t")
+            for t in range(first, last):
+                nc.tensor.transpose(out=bank[:, t, :], in_=feat[:, slot, t, :], identity=ident_bf[:])
+            src = bank[:, first:last, :].rearrange("p t c -> p (t c)")
+            if on_scalar:
+                nc.scalar.copy(out=featT[slot][:, first * P : last * P], in_=src)
             else:
-                nc.scalar.copy(out=featT[slot][:], in_=bank[:].rearrange("p t c -> p (t c)"))
+                nc.vector.tensor_copy(out=featT[slot][:, first * P : last * P], in_=src)
 
         dist = [const.tile([P, NT, S], F32, name="dT%d" % b) for b in range(B)]
 
@@ -170,8 +176,27 @@ def tile_rbfbias_kernel(tc, q, k, v, qs_s, ks_s, alpha, beta, out):
             else:
                 nc.vector.tensor_copy(out=dst, in_=bank[:])
 
-        for c in range(NT):
-            dist_by_matmul(0, 0, c, ps_w, "w", c % 2 == 1)
+        def dist_of_pair(pair, c_pair, pool, tag, on_scalar):
+            bank = pool.tile([P, 2, 2 * P], F32, name="dps", tag=tag)
+            for i in range(2):
+                c = 2 * c_pair + i
+                nc.tensor.matmul(
+                    out=bank[:, i, :],
+                    lhsT=featT[2][:, c * P : (c + 1) * P],
+                    rhs=featT[0][:, pair * 2 * P : (pair + 1) * 2 * P],
+                    start=True,
+                    stop=True,
+                )
+            dst = dist[0][:, 2 * c_pair : 2 * c_pair + 2, pair * 2 * P : (pair + 1) * 2 * P]
+            if on_scalar:
+                nc.scalar.copy(out=dst, in_=bank[:])
+            else:
+                nc.vector.tensor_copy(out=dst, in_=bank[:])
+
+        transpose_feat(2, 0, NT, False)
+        transpose_feat(0, 0, 2, False)
+        for c_pair in range(NT // 2):
+            dist_of_pair(0, c_pair, ps_w, "w", c_pair % 2 == 1)
 
         key_feature = key_row[:].rearrange("x (p j f) -> x f j p", j=PACK, f=NF)
         products = {}
@@ -448,6 +473,7 @@ def tile_rbfbias_kernel(tc, q, k, v, qs_s, ks_s, alpha, beta, out):
         copy_qT(0)
         transpose_k(0)
         copy_kT(0)
+        transpose_feat(0, 2, NT, False)
         group_v(0)
 
         def is_tile(x):
@@ -459,9 +485,11 @@ def tile_rbfbias_kernel(tc, q, k, v, qs_s, ks_s, alpha, beta, out):
         def head_starting_at(x):
             return x // NT if (x % NT == 0 and NT <= x < NTILES) else -1
 
-        later_dist = [(False, q_half, c) for q_half in range(2) for c in range(FIRST_SUMMED_CHUNK)] + [
-            (c < NT - 1, 1, c) for c in range(FIRST_SUMMED_CHUNK, NT)
-        ]
+        later_dist = (
+            [(True, 0, c) for c in range(FIRST_SUMMED_CHUNK, NT)]
+            + [(False, q_half, c) for q_half in range(2) for c in range(FIRST_SUMMED_CHUNK)]
+            + [(c < NT - 1, 1, c) for c in range(FIRST_SUMMED_CHUNK, NT)]
+        )
         later_done = 0
 
         for n in range(-4, NTILES + 1):
@@ -508,15 +536,13 @@ def tile_rbfbias_kernel(tc, q, k, v, qs_s, ks_s, alpha, beta, out):
                 transpose_k(head_starting_at(n + 5))
             if n % NT == 0 and n // NT + RAWB < NHEAD:
                 load(n // NT + RAWB)
-            if n == -4 or n == -3:
-                for step in range(4):
-                    dist_by_matmul(0, 1, (n + 4) * 4 + step, ps_t, "t", False)
-            if n == -1 or n == 0:
-                for step in range(2):
-                    dist_by_transposes(0, FIRST_SUMMED_CHUNK + (n + 1) * 2 + step)
-            if n == 0:
-                for t in range(TILES_PER_BANK, NT):
-                    product_tile(t)
+            if n in (-4, -2, 0):
+                for c_pair in range(NT // 2):
+                    dist_of_pair((n + 6) // 2, c_pair, ps_t, "t", False)
+            if n == 2:
+                transpose_feat(1, 0, NT, False)
+            if n == 4:
+                transpose_feat(3, 0, NT, True)
             if n >= 5 and n % NT in (2, 5, 6, 7) and later_done < len(later_dist):
                 by_transposes, q_half, c = later_dist[later_done]
                 later_done += 1
@@ -524,6 +550,9 @@ def tile_rbfbias_kernel(tc, q, k, v, qs_s, ks_s, alpha, beta, out):
                     dist_by_transposes(q_half, c)
                 else:
                     dist_by_matmul(1, q_half, c, ps_t, "t", False)
+                if later_done == NT - FIRST_SUMMED_CHUNK:
+                    for t in range(TILES_PER_BANK, NT):
+                        product_tile(t)
             if n == NTILES - 1:
                 quantise_tile(NTILES - 4)
                 multiply_tile(NTILES - 4)

@@ -201,17 +201,17 @@ def tile_rbfbias_kernel(tc, q, k, v, qs_s, ks_s, alpha, beta, out):
         key_feature = key_row[:].rearrange("x (p j f) -> x f j p", j=PACK, f=NF)
         products = {}
 
-        def product_tile(t):
-            products[t] = upool.tile([P, NF, BANK], F32, name="uu", tag="uu")
-            for f in range(NF):
-                nc.gpsimd.tensor_scalar(
-                    out=products[t][:, f, :].rearrange("x (j p) -> x j p", j=PACK),
-                    in0=key_feature[:, f],
-                    scalar1=minus_2x[:, t * NF + f : t * NF + f + 1],
-                    scalar2=(norm2[:, 1, t : t + 1] if f == 0 else 0.0),
-                    op0=ALU.mult,
-                    op1=ALU.add,
-                )
+        def product(t, f):
+            if f == 0:
+                products[t] = upool.tile([P, NF, BANK], F32, name="uu", tag="uu")
+            nc.gpsimd.tensor_scalar(
+                out=products[t][:, f, :].rearrange("x (j p) -> x j p", j=PACK),
+                in0=key_feature[:, f],
+                scalar1=minus_2x[:, t * NF + f : t * NF + f + 1],
+                scalar2=(norm2[:, 1, t : t + 1] if f == 0 else 0.0),
+                op0=ALU.mult,
+                op1=ALU.add,
+            )
 
         def dist_by_transposes(q_half, c):
             bank = ps_t.tile([P, BANK], F32, name="dps", tag="t")
@@ -234,8 +234,7 @@ def tile_rbfbias_kernel(tc, q, k, v, qs_s, ks_s, alpha, beta, out):
                 op0=ALU.add,
             )
 
-        for t in range(TILES_PER_BANK):
-            product_tile(t)
+        products_to_do = [(t, f) for t in range(TILES_PER_BANK) for f in range(NF)]
 
         t_bank = {}
         qT = {}
@@ -349,26 +348,24 @@ def tile_rbfbias_kernel(tc, q, k, v, qs_s, ks_s, alpha, beta, out):
             h = (tile // NT) % H
             if g == 0:
                 minus_z[tile] = work4.tile([P, S], F32, name="zt", tag="zt")
-                minus_max_half[tile] = small.tile([P, 1], F32, name="nb0", tag="nb0")
-                nc.vector.tensor_scalar(
-                    out=minus_z[tile][:, 0:BANK],
-                    in0=w_banks[tile][0][:],
-                    scalar1=to_minus_z[:, h : h + 1],
-                    scalar2=None,
-                    op0=ALU.mult,
-                    op1=ALU.min,
-                    accum_out=minus_max_half[tile][:],
-                )
-            else:
+                minus_max_half[tile] = work4.tile([P, PASSES], F32, name="nb0", tag="nb0")
+            nc.vector.tensor_scalar(
+                out=minus_z[tile][:, g * BANK : (g + 1) * BANK],
+                in0=w_banks[tile][g][:],
+                scalar1=to_minus_z[:, h : h + 1],
+                scalar2=None,
+                op0=ALU.mult,
+                op1=ALU.min,
+                accum_out=minus_max_half[tile][:, g : g + 1],
+            )
+            if g == PASSES - 1:
                 minus_max[tile] = work4.tile([P, 1], F32, name="nb", tag="nb")
-                nc.vector.tensor_scalar(
-                    out=minus_z[tile][:, BANK:S],
-                    in0=w_banks[tile][1][:],
-                    scalar1=to_minus_z[:, h : h + 1],
-                    scalar2=minus_max_half[tile][:],
-                    op0=ALU.mult,
-                    op1=ALU.min,
-                    accum_out=minus_max[tile][:],
+                nc.gpsimd.tensor_scalar(
+                    out=minus_max[tile][:],
+                    in0=minus_max_half[tile][:, 0:1],
+                    scalar1=minus_max_half[tile][:, 1:2],
+                    scalar2=None,
+                    op0=ALU.min,
                 )
 
         def softmax_exp(tile):
@@ -449,25 +446,21 @@ def tile_rbfbias_kernel(tc, q, k, v, qs_s, ks_s, alpha, beta, out):
             for rank in range(GROUP):
                 multiply_tile(u * GROUP + rank)
 
-        def normalise(u, g_half):
+        def normalise(u, lo, hi):
             bh, first = u // GROUPS_PER_HEAD, (u % GROUPS_PER_HEAD) * GROUP
             b, h = bh // H, bh % H
-            if first == 0 and g_half == 0:
+            if first == 0 and lo == 0:
                 o_sb[bh] = work2.tile([P, NT, D], F32, name="osb", tag="osb")
-            t0 = first + g_half * 2
             nc.vector.tensor_tensor(
-                out=o_sb[bh][:, t0 : t0 + 2, :],
-                in0=o_bank[u][:, g_half * 2 : g_half * 2 + 2, :],
-                in1=inv_sums[u][:, g_half * 2 : g_half * 2 + 2].unsqueeze(2).to_broadcast([P, 2, D]),
+                out=o_sb[bh][:, first + lo : first + hi, :],
+                in0=o_bank[u][:, lo:hi, :],
+                in1=inv_sums[u][:, lo:hi].unsqueeze(2).to_broadcast([P, hi - lo, D]),
                 op=ALU.mult,
             )
-            dram = out[b, h].rearrange("(p t) d -> p t d", t=NT)
-            if u == NGROUPS - 1:
-                nc.sync.dma_start(out=dram[:, t0 : t0 + 2, :], in_=o_sb[bh][:, t0 : t0 + 2, :])
-            elif g_half == 1:
-                nc.sync.dma_start(
-                    out=dram[:, first : first + GROUP, :], in_=o_sb[bh][:, first : first + GROUP, :]
-                )
+            nc.sync.dma_start(
+                out=out[b, h].rearrange("(p t) d -> p t d", t=NT)[:, first + lo : first + hi, :],
+                in_=o_sb[bh][:, first + lo : first + hi, :],
+            )
 
         transpose_q(0)
         copy_qT(0)
@@ -492,7 +485,7 @@ def tile_rbfbias_kernel(tc, q, k, v, qs_s, ks_s, alpha, beta, out):
         )
         later_done = 0
 
-        for n in range(-4, NTILES + 1):
+        for n in range(-4, NTILES - 2):
             rank = (n - 2) % GROUP
             if is_tile(n):
                 softmax_exp(n)
@@ -502,16 +495,16 @@ def tile_rbfbias_kernel(tc, q, k, v, qs_s, ks_s, alpha, beta, out):
                 multiply_group(group_ending_at(n - 5))
             if is_tile(n + 2):
                 row_max(n + 2, 0)
+            if n + 2 == NTILES - 1:
+                row_max(n + 2, 1)
+            if rank != 0 and is_tile(n - 2) and n - 2 < NTILES - 2 and (n - 2) % NT not in SCALAR_TILES:
+                group_e(n - 2, False)
             if group_ending_at(n - 6) >= 0:
-                normalise(group_ending_at(n - 6), 0)
-            if group_ending_at(n - 7) >= 0:
-                normalise(group_ending_at(n - 7), 1)
+                normalise(group_ending_at(n - 6), 0, GROUP)
             if group_ending_at(n - 5) >= 0:
                 invert_sums(group_ending_at(n - 5))
             if head_starting_at(n + 4) >= 0:
                 copy_kT(head_starting_at(n + 4))
-            if rank != 0 and is_tile(n - 2) and n - 2 < NTILES - 2 and (n - 2) % NT not in SCALAR_TILES:
-                group_e(n - 2, False)
             if is_tile(n + 4) and n % 2 == 0:
                 bias_exp((n + 4) // 2)
             if is_tile(n - 2) and n - 2 < NTILES - 2 and (n - 2) % NT in SCALAR_TILES:
@@ -520,7 +513,7 @@ def tile_rbfbias_kernel(tc, q, k, v, qs_s, ks_s, alpha, beta, out):
                 copy_qT(head_starting_at(n + 6))
             if is_tile(n + 3):
                 scores(n + 3)
-            if is_tile(n + 2):
+            if is_tile(n + 2) and n + 2 < NTILES - 1:
                 row_max(n + 2, 1)
             if n == 2 or head_starting_at(n - 2) >= 0:
                 quantise_v((n - 2) // NT)
@@ -528,6 +521,9 @@ def tile_rbfbias_kernel(tc, q, k, v, qs_s, ks_s, alpha, beta, out):
                 quantise_group(group_ending_at(n - 3))
             if rank == 0 and is_tile(n - 2) and (n - 2) % NT not in SCALAR_TILES:
                 group_e(n - 2, False)
+            for t, f in products_to_do[0:2]:
+                product(t, f)
+            products_to_do = products_to_do[2:]
             if head_starting_at(n + 1) >= 0:
                 group_v(head_starting_at(n + 1))
             if head_starting_at(n + 7) >= 0:
@@ -551,23 +547,26 @@ def tile_rbfbias_kernel(tc, q, k, v, qs_s, ks_s, alpha, beta, out):
                 else:
                     dist_by_matmul(1, q_half, c, ps_t, "t", False)
                 if later_done == NT - FIRST_SUMMED_CHUNK:
-                    for t in range(TILES_PER_BANK, NT):
-                        product_tile(t)
-            if n == NTILES - 1:
-                quantise_tile(NTILES - 4)
-                multiply_tile(NTILES - 4)
-            if n == NTILES:
-                group_e(NTILES - 2, True)
-                quantise_tile(NTILES - 3)
-                multiply_tile(NTILES - 3)
-                invert_sums(NGROUPS - 1)
+                    products_to_do.extend([(t, f) for t in range(TILES_PER_BANK, NT) for f in range(NF)])
 
-        group_e(NTILES - 1, False)
-        quantise_tile(NTILES - 2)
-        quantise_tile(NTILES - 1)
-        multiply_tile(NTILES - 2)
-        multiply_tile(NTILES - 1)
-        normalise(NGROUPS - 2, 0)
-        normalise(NGROUPS - 2, 1)
-        normalise(NGROUPS - 1, 0)
-        normalise(NGROUPS - 1, 1)
+        before, last = NGROUPS - 2, NGROUPS - 1
+        t0 = last * GROUP
+        softmax_exp(t0 + 2)
+        transpose_e(t0 + 1)
+        group_e(t0, True)
+        softmax_exp(t0 + 3)
+        transpose_e(t0 + 2)
+        group_e(t0 + 1, True)
+        transpose_e(t0 + 3)
+        group_e(t0 + 2, True)
+        group_e(t0 + 3, True)
+        quantise_group(before)
+        multiply_group(before)
+        for rank in range(GROUP):
+            quantise_tile(t0 + rank)
+            multiply_tile(t0 + rank)
+        invert_sums(before)
+        normalise(before, 0, GROUP)
+        invert_sums(last)
+        normalise(last, 0, 2)
+        normalise(last, 2, GROUP)

@@ -45,7 +45,6 @@ def tile_rbfbias_kernel(tc, q, k, v, qs_s, ks_s, alpha, beta, out):
         small = ctx.enter_context(tc.tile_pool(name="small", bufs=3))
         raw = ctx.enter_context(tc.tile_pool(name="raw", bufs=RAWB))
         work2 = ctx.enter_context(tc.tile_pool(name="work2", bufs=2))
-        work3 = ctx.enter_context(tc.tile_pool(name="work3", bufs=3))
         upool = ctx.enter_context(tc.tile_pool(name="upool", bufs=4))
         work4 = ctx.enter_context(tc.tile_pool(name="work4", bufs=4))
         ps_w = ctx.enter_context(tc.psum_pool(name="ps_w", bufs=4))
@@ -372,7 +371,7 @@ def tile_rbfbias_kernel(tc, q, k, v, qs_s, ks_s, alpha, beta, out):
             bh, t = tile // NT, tile % NT
             if t == 0:
                 row_sums[bh] = work2.tile([P, NT], F32, name="rs", tag="rs")
-            e_sb[tile] = work3.tile([P, S], BF16, name="ee", tag="ee")
+            e_sb[tile] = work4.tile([P, S], BF16, name="ee", tag="ee")
             nc.scalar.activation(
                 out=e_sb[tile][:].rearrange("q (a p e) -> q a p e", a=WORD_BLOCKS, e=2),
                 in_=minus_z[tile][:].rearrange("q (a e p) -> q a p e", a=WORD_BLOCKS, e=2),

@@ -33,6 +33,7 @@ NHEAD = B * H
 NTILES = NHEAD * NT
 NGROUPS = NTILES // GROUP
 FIRST_SUMMED_CHUNK = 4
+CATCH_UP = 7
 RAWB = 4
 SCALAR_TILES = (0, 4)
 
@@ -45,6 +46,7 @@ def tile_rbfbias_kernel(tc, q, k, v, qs_s, ks_s, alpha, beta, out):
         small = ctx.enter_context(tc.tile_pool(name="small", bufs=3))
         raw = ctx.enter_context(tc.tile_pool(name="raw", bufs=RAWB))
         work2 = ctx.enter_context(tc.tile_pool(name="work2", bufs=2))
+        work3 = ctx.enter_context(tc.tile_pool(name="work3", bufs=3))
         upool = ctx.enter_context(tc.tile_pool(name="upool", bufs=4))
         work4 = ctx.enter_context(tc.tile_pool(name="work4", bufs=4))
         ps_w = ctx.enter_context(tc.psum_pool(name="ps_w", bufs=4))
@@ -160,21 +162,6 @@ def tile_rbfbias_kernel(tc, q, k, v, qs_s, ks_s, alpha, beta, out):
 
         dist = [const.tile([P, NT, S], F32, name="dT%d" % b) for b in range(B)]
 
-        def dist_by_matmul(b, q_half, c, pool, tag, on_scalar):
-            bank = pool.tile([P, BANK], F32, name="dps", tag=tag)
-            nc.tensor.matmul(
-                out=bank[:],
-                lhsT=featT[2 + b][:, c * P : (c + 1) * P],
-                rhs=featT[b][:, q_half * BANK : (q_half + 1) * BANK],
-                start=True,
-                stop=True,
-            )
-            dst = dist[b][:, c, q_half * BANK : (q_half + 1) * BANK]
-            if on_scalar:
-                nc.scalar.copy(out=dst, in_=bank[:])
-            else:
-                nc.vector.tensor_copy(out=dst, in_=bank[:])
-
         def dist_of_pair(pair, c_pair, pool, tag, on_scalar):
             bank = pool.tile([P, 2, 2 * P], F32, name="dps", tag=tag)
             for i in range(2):
@@ -212,8 +199,20 @@ def tile_rbfbias_kernel(tc, q, k, v, qs_s, ks_s, alpha, beta, out):
                 op1=ALU.add,
             )
 
-        def dist_by_transposes(q_half, c):
+        dist_bank = {}
+
+        def fill_dist_bank(by_transposes, q_half, c):
             bank = ps_t.tile([P, BANK], F32, name="dps", tag="t")
+            dist_bank[(q_half, c)] = bank
+            if not by_transposes:
+                nc.tensor.matmul(
+                    out=bank[:],
+                    lhsT=featT[3][:, c * P : (c + 1) * P],
+                    rhs=featT[1][:, q_half * BANK : (q_half + 1) * BANK],
+                    start=True,
+                    stop=True,
+                )
+                return
             col = c - FIRST_SUMMED_CHUNK
             for tq in range(TILES_PER_BANK):
                 for f in range(NF):
@@ -225,10 +224,12 @@ def tile_rbfbias_kernel(tc, q, k, v, qs_s, ks_s, alpha, beta, out):
                         start=(tq == 0 and f == 0),
                         stop=(tq == TILES_PER_BANK - 1 and f == NF - 1),
                     )
+
+        def empty_dist_bank(by_transposes, q_half, c):
             nc.vector.tensor_scalar(
                 out=dist[1][:, c, q_half * BANK : (q_half + 1) * BANK],
-                in0=bank[:],
-                scalar1=norm2[:, 3, c : c + 1],
+                in0=dist_bank[(q_half, c)][:],
+                scalar1=(norm2[:, 3, c : c + 1] if by_transposes else 0.0),
                 scalar2=None,
                 op0=ALU.add,
             )
@@ -307,7 +308,7 @@ def tile_rbfbias_kernel(tc, q, k, v, qs_s, ks_s, alpha, beta, out):
             tile = pair * 2
             bh, t = tile // NT, tile % NT
             b, h = bh // H, bh % H
-            bias[pair] = work2.tile([P, NT, 2 * P], F32, name="et", tag="et")
+            bias[pair] = work3.tile([P, NT, 2 * P], F32, name="et", tag="et")
             cuts = 2 if pair == 0 else 1
             width = 2 * P // cuts
             for cut in range(cuts):
@@ -332,7 +333,6 @@ def tile_rbfbias_kernel(tc, q, k, v, qs_s, ks_s, alpha, beta, out):
                     stop=False,
                 )
                 w_banks[tile].append(bank)
-            for g in range(PASSES):
                 for j in range(PACK):
                     nc.tensor.matmul(
                         out=w_banks[tile][g][:, j * P : (j + 1) * P],
@@ -484,8 +484,17 @@ def tile_rbfbias_kernel(tc, q, k, v, qs_s, ks_s, alpha, beta, out):
         )
         later_done = 0
 
+        def bias_period(pair):
+            return 2 * pair - 4 if pair < CATCH_UP else 2 * pair - 6
+
         for n in range(-4, NTILES - 2):
             rank = (n - 2) % GROUP
+            if is_tile(n + 3):
+                scores(n + 3)
+            dist_now = n >= 5 and n % NT in (2, 5, 6, 7) and later_done < len(later_dist)
+            if dist_now:
+                by_transposes, q_half, c = later_dist[later_done]
+                fill_dist_bank(by_transposes, q_half, c)
             if is_tile(n):
                 softmax_exp(n)
             if is_tile(n - 1):
@@ -504,14 +513,13 @@ def tile_rbfbias_kernel(tc, q, k, v, qs_s, ks_s, alpha, beta, out):
                 invert_sums(group_ending_at(n - 5))
             if head_starting_at(n + 4) >= 0:
                 copy_kT(head_starting_at(n + 4))
-            if is_tile(n + 4) and n % 2 == 0:
-                bias_exp((n + 4) // 2)
+            for pair in range(NTILES // 2):
+                if bias_period(pair) == n:
+                    bias_exp(pair)
             if is_tile(n - 2) and n - 2 < NTILES - 2 and (n - 2) % NT in SCALAR_TILES:
                 group_e(n - 2, True)
             if head_starting_at(n + 6) >= 0:
                 copy_qT(head_starting_at(n + 6))
-            if is_tile(n + 3):
-                scores(n + 3)
             if is_tile(n + 2) and n + 2 < NTILES - 1:
                 row_max(n + 2, 1)
             if n == 2 or head_starting_at(n - 2) >= 0:
@@ -538,13 +546,10 @@ def tile_rbfbias_kernel(tc, q, k, v, qs_s, ks_s, alpha, beta, out):
                 transpose_feat(1, 0, NT, False)
             if n == 4:
                 transpose_feat(3, 0, NT, True)
-            if n >= 5 and n % NT in (2, 5, 6, 7) and later_done < len(later_dist):
+            if dist_now:
                 by_transposes, q_half, c = later_dist[later_done]
+                empty_dist_bank(by_transposes, q_half, c)
                 later_done += 1
-                if by_transposes:
-                    dist_by_transposes(q_half, c)
-                else:
-                    dist_by_matmul(1, q_half, c, ps_t, "t", False)
                 if later_done == NT - FIRST_SUMMED_CHUNK:
                     products_to_do.extend([(t, f) for t in range(TILES_PER_BANK, NT) for f in range(NF)])
 

@@ -49,6 +49,7 @@ def tile_rbfbias_kernel(tc, q, k, v, qs_s, ks_s, alpha, beta, out):
         work3 = ctx.enter_context(tc.tile_pool(name="work3", bufs=3))
         upool = ctx.enter_context(tc.tile_pool(name="upool", bufs=4))
         work4 = ctx.enter_context(tc.tile_pool(name="work4", bufs=4))
+        work5 = ctx.enter_context(tc.tile_pool(name="work5", bufs=5))
         ps_w = ctx.enter_context(tc.psum_pool(name="ps_w", bufs=4))
         ps_t = ctx.enter_context(tc.psum_pool(name="ps_t", bufs=4))
         ctx.enter_context(tc.manual_schedule())
@@ -346,8 +347,8 @@ def tile_rbfbias_kernel(tc, q, k, v, qs_s, ks_s, alpha, beta, out):
         def row_max(tile, g):
             h = (tile // NT) % H
             if g == 0:
-                minus_z[tile] = work4.tile([P, S], F32, name="zt", tag="zt")
-                minus_max_half[tile] = work4.tile([P, PASSES], F32, name="nb0", tag="nb0")
+                minus_z[tile] = work5.tile([P, S], F32, name="zt", tag="zt")
+                minus_max_half[tile] = work5.tile([P, PASSES], F32, name="nb0", tag="nb0")
             nc.vector.tensor_scalar(
                 out=minus_z[tile][:, g * BANK : (g + 1) * BANK],
                 in0=w_banks[tile][g][:],

@@ -27,15 +27,13 @@ PACK = 4
 PASSES = 2
 WORD_BLOCKS = 4
 GROUP = 4
-GROUPS_PER_HEAD = NT // GROUP
-TILES_PER_BANK = BANK // P
-NHEAD = B * H
-NTILES = NHEAD * NT
+HALVES = NT // GROUP
+SWEEPS = B * HALVES
+NTILES = B * H * NT
 NGROUPS = NTILES // GROUP
-FIRST_SUMMED_CHUNK = 4
 CATCH_UP = 7
 RAWB = 4
-SCALAR_TILES = (0, 4)
+HEADS_KEPT = 10
 
 
 def tile_rbfbias_kernel(tc, q, k, v, qs_s, ks_s, alpha, beta, out):
@@ -43,41 +41,57 @@ def tile_rbfbias_kernel(tc, q, k, v, qs_s, ks_s, alpha, beta, out):
     scale = 1.0 / math.sqrt(D)
     with ExitStack() as ctx:
         const = ctx.enter_context(tc.tile_pool(name="const", bufs=1))
-        small = ctx.enter_context(tc.tile_pool(name="small", bufs=3))
+        small = ctx.enter_context(tc.tile_pool(name="small", bufs=4))
         raw = ctx.enter_context(tc.tile_pool(name="raw", bufs=RAWB))
+        kept = ctx.enter_context(tc.tile_pool(name="kept", bufs=HEADS_KEPT))
         work2 = ctx.enter_context(tc.tile_pool(name="work2", bufs=2))
         work3 = ctx.enter_context(tc.tile_pool(name="work3", bufs=3))
-        upool = ctx.enter_context(tc.tile_pool(name="upool", bufs=4))
         work4 = ctx.enter_context(tc.tile_pool(name="work4", bufs=4))
         work5 = ctx.enter_context(tc.tile_pool(name="work5", bufs=5))
         ps_w = ctx.enter_context(tc.psum_pool(name="ps_w", bufs=4))
         ps_t = ctx.enter_context(tc.psum_pool(name="ps_t", bufs=4))
         ctx.enter_context(tc.manual_schedule())
 
-        pos = const.tile([P, 4, 32], BF16, name="pos")
-        for b in range(B):
+        pos = const.tile([P, 2, 32], BF16, name="pos")
+        pos_k1 = const.tile([P, 32], BF16, name="pos_k1")
+
+        def load_key_positions(dst, b):
             nc.sync.dma_start(
-                out=pos[:, b, 0 : NT * NF].rearrange("p (t f) -> p t f", f=NF),
-                in_=qs_s[b].rearrange("(p t) f -> p t f", t=NT),
-            )
-            nc.sync.dma_start(
-                out=pos[:, 2 + b, 0 : NT * NF].rearrange("p (g j f) -> p g j f", g=PASSES, f=NF),
+                out=dst.rearrange("p (g j f) -> p g j f", g=PASSES, f=NF),
                 in_=ks_s[b].rearrange("(g p j) f -> p g j f", g=PASSES, j=PACK),
             )
-        key_row = const.tile([P, BANK * NF], BF16, name="yraw")
+
+        load_key_positions(pos[:, 1, 0 : NT * NF], 0)
+        nc.sync.dma_start(
+            out=pos[:, 0, 0 : NT * NF].rearrange("p (t f) -> p t f", f=NF),
+            in_=qs_s[0].rearrange("(p t) f -> p t f", t=NT),
+        )
         alpha_bf = const.tile([P, H], BF16, name="al_bf")
         beta_bf = const.tile([P, H], BF16, name="be_bf")
         nc.sync.dma_start(out=alpha_bf[:], in_=alpha.rearrange("h o -> (h o)").partition_broadcast(P))
         nc.sync.dma_start(out=beta_bf[:], in_=beta.rearrange("h o -> (h o)").partition_broadcast(P))
 
+        def place(u):
+            return u // (HALVES * H), (u // H) % HALVES, u % H
+
+        def head_of(u):
+            b, half, h = place(u)
+            return b * H + h
+
         q_raw = {}
         k_raw = {}
         v_raw = {}
 
-        def load(bh):
-            b, h = bh // H, bh % H
-            q_raw[bh] = raw.tile([P, NT, D], BF16, name="qr", tag="qr")
-            nc.sync.dma_start(out=q_raw[bh][:], in_=q[b, h].rearrange("(p t) d -> p t d", t=NT))
+        def load(u):
+            b, half, h = place(u)
+            bh = head_of(u)
+            q_raw[u] = raw.tile([P, GROUP, D], BF16, name="qr", tag="qr")
+            nc.sync.dma_start(
+                out=q_raw[u][:],
+                in_=q[b, h].rearrange("(p t) d -> p t d", t=NT)[:, half * GROUP : (half + 1) * GROUP, :],
+            )
+            if half > 0:
+                return
             k_raw[bh] = raw.tile([P, PASSES, PACK, D], BF16, name="kr", tag="kr")
             nc.sync.dma_start(
                 out=k_raw[bh][:], in_=k[b, h].rearrange("(g p j) d -> p g j d", g=PASSES, j=PACK)
@@ -88,36 +102,49 @@ def tile_rbfbias_kernel(tc, q, k, v, qs_s, ks_s, alpha, beta, out):
             )
 
         load(0)
-        nc.sync.dma_start(
-            out=key_row[:], in_=ks_s[1, BANK:S, :].rearrange("k f -> (k f)").partition_broadcast(P)
-        )
-        for bh in range(1, RAWB):
-            load(bh)
+        load(1)
+        x_row = const.tile([P, S * NF], BF16, name="xrow")
+        nc.sync.dma_start(out=x_row[:], in_=qs_s[1].rearrange("k f -> (k f)").partition_broadcast(P))
+        load_key_positions(pos_k1[:, 0 : NT * NF], 1)
+        for u in range(2, RAWB):
+            load(u)
 
         ident_bf = const.tile([P, P], BF16, name="ident_bf")
         masks.make_identity(nc, ident_bf[:])
         ident_f = const.tile([P, P], F32, name="ident_f")
         masks.make_identity(nc, ident_f[:])
 
-        feat = const.tile([P, 4, NT, P], BF16, name="feat")
-        nc.vector.memset(feat[:], 0.0)
-        nc.vector.memset(feat[:, 0:2, :, 9:15], 1.0)
-        nc.vector.memset(feat[:, 2:4, :, 3:9], 1.0)
+        feat_k = const.tile([P, NT, P], BF16, name="feat_k")
+        feat_q = [const.tile([P, GROUP, P], BF16, name="feat_q%d" % half) for half in range(HALVES)]
+        nc.vector.memset(feat_k[:], 0.0)
+        nc.vector.memset(feat_k[:, :, 3:9], 1.0)
         pos_v = pos[:, :, 0 : NT * NF].rearrange("p w (t f) -> p w t f", f=NF)
-        squares = const.tile([P, 4, NT, NF], F32, name="sq")
+        squares = const.tile([P, 2, NT, NF], F32, name="sq")
+
+        def clear_query_features(half):
+            nc.vector.memset(feat_q[half][:], 0.0)
+            nc.vector.memset(feat_q[half][:, :, 9:15], 1.0)
+
+        clear_query_features(0)
         nc.vector.tensor_tensor(out=squares[:], in0=pos_v, in1=pos_v, op=ALU.mult)
-        nc.vector.tensor_copy(out=feat[:, 0:2, :, 3:6], in_=squares[:, 0:2])
-        nc.vector.tensor_copy(out=feat[:, 2:4, :, 9:12], in_=squares[:, 2:4])
-        nc.vector.tensor_scalar(
-            out=feat[:, 0:2, :, 0:3], in0=pos_v[:, 0:2], scalar1=-2.0, scalar2=None, op0=ALU.mult
-        )
-        nc.vector.tensor_copy(out=feat[:, 2:4, :, 0:3], in_=pos_v[:, 2:4])
+
+        def query_features(half):
+            tiles = slice(half * GROUP, (half + 1) * GROUP)
+            feat = feat_q[half]
+            nc.vector.tensor_copy(out=feat[:, :, 3:6], in_=squares[:, 0, tiles])
+            nc.vector.tensor_scalar(
+                out=feat[:, :, 0:3], in0=pos_v[:, 0, tiles], scalar1=-2.0, scalar2=None, op0=ALU.mult
+            )
+            nc.vector.tensor_tensor(
+                out=feat[:, :, 6:9], in0=squares[:, 0, tiles], in1=feat[:, :, 3:6], op=ALU.subtract
+            )
+
+        nc.vector.tensor_copy(out=feat_k[:, :, 9:12], in_=squares[:, 1])
+        nc.vector.tensor_copy(out=feat_k[:, :, 0:3], in_=pos_v[:, 1])
         nc.vector.tensor_tensor(
-            out=feat[:, 0:2, :, 6:9], in0=squares[:, 0:2], in1=feat[:, 0:2, :, 3:6], op=ALU.subtract
+            out=feat_k[:, :, 12:15], in0=squares[:, 1], in1=feat_k[:, :, 9:12], op=ALU.subtract
         )
-        nc.vector.tensor_tensor(
-            out=feat[:, 2:4, :, 12:15], in0=squares[:, 2:4], in1=feat[:, 2:4, :, 9:12], op=ALU.subtract
-        )
+        query_features(0)
 
         alpha_f = const.tile([P, H], F32, name="al")
         nc.vector.tensor_copy(out=alpha_f[:], in_=alpha_bf[:])
@@ -140,28 +167,25 @@ def tile_rbfbias_kernel(tc, q, k, v, qs_s, ks_s, alpha, beta, out):
         to_minus_z = const.tile([P, H], F32, name="scneg")
         nc.vector.tensor_scalar(out=to_minus_z[:], in0=sign[:], scalar1=-scale, scalar2=None, op0=ALU.mult)
 
-        norm2 = const.tile([P, 4, NT], F32, name="s2")
-        nc.vector.tensor_reduce(out=norm2[:], in_=squares[:], axis=AX.X, op=ALU.add)
-        minus_2x = const.tile([P, NT * NF], F32, name="m2x")
-        nc.vector.tensor_scalar(
-            out=minus_2x[:], in0=pos[:, 1, 0 : NT * NF], scalar1=-2.0, scalar2=None, op0=ALU.mult
-        )
+        feat_kT = const.tile([P, NT * P], BF16, name="feat_kT")
+        feat_qT = [const.tile([P, GROUP * P], BF16, name="feat_qT%d" % half) for half in range(HALVES)]
+        k_bank = ps_t.tile([P, NT, P], BF16, name="fkb", tag="t")
+        for c in range(NT):
+            nc.tensor.transpose(out=k_bank[:, c, :], in_=feat_k[:, c, :], identity=ident_bf[:])
+        nc.vector.tensor_copy(out=feat_kT[:], in_=k_bank[:].rearrange("p t c -> p (t c)"))
 
-        featT = {}
-        for slot in range(4):
-            featT[slot] = const.tile([P, NT * P], BF16, name="featT%d" % slot)
+        def transpose_query_features(half):
+            q_bank = ps_t.tile([P, GROUP, P], BF16, name="fqb", tag="t")
+            for t in range(GROUP):
+                nc.tensor.transpose(out=q_bank[:, t, :], in_=feat_q[half][:, t, :], identity=ident_bf[:])
+            nc.vector.tensor_copy(out=feat_qT[half][:], in_=q_bank[:].rearrange("p t c -> p (t c)"))
 
-        def transpose_feat(slot, first, last, on_scalar):
-            bank = ps_t.tile([P, NT, P], BF16, name="tp", tag="t")
-            for t in range(first, last):
-                nc.tensor.transpose(out=bank[:, t, :], in_=feat[:, slot, t, :], identity=ident_bf[:])
-            src = bank[:, first:last, :].rearrange("p t c -> p (t c)")
-            if on_scalar:
-                nc.scalar.copy(out=featT[slot][:, first * P : last * P], in_=src)
-            else:
-                nc.vector.tensor_copy(out=featT[slot][:, first * P : last * P], in_=src)
+        transpose_query_features(0)
 
-        dist = [const.tile([P, NT, S], F32, name="dT%d" % b) for b in range(B)]
+        dist = {}
+
+        def new_dist(sweep):
+            dist[sweep] = work3.tile([P, NT, BANK], F32, name="dT", tag="dT")
 
         def dist_of_pair(pair, c_pair, pool, tag, on_scalar):
             bank = pool.tile([P, 2, 2 * P], F32, name="dps", tag=tag)
@@ -169,8 +193,8 @@ def tile_rbfbias_kernel(tc, q, k, v, qs_s, ks_s, alpha, beta, out):
                 c = 2 * c_pair + i
                 nc.tensor.matmul(
                     out=bank[:, i, :],
-                    lhsT=featT[2][:, c * P : (c + 1) * P],
-                    rhs=featT[0][:, pair * 2 * P : (pair + 1) * 2 * P],
+                    lhsT=feat_kT[:, c * P : (c + 1) * P],
+                    rhs=feat_qT[0][:, pair * 2 * P : (pair + 1) * 2 * P],
                     start=True,
                     stop=True,
                 )
@@ -180,62 +204,104 @@ def tile_rbfbias_kernel(tc, q, k, v, qs_s, ks_s, alpha, beta, out):
             else:
                 nc.vector.tensor_copy(out=dst, in_=bank[:])
 
-        transpose_feat(2, 0, NT, False)
-        transpose_feat(0, 0, 2, False)
+        dist_bank = {}
+
+        def fill_dist_bank(c):
+            dist_bank[c] = ps_t.tile([P, BANK], F32, name="dps", tag="t")
+            nc.tensor.matmul(
+                out=dist_bank[c][:],
+                lhsT=feat_kT[:, c * P : (c + 1) * P],
+                rhs=feat_qT[1][:],
+                start=True,
+                stop=True,
+            )
+
+        def empty_dist_bank(c):
+            nc.vector.tensor_copy(out=dist[1][:, c, :], in_=dist_bank[c][:])
+
+        new_dist(0)
         for c_pair in range(NT // 2):
             dist_of_pair(0, c_pair, ps_w, "w", c_pair % 2 == 1)
 
-        key_feature = key_row[:].rearrange("x (p j f) -> x f j p", j=PACK, f=NF)
-        products = {}
+        key_squares = const.tile([P, NT, NF], F32, name="sq_k1")
+        key_norm = const.tile([P, NT], F32, name="y2")
+        minus_2y = const.tile([P, NT * NF], F32, name="m2y")
 
-        def product(t, f):
-            if f == 0:
-                products[t] = upool.tile([P, NF, BANK], F32, name="uu", tag="uu")
-            nc.gpsimd.tensor_scalar(
-                out=products[t][:, f, :].rearrange("x (j p) -> x j p", j=PACK),
-                in0=key_feature[:, f],
-                scalar1=minus_2x[:, t * NF + f : t * NF + f + 1],
-                scalar2=(norm2[:, 1, t : t + 1] if f == 0 else 0.0),
-                op0=ALU.mult,
-                op1=ALU.add,
-            )
-
-        dist_bank = {}
-
-        def fill_dist_bank(by_transposes, q_half, c):
-            bank = ps_t.tile([P, BANK], F32, name="dps", tag="t")
-            dist_bank[(q_half, c)] = bank
-            if not by_transposes:
-                nc.tensor.matmul(
-                    out=bank[:],
-                    lhsT=featT[3][:, c * P : (c + 1) * P],
-                    rhs=featT[1][:, q_half * BANK : (q_half + 1) * BANK],
-                    start=True,
-                    stop=True,
-                )
-                return
-            col = c - FIRST_SUMMED_CHUNK
-            for tq in range(TILES_PER_BANK):
-                for f in range(NF):
-                    nc.tensor.matmul(
-                        out=bank[:, tq * P : (tq + 1) * P],
-                        lhsT=products[q_half * TILES_PER_BANK + tq][:, f, col * P : (col + 1) * P],
-                        rhs=ident_f[:],
-                        is_transpose=True,
-                        start=(tq == 0 and f == 0),
-                        stop=(tq == TILES_PER_BANK - 1 and f == NF - 1),
-                    )
-
-        def empty_dist_bank(by_transposes, q_half, c):
+        def key_scalars():
+            by_chunk = pos_k1[:, 0 : NT * NF].rearrange("p (t f) -> p t f", f=NF)
+            nc.vector.tensor_tensor(out=key_squares[:], in0=by_chunk, in1=by_chunk, op=ALU.mult)
             nc.vector.tensor_scalar(
-                out=dist[1][:, c, q_half * BANK : (q_half + 1) * BANK],
-                in0=dist_bank[(q_half, c)][:],
-                scalar1=(norm2[:, 3, c : c + 1] if by_transposes else 0.0),
-                scalar2=None,
-                op0=ALU.add,
+                out=minus_2y[:], in0=pos_k1[:, 0 : NT * NF], scalar1=-2.0, scalar2=None, op0=ALU.mult
             )
+            nc.vector.tensor_reduce(out=key_norm[:], in_=key_squares[:], axis=AX.X, op=ALU.add)
 
-        products_to_do = [(t, f) for t in range(TILES_PER_BANK) for f in range(NF)]
+        x_planes = {}
+        x_squares = {}
+        x_norm = {}
+        sums = {}
+        parts = {}
+
+        def queries_step(sweep, i):
+            half = sweep % HALVES
+            if i == 0:
+                x_planes[sweep] = work2.tile([P, NF, BANK], BF16, name="xp", tag="xp")
+                nc.gpsimd.tensor_scalar(
+                    out=x_planes[sweep][:].rearrange("x f (t p) -> x f t p", t=GROUP),
+                    in0=x_row[:].rearrange("x (p t f) -> x f t p", t=NT, f=NF)[
+                        :, :, half * GROUP : (half + 1) * GROUP, :
+                    ],
+                    scalar1=1.0,
+                    scalar2=0.0,
+                    op0=ALU.mult,
+                    op1=ALU.add,
+                )
+            elif i == 1:
+                x_squares[sweep] = const.tile([P, NF, BANK], F32, name="xs", tag="xs")
+                nc.gpsimd.tensor_tensor(
+                    out=x_squares[sweep][:], in0=x_planes[sweep][:], in1=x_planes[sweep][:], op=ALU.mult
+                )
+            elif i == 2:
+                x_norm[sweep] = work2.tile([P, BANK], F32, name="xn", tag="xn")
+                nc.gpsimd.tensor_tensor(
+                    out=x_norm[sweep][:], in0=x_squares[sweep][:, 0], in1=x_squares[sweep][:, 1], op=ALU.add
+                )
+            else:
+                nc.gpsimd.tensor_tensor(
+                    out=x_norm[sweep][:], in0=x_norm[sweep][:], in1=x_squares[sweep][:, 2], op=ALU.add
+                )
+
+        def chunk_step(sweep, c, i):
+            def product(out, f, plus):
+                nc.gpsimd.tensor_scalar(
+                    out=out,
+                    in0=x_planes[sweep][:, f],
+                    scalar1=minus_2y[:, c * NF + f : c * NF + f + 1],
+                    scalar2=plus,
+                    op0=ALU.mult,
+                    op1=ALU.add,
+                )
+
+            if i == 0:
+                if c == 0:
+                    new_dist(sweep)
+                sums[sweep, c] = work2.tile([P, BANK], F32, name="ds", tag="ds")
+                product(sums[sweep, c][:], 0, key_norm[:, c : c + 1])
+            elif i in (1, 3):
+                parts[sweep, c] = work2.tile([P, BANK], F32, name="dp", tag="dp")
+                product(parts[sweep, c][:], (i + 1) // 2, 0.0)
+            elif i in (2, 4):
+                nc.gpsimd.tensor_tensor(
+                    out=sums[sweep, c][:], in0=sums[sweep, c][:], in1=parts[sweep, c][:], op=ALU.add
+                )
+            else:
+                nc.gpsimd.tensor_tensor(
+                    out=dist[sweep][:, c, :], in0=sums[sweep, c][:], in1=x_norm[sweep][:], op=ALU.add
+                )
+
+        dist_steps = []
+        for sweep in range(HALVES, SWEEPS):
+            dist_steps.extend([(queries_step, (sweep, i)) for i in range(4)])
+            dist_steps.extend([(chunk_step, (sweep, c, i)) for c in range(NT) for i in range(6)])
 
         t_bank = {}
         qT = {}
@@ -258,32 +324,32 @@ def tile_rbfbias_kernel(tc, q, k, v, qs_s, ks_s, alpha, beta, out):
         o_bank = {}
         o_sb = {}
 
-        def transpose_q(bh):
-            t_bank[bh] = ps_t.tile([P, NT, P], BF16, name="tq", tag="t")
-            for t in range(NT):
-                nc.tensor.transpose(out=t_bank[bh][:, t, :], in_=q_raw[bh][:, t, :], identity=ident_bf[:])
+        def transpose_q(u):
+            t_bank[u] = ps_t.tile([P, GROUP, P], BF16, name="tq", tag="t")
+            for t in range(GROUP):
+                nc.tensor.transpose(out=t_bank[u][:, t, :], in_=q_raw[u][:, t, :], identity=ident_bf[:])
 
-        def copy_qT(bh):
-            h = bh % H
-            qT[bh] = work2.tile([P, NT * P], BF16, name="qT", tag="qT")
+        def copy_qT(u):
+            h = u % H
+            qT[u] = work3.tile([P, GROUP * P], BF16, name="qT", tag="qT")
             nc.vector.tensor_scalar(
-                out=qT[bh][:],
-                in0=t_bank[bh][:].rearrange("p t c -> p (t c)"),
+                out=qT[u][:],
+                in0=t_bank[u][:].rearrange("p t c -> p (t c)"),
                 scalar1=sign[:, h : h + 1],
                 scalar2=None,
                 op0=ALU.mult,
             )
 
         def transpose_k(bh):
-            t_bank[bh] = ps_t.tile([P, NT, P], BF16, name="tq", tag="t")
+            t_bank["k", bh] = ps_t.tile([P, NT, P], BF16, name="tq", tag="t")
             for c in range(NT):
                 nc.tensor.transpose(
-                    out=t_bank[bh][:, c, :], in_=k_raw[bh][:, c // PACK, c % PACK, :], identity=ident_bf[:]
+                    out=t_bank["k", bh][:, c, :], in_=k_raw[bh][:, c // PACK, c % PACK, :], identity=ident_bf[:]
                 )
 
         def copy_kT(bh):
-            kT[bh] = work2.tile([P, NT * P], BF16, name="kT", tag="kT")
-            nc.vector.tensor_copy(out=kT[bh][:], in_=t_bank[bh][:].rearrange("p t c -> p (t c)"))
+            kT[bh] = kept.tile([P, NT * P], BF16, name="kT", tag="kT")
+            nc.vector.tensor_copy(out=kT[bh][:], in_=t_bank["k", bh][:].rearrange("p t c -> p (t c)"))
 
         def group_v(bh):
             v_grouped[bh] = work2.tile([P, PASSES, D, PACK], BF16, name="vg", tag="vg", align_bytes=64)
@@ -297,8 +363,8 @@ def tile_rbfbias_kernel(tc, q, k, v, qs_s, ks_s, alpha, beta, out):
             )
 
         def quantise_v(bh):
-            v_codes[bh] = work2.tile([P, PASSES * D], U32, name="vc", tag="vc", align_bytes=64)
-            v_scales[bh] = work2.tile([P, PASSES * D], U8, name="vs", tag="vs", align_bytes=64)
+            v_codes[bh] = kept.tile([P, PASSES * D], U32, name="vc", tag="vc", align_bytes=64)
+            v_scales[bh] = kept.tile([P, PASSES * D], U8, name="vs", tag="vs", align_bytes=64)
             nc.vector.quantize_mx(
                 out=v_codes[bh][:].bitcast(FP8X4),
                 scales=v_scales[bh][:],
@@ -306,30 +372,30 @@ def tile_rbfbias_kernel(tc, q, k, v, qs_s, ks_s, alpha, beta, out):
             )
 
         def bias_exp(pair):
-            tile = pair * 2
-            bh, t = tile // NT, tile % NT
-            b, h = bh // H, bh % H
+            u = pair * 2 // GROUP
+            sweep, h = u // H, u % H
+            first = (pair * 2 % GROUP) * P
             bias[pair] = work3.tile([P, NT, 2 * P], F32, name="et", tag="et")
             cuts = 2 if pair == 0 else 1
             width = 2 * P // cuts
             for cut in range(cuts):
                 nc.scalar.activation(
                     out=bias[pair][:, :, cut * width : (cut + 1) * width],
-                    in_=dist[b][:, :, t * P + cut * width : t * P + (cut + 1) * width],
+                    in_=dist[sweep][:, :, first + cut * width : first + (cut + 1) * width],
                     func=ACTF.Exp,
                     scale=minus_beta[:, h : h + 1],
                     bias=ln_height[:, h : h + 1],
                 )
 
         def scores(tile):
-            bh, t = tile // NT, tile % NT
+            u, rank = tile // GROUP, tile % GROUP
             w_banks[tile] = []
             for g in range(PASSES):
                 bank = ps_w.tile([P, BANK], F32, name="wg", tag="w")
                 nc.tensor.matmul(
                     out=bank[:],
-                    lhsT=qT[bh][:, t * P : (t + 1) * P],
-                    rhs=kT[bh][:, g * BANK : (g + 1) * BANK],
+                    lhsT=qT[u][:, rank * P : (rank + 1) * P],
+                    rhs=kT[head_of(u)][:, g * BANK : (g + 1) * BANK],
                     start=True,
                     stop=False,
                 )
@@ -345,7 +411,7 @@ def tile_rbfbias_kernel(tc, q, k, v, qs_s, ks_s, alpha, beta, out):
                     )
 
         def row_max(tile, g):
-            h = (tile // NT) % H
+            h = (tile // GROUP) % H
             if g == 0:
                 minus_z[tile] = work5.tile([P, S], F32, name="zt", tag="zt")
                 minus_max_half[tile] = work5.tile([P, PASSES], F32, name="nb0", tag="nb0")
@@ -369,9 +435,9 @@ def tile_rbfbias_kernel(tc, q, k, v, qs_s, ks_s, alpha, beta, out):
                 )
 
         def softmax_exp(tile):
-            bh, t = tile // NT, tile % NT
-            if t == 0:
-                row_sums[bh] = work2.tile([P, NT], F32, name="rs", tag="rs")
+            u, rank = tile // GROUP, tile % GROUP
+            if rank == 0:
+                row_sums[u] = small.tile([P, GROUP], F32, name="rs", tag="rs")
             e_sb[tile] = work4.tile([P, S], BF16, name="ee", tag="ee")
             nc.scalar.activation(
                 out=e_sb[tile][:].rearrange("q (a p e) -> q a p e", a=WORD_BLOCKS, e=2),
@@ -379,7 +445,7 @@ def tile_rbfbias_kernel(tc, q, k, v, qs_s, ks_s, alpha, beta, out):
                 func=ACTF.Exp,
                 scale=-1.0,
                 bias=minus_max[tile][:],
-                accum_out=row_sums[bh][:, t : t + 1],
+                accum_out=row_sums[u][:, rank : rank + 1],
             )
 
         def transpose_e(tile):
@@ -422,13 +488,12 @@ def tile_rbfbias_kernel(tc, q, k, v, qs_s, ks_s, alpha, beta, out):
             )
 
         def invert_sums(u):
-            bh, first = u // GROUPS_PER_HEAD, (u % GROUPS_PER_HEAD) * GROUP
             inv_sums[u] = small.tile([P, GROUP], F32, name="rinv", tag="rinv")
-            nc.vector.reciprocal(out=inv_sums[u][:], in_=row_sums[bh][:, first : first + GROUP])
+            nc.vector.reciprocal(out=inv_sums[u][:], in_=row_sums[u][:])
 
         def multiply_tile(tile):
             u, rank = tile // GROUP, tile % GROUP
-            bh = u // GROUPS_PER_HEAD
+            bh = head_of(u)
             if rank == 0:
                 o_bank[u] = ps_t.tile([P, GROUP, D], F32, name="ob", tag="t")
             for g in range(PASSES):
@@ -447,26 +512,24 @@ def tile_rbfbias_kernel(tc, q, k, v, qs_s, ks_s, alpha, beta, out):
                 multiply_tile(u * GROUP + rank)
 
         def normalise(u, lo, hi):
-            bh, first = u // GROUPS_PER_HEAD, (u % GROUPS_PER_HEAD) * GROUP
-            b, h = bh // H, bh % H
-            if first == 0 and lo == 0:
-                o_sb[bh] = work2.tile([P, NT, D], F32, name="osb", tag="osb")
+            b, half, h = place(u)
+            if lo == 0:
+                o_sb[u] = work3.tile([P, GROUP, D], F32, name="osb", tag="osb")
             nc.vector.tensor_tensor(
-                out=o_sb[bh][:, first + lo : first + hi, :],
+                out=o_sb[u][:, lo:hi, :],
                 in0=o_bank[u][:, lo:hi, :],
                 in1=inv_sums[u][:, lo:hi].unsqueeze(2).to_broadcast([P, hi - lo, D]),
                 op=ALU.mult,
             )
             nc.sync.dma_start(
-                out=out[b, h].rearrange("(p t) d -> p t d", t=NT)[:, first + lo : first + hi, :],
-                in_=o_sb[bh][:, first + lo : first + hi, :],
+                out=out[b, h].rearrange("(p t) d -> p t d", t=NT)[:, half * GROUP + lo : half * GROUP + hi, :],
+                in_=o_sb[u][:, lo:hi, :],
             )
 
         transpose_q(0)
         copy_qT(0)
         transpose_k(0)
         copy_kT(0)
-        transpose_feat(0, 2, NT, False)
         group_v(0)
 
         def is_tile(x):
@@ -475,15 +538,15 @@ def tile_rbfbias_kernel(tc, q, k, v, qs_s, ks_s, alpha, beta, out):
         def group_ending_at(x):
             return x // GROUP if (x % GROUP == GROUP - 1 and is_tile(x)) else -1
 
-        def head_starting_at(x):
-            return x // NT if (x % NT == 0 and NT <= x < NTILES) else -1
+        def group_starting_at(x):
+            return x // GROUP if (x % GROUP == 0 and GROUP <= x < NTILES) else -1
 
-        later_dist = (
-            [(True, 0, c) for c in range(FIRST_SUMMED_CHUNK, NT)]
-            + [(False, q_half, c) for q_half in range(2) for c in range(FIRST_SUMMED_CHUNK)]
-            + [(c < NT - 1, 1, c) for c in range(FIRST_SUMMED_CHUNK, NT)]
-        )
-        later_done = 0
+        def head_starting_at(x):
+            u = group_starting_at(x)
+            return head_of(u) if (u >= 0 and place(u)[1] == 0) else -1
+
+        def on_scalar(tile):
+            return tile % GROUP == 0 and place(tile // GROUP)[1] == 0
 
         def bias_period(pair):
             return 2 * pair - 4 if pair < CATCH_UP else 2 * pair - 6
@@ -492,10 +555,8 @@ def tile_rbfbias_kernel(tc, q, k, v, qs_s, ks_s, alpha, beta, out):
             rank = (n - 2) % GROUP
             if is_tile(n + 3):
                 scores(n + 3)
-            dist_now = n >= 5 and n % NT in (2, 5, 6, 7) and later_done < len(later_dist)
-            if dist_now:
-                by_transposes, q_half, c = later_dist[later_done]
-                fill_dist_bank(by_transposes, q_half, c)
+            if 0 <= n < NT:
+                fill_dist_bank(n)
             if is_tile(n):
                 softmax_exp(n)
             if is_tile(n - 1):
@@ -506,7 +567,7 @@ def tile_rbfbias_kernel(tc, q, k, v, qs_s, ks_s, alpha, beta, out):
                 row_max(n + 2, 0)
             if n + 2 == NTILES - 1:
                 row_max(n + 2, 1)
-            if rank != 0 and is_tile(n - 2) and n - 2 < NTILES - 2 and (n - 2) % NT not in SCALAR_TILES:
+            if rank != 0 and is_tile(n - 2) and n - 2 < NTILES - 2 and not on_scalar(n - 2):
                 group_e(n - 2, False)
             if group_ending_at(n - 6) >= 0:
                 normalise(group_ending_at(n - 6), 0, GROUP)
@@ -517,42 +578,42 @@ def tile_rbfbias_kernel(tc, q, k, v, qs_s, ks_s, alpha, beta, out):
             for pair in range(NTILES // 2):
                 if bias_period(pair) == n:
                     bias_exp(pair)
-            if is_tile(n - 2) and n - 2 < NTILES - 2 and (n - 2) % NT in SCALAR_TILES:
+            if is_tile(n - 2) and n - 2 < NTILES - 2 and on_scalar(n - 2):
                 group_e(n - 2, True)
-            if head_starting_at(n + 6) >= 0:
-                copy_qT(head_starting_at(n + 6))
+            if group_starting_at(n + 6) >= 0:
+                copy_qT(group_starting_at(n + 6))
             if is_tile(n + 2) and n + 2 < NTILES - 1:
                 row_max(n + 2, 1)
-            if n == 2 or head_starting_at(n - 2) >= 0:
-                quantise_v((n - 2) // NT)
+            if n == 3 or head_starting_at(n - 3) >= 0:
+                quantise_v(0 if n == 3 else head_starting_at(n - 3))
             if group_ending_at(n - 3) >= 0:
                 quantise_group(group_ending_at(n - 3))
-            if rank == 0 and is_tile(n - 2) and (n - 2) % NT not in SCALAR_TILES:
+            if rank == 0 and is_tile(n - 2) and not on_scalar(n - 2):
                 group_e(n - 2, False)
-            for t, f in products_to_do[0:2]:
-                product(t, f)
-            products_to_do = products_to_do[2:]
+            steps = 0 if n < 0 else 1 + n % 2
+            for step, args in dist_steps[0:steps]:
+                step(*args)
+            dist_steps = dist_steps[steps:]
             if head_starting_at(n + 1) >= 0:
                 group_v(head_starting_at(n + 1))
-            if head_starting_at(n + 7) >= 0:
-                transpose_q(head_starting_at(n + 7))
+            if group_starting_at(n + 7) >= 0:
+                transpose_q(group_starting_at(n + 7))
             if head_starting_at(n + 5) >= 0:
                 transpose_k(head_starting_at(n + 5))
-            if n % NT == 0 and n // NT + RAWB < NHEAD:
-                load(n // NT + RAWB)
-            if n in (-4, -2, 0):
+            if n % GROUP == 0 and n >= 0 and n // GROUP + RAWB < NGROUPS:
+                load(n // GROUP + RAWB)
+            if n == -4:
                 for c_pair in range(NT // 2):
-                    dist_of_pair((n + 6) // 2, c_pair, ps_t, "t", False)
-            if n == 2:
-                transpose_feat(1, 0, NT, False)
-            if n == 4:
-                transpose_feat(3, 0, NT, True)
-            if dist_now:
-                by_transposes, q_half, c = later_dist[later_done]
-                empty_dist_bank(by_transposes, q_half, c)
-                later_done += 1
-                if later_done == NT - FIRST_SUMMED_CHUNK:
-                    products_to_do.extend([(t, f) for t in range(TILES_PER_BANK, NT) for f in range(NF)])
+                    dist_of_pair(1, c_pair, ps_t, "t", False)
+                clear_query_features(1)
+                query_features(1)
+            if n == -3:
+                new_dist(1)
+                transpose_query_features(1)
+            if 0 <= n < NT:
+                empty_dist_bank(n)
+            if n == -2:
+                key_scalars()
 
         before, last = NGROUPS - 2, NGROUPS - 1
         t0 = last * GROUP

@@ -32,8 +32,9 @@ SWEEPS = B * HALVES
 NTILES = B * H * NT
 NGROUPS = NTILES // GROUP
 CATCH_UP = 7
-RAWB = 4
-HEADS_KEPT = 10
+RAWB = 3
+HEADS_KEPT = 9
+FIRST_SUMMED_CHUNK = 1
 
 
 def tile_rbfbias_kernel(tc, q, k, v, qs_s, ks_s, alpha, beta, out):
@@ -47,25 +48,25 @@ def tile_rbfbias_kernel(tc, q, k, v, qs_s, ks_s, alpha, beta, out):
         work2 = ctx.enter_context(tc.tile_pool(name="work2", bufs=2))
         work3 = ctx.enter_context(tc.tile_pool(name="work3", bufs=3))
         work4 = ctx.enter_context(tc.tile_pool(name="work4", bufs=4))
+        dists = ctx.enter_context(tc.tile_pool(name="dists", bufs=SWEEPS))
         work5 = ctx.enter_context(tc.tile_pool(name="work5", bufs=5))
         ps_w = ctx.enter_context(tc.psum_pool(name="ps_w", bufs=4))
         ps_t = ctx.enter_context(tc.psum_pool(name="ps_t", bufs=4))
         ctx.enter_context(tc.manual_schedule())
 
-        pos = const.tile([P, 2, 32], BF16, name="pos")
-        pos_k1 = const.tile([P, 32], BF16, name="pos_k1")
+        pos = [const.tile([P, 2, 32], BF16, name="pos%d" % b) for b in range(B)]
 
-        def load_key_positions(dst, b):
+        def load_positions(b):
             nc.sync.dma_start(
-                out=dst.rearrange("p (g j f) -> p g j f", g=PASSES, f=NF),
+                out=pos[b][:, 1, 0 : NT * NF].rearrange("p (g j f) -> p g j f", g=PASSES, f=NF),
                 in_=ks_s[b].rearrange("(g p j) f -> p g j f", g=PASSES, j=PACK),
             )
+            nc.sync.dma_start(
+                out=pos[b][:, 0, 0 : NT * NF].rearrange("p (t f) -> p t f", f=NF),
+                in_=qs_s[b].rearrange("(p t) f -> p t f", t=NT),
+            )
 
-        load_key_positions(pos[:, 1, 0 : NT * NF], 0)
-        nc.sync.dma_start(
-            out=pos[:, 0, 0 : NT * NF].rearrange("p (t f) -> p t f", f=NF),
-            in_=qs_s[0].rearrange("(p t) f -> p t f", t=NT),
-        )
+        load_positions(0)
         alpha_bf = const.tile([P, H], BF16, name="al_bf")
         beta_bf = const.tile([P, H], BF16, name="be_bf")
         nc.sync.dma_start(out=alpha_bf[:], in_=alpha.rearrange("h o -> (h o)").partition_broadcast(P))
@@ -105,7 +106,7 @@ def tile_rbfbias_kernel(tc, q, k, v, qs_s, ks_s, alpha, beta, out):
         load(1)
         x_row = const.tile([P, S * NF], BF16, name="xrow")
         nc.sync.dma_start(out=x_row[:], in_=qs_s[1].rearrange("k f -> (k f)").partition_broadcast(P))
-        load_key_positions(pos_k1[:, 0 : NT * NF], 1)
+        load_positions(1)
         for u in range(2, RAWB):
             load(u)
 
@@ -118,33 +119,37 @@ def tile_rbfbias_kernel(tc, q, k, v, qs_s, ks_s, alpha, beta, out):
         feat_q = [const.tile([P, GROUP, P], BF16, name="feat_q%d" % half) for half in range(HALVES)]
         nc.vector.memset(feat_k[:], 0.0)
         nc.vector.memset(feat_k[:, :, 3:9], 1.0)
-        pos_v = pos[:, :, 0 : NT * NF].rearrange("p w (t f) -> p w t f", f=NF)
-        squares = const.tile([P, 2, NT, NF], F32, name="sq")
+        squares = [const.tile([P, 2, NT, NF], F32, name="sq%d" % b) for b in range(B)]
+
+        def by_tile(b):
+            return pos[b][:, :, 0 : NT * NF].rearrange("p w (t f) -> p w t f", f=NF)
+
+        def square_positions(b):
+            nc.vector.tensor_tensor(out=squares[b][:], in0=by_tile(b), in1=by_tile(b), op=ALU.mult)
 
         def clear_query_features(half):
             nc.vector.memset(feat_q[half][:], 0.0)
             nc.vector.memset(feat_q[half][:, :, 9:15], 1.0)
 
-        clear_query_features(0)
-        nc.vector.tensor_tensor(out=squares[:], in0=pos_v, in1=pos_v, op=ALU.mult)
+        def key_features(b):
+            sq = squares[b][:, 1]
+            nc.vector.tensor_copy(out=feat_k[:, :, 9:12], in_=sq)
+            nc.vector.tensor_copy(out=feat_k[:, :, 0:3], in_=by_tile(b)[:, 1])
+            nc.vector.tensor_tensor(out=feat_k[:, :, 12:15], in0=sq, in1=feat_k[:, :, 9:12], op=ALU.subtract)
 
-        def query_features(half):
+        def query_features(b, half):
             tiles = slice(half * GROUP, (half + 1) * GROUP)
-            feat = feat_q[half]
-            nc.vector.tensor_copy(out=feat[:, :, 3:6], in_=squares[:, 0, tiles])
+            sq, feat = squares[b][:, 0, tiles], feat_q[half]
+            nc.vector.tensor_copy(out=feat[:, :, 3:6], in_=sq)
             nc.vector.tensor_scalar(
-                out=feat[:, :, 0:3], in0=pos_v[:, 0, tiles], scalar1=-2.0, scalar2=None, op0=ALU.mult
+                out=feat[:, :, 0:3], in0=by_tile(b)[:, 0, tiles], scalar1=-2.0, scalar2=None, op0=ALU.mult
             )
-            nc.vector.tensor_tensor(
-                out=feat[:, :, 6:9], in0=squares[:, 0, tiles], in1=feat[:, :, 3:6], op=ALU.subtract
-            )
+            nc.vector.tensor_tensor(out=feat[:, :, 6:9], in0=sq, in1=feat[:, :, 3:6], op=ALU.subtract)
 
-        nc.vector.tensor_copy(out=feat_k[:, :, 9:12], in_=squares[:, 1])
-        nc.vector.tensor_copy(out=feat_k[:, :, 0:3], in_=pos_v[:, 1])
-        nc.vector.tensor_tensor(
-            out=feat_k[:, :, 12:15], in0=squares[:, 1], in1=feat_k[:, :, 9:12], op=ALU.subtract
-        )
-        query_features(0)
+        clear_query_features(0)
+        square_positions(0)
+        key_features(0)
+        query_features(0, 0)
 
         alpha_f = const.tile([P, H], F32, name="al")
         nc.vector.tensor_copy(out=alpha_f[:], in_=alpha_bf[:])
@@ -167,25 +172,30 @@ def tile_rbfbias_kernel(tc, q, k, v, qs_s, ks_s, alpha, beta, out):
         to_minus_z = const.tile([P, H], F32, name="scneg")
         nc.vector.tensor_scalar(out=to_minus_z[:], in0=sign[:], scalar1=-scale, scalar2=None, op0=ALU.mult)
 
-        feat_kT = const.tile([P, NT * P], BF16, name="feat_kT")
-        feat_qT = [const.tile([P, GROUP * P], BF16, name="feat_qT%d" % half) for half in range(HALVES)]
-        k_bank = ps_t.tile([P, NT, P], BF16, name="fkb", tag="t")
-        for c in range(NT):
-            nc.tensor.transpose(out=k_bank[:, c, :], in_=feat_k[:, c, :], identity=ident_bf[:])
-        nc.vector.tensor_copy(out=feat_kT[:], in_=k_bank[:].rearrange("p t c -> p (t c)"))
+        feat_kT = {}
+        feat_qT = {}
 
-        def transpose_query_features(half):
-            q_bank = ps_t.tile([P, GROUP, P], BF16, name="fqb", tag="t")
+        def transpose_key_features(b):
+            feat_kT[b] = const.tile([P, NT * P], BF16, name="feat_kT%d" % b)
+            bank = ps_t.tile([P, NT, P], BF16, name="fb", tag="t")
+            for c in range(NT):
+                nc.tensor.transpose(out=bank[:, c, :], in_=feat_k[:, c, :], identity=ident_bf[:])
+            nc.vector.tensor_copy(out=feat_kT[b][:], in_=bank[:].rearrange("p t c -> p (t c)"))
+
+        def transpose_query_features(b, half):
+            feat_qT[b, half] = const.tile([P, GROUP * P], BF16, name="feat_qT%d_%d" % (b, half))
+            bank = ps_t.tile([P, GROUP, P], BF16, name="fb", tag="t")
             for t in range(GROUP):
-                nc.tensor.transpose(out=q_bank[:, t, :], in_=feat_q[half][:, t, :], identity=ident_bf[:])
-            nc.vector.tensor_copy(out=feat_qT[half][:], in_=q_bank[:].rearrange("p t c -> p (t c)"))
+                nc.tensor.transpose(out=bank[:, t, :], in_=feat_q[half][:, t, :], identity=ident_bf[:])
+            nc.vector.tensor_copy(out=feat_qT[b, half][:], in_=bank[:].rearrange("p t c -> p (t c)"))
 
-        transpose_query_features(0)
+        transpose_key_features(0)
+        transpose_query_features(0, 0)
 
         dist = {}
 
         def new_dist(sweep):
-            dist[sweep] = work3.tile([P, NT, BANK], F32, name="dT", tag="dT")
+            dist[sweep] = dists.tile([P, NT, BANK], F32, name="dT", tag="dT")
 
         def dist_of_pair(pair, c_pair, pool, tag, on_scalar):
             bank = pool.tile([P, 2, 2 * P], F32, name="dps", tag=tag)
@@ -193,8 +203,8 @@ def tile_rbfbias_kernel(tc, q, k, v, qs_s, ks_s, alpha, beta, out):
                 c = 2 * c_pair + i
                 nc.tensor.matmul(
                     out=bank[:, i, :],
-                    lhsT=feat_kT[:, c * P : (c + 1) * P],
-                    rhs=feat_qT[0][:, pair * 2 * P : (pair + 1) * 2 * P],
+                    lhsT=feat_kT[0][:, c * P : (c + 1) * P],
+                    rhs=feat_qT[0, 0][:, pair * 2 * P : (pair + 1) * 2 * P],
                     start=True,
                     stop=True,
                 )
@@ -206,102 +216,84 @@ def tile_rbfbias_kernel(tc, q, k, v, qs_s, ks_s, alpha, beta, out):
 
         dist_bank = {}
 
-        def fill_dist_bank(c):
-            dist_bank[c] = ps_t.tile([P, BANK], F32, name="dps", tag="t")
+        def fill_dist_bank(sweep, c):
+            b, half = sweep // HALVES, sweep % HALVES
+            dist_bank[sweep, c] = ps_t.tile([P, BANK], F32, name="dps", tag="t")
             nc.tensor.matmul(
-                out=dist_bank[c][:],
-                lhsT=feat_kT[:, c * P : (c + 1) * P],
-                rhs=feat_qT[1][:],
+                out=dist_bank[sweep, c][:],
+                lhsT=feat_kT[b][:, c * P : (c + 1) * P],
+                rhs=feat_qT[b, half][:],
                 start=True,
                 stop=True,
             )
 
-        def empty_dist_bank(c):
-            nc.vector.tensor_copy(out=dist[1][:, c, :], in_=dist_bank[c][:])
+        def empty_dist_bank(sweep, c):
+            nc.vector.tensor_copy(out=dist[sweep][:, c, :], in_=dist_bank[sweep, c][:])
 
-        new_dist(0)
+        for sweep in range(SWEEPS):
+            new_dist(sweep)
         for c_pair in range(NT // 2):
             dist_of_pair(0, c_pair, ps_w, "w", c_pair % 2 == 1)
 
-        key_squares = const.tile([P, NT, NF], F32, name="sq_k1")
         key_norm = const.tile([P, NT], F32, name="y2")
         minus_2y = const.tile([P, NT * NF], F32, name="m2y")
 
         def key_scalars():
-            by_chunk = pos_k1[:, 0 : NT * NF].rearrange("p (t f) -> p t f", f=NF)
-            nc.vector.tensor_tensor(out=key_squares[:], in0=by_chunk, in1=by_chunk, op=ALU.mult)
+            nc.vector.tensor_reduce(out=key_norm[:], in_=squares[1][:, 1], axis=AX.X, op=ALU.add)
             nc.vector.tensor_scalar(
-                out=minus_2y[:], in0=pos_k1[:, 0 : NT * NF], scalar1=-2.0, scalar2=None, op0=ALU.mult
+                out=minus_2y[:], in0=pos[1][:, 1, 0 : NT * NF], scalar1=-2.0, scalar2=None, op0=ALU.mult
             )
-            nc.vector.tensor_reduce(out=key_norm[:], in_=key_squares[:], axis=AX.X, op=ALU.add)
 
-        x_planes = {}
-        x_squares = {}
-        x_norm = {}
-        sums = {}
+        x_planes = const.tile([P, NF, BANK], BF16, name="xp")
+        x_norm = const.tile([P, BANK], F32, name="xn")
         parts = {}
 
-        def queries_step(sweep, i):
-            half = sweep % HALVES
-            if i == 0:
-                x_planes[sweep] = work2.tile([P, NF, BANK], BF16, name="xp", tag="xp")
-                nc.gpsimd.tensor_scalar(
-                    out=x_planes[sweep][:].rearrange("x f (t p) -> x f t p", t=GROUP),
-                    in0=x_row[:].rearrange("x (p t f) -> x f t p", t=NT, f=NF)[
-                        :, :, half * GROUP : (half + 1) * GROUP, :
-                    ],
-                    scalar1=1.0,
-                    scalar2=0.0,
-                    op0=ALU.mult,
-                    op1=ALU.add,
-                )
-            elif i == 1:
-                x_squares[sweep] = const.tile([P, NF, BANK], F32, name="xs", tag="xs")
-                nc.gpsimd.tensor_tensor(
-                    out=x_squares[sweep][:], in0=x_planes[sweep][:], in1=x_planes[sweep][:], op=ALU.mult
-                )
-            elif i == 2:
-                x_norm[sweep] = work2.tile([P, BANK], F32, name="xn", tag="xn")
-                nc.gpsimd.tensor_tensor(
-                    out=x_norm[sweep][:], in0=x_squares[sweep][:, 0], in1=x_squares[sweep][:, 1], op=ALU.add
-                )
+        def split_features():
+            nc.gpsimd.tensor_scalar(
+                out=x_planes[:].rearrange("x f (t p) -> x f t p", t=GROUP),
+                in0=x_row[:].rearrange("x (p t f) -> x f t p", t=NT, f=NF)[:, :, NT - GROUP : NT, :],
+                scalar1=1.0,
+                scalar2=0.0,
+                op0=ALU.mult,
+                op1=ALU.add,
+            )
+
+        def square_feature(f):
+            if f == 0:
+                out = x_norm
             else:
-                nc.gpsimd.tensor_tensor(
-                    out=x_norm[sweep][:], in0=x_norm[sweep][:], in1=x_squares[sweep][:, 2], op=ALU.add
-                )
+                parts["x", f] = out = work2.tile([P, BANK], F32, name="dp", tag="dp")
+            nc.gpsimd.tensor_tensor(out=out[:], in0=x_planes[:, f], in1=x_planes[:, f], op=ALU.mult)
 
-        def chunk_step(sweep, c, i):
-            def product(out, f, plus):
-                nc.gpsimd.tensor_scalar(
-                    out=out,
-                    in0=x_planes[sweep][:, f],
-                    scalar1=minus_2y[:, c * NF + f : c * NF + f + 1],
-                    scalar2=plus,
-                    op0=ALU.mult,
-                    op1=ALU.add,
-                )
+        def add_square(f):
+            nc.gpsimd.tensor_tensor(out=x_norm[:], in0=x_norm[:], in1=parts["x", f][:], op=ALU.add)
 
-            if i == 0:
-                if c == 0:
-                    new_dist(sweep)
-                sums[sweep, c] = work2.tile([P, BANK], F32, name="ds", tag="ds")
-                product(sums[sweep, c][:], 0, key_norm[:, c : c + 1])
-            elif i in (1, 3):
-                parts[sweep, c] = work2.tile([P, BANK], F32, name="dp", tag="dp")
-                product(parts[sweep, c][:], (i + 1) // 2, 0.0)
-            elif i in (2, 4):
-                nc.gpsimd.tensor_tensor(
-                    out=sums[sweep, c][:], in0=sums[sweep, c][:], in1=parts[sweep, c][:], op=ALU.add
-                )
-            else:
-                nc.gpsimd.tensor_tensor(
-                    out=dist[sweep][:, c, :], in0=sums[sweep, c][:], in1=x_norm[sweep][:], op=ALU.add
-                )
+        def product(c, f):
+            parts[c, f] = work3.tile([P, BANK], F32, name="ds", tag="ds")
+            nc.gpsimd.tensor_scalar(
+                out=parts[c, f][:],
+                in0=x_planes[:, f],
+                scalar1=minus_2y[:, c * NF + f : c * NF + f + 1],
+                scalar2=(key_norm[:, c : c + 1] if f == 0 else 0.0),
+                op0=ALU.mult,
+                op1=ALU.add,
+            )
 
-        dist_steps = []
-        for sweep in range(HALVES, SWEEPS):
-            dist_steps.extend([(queries_step, (sweep, i)) for i in range(4)])
-            dist_steps.extend([(chunk_step, (sweep, c, i)) for c in range(NT) for i in range(6)])
+        def add_product(c, f):
+            nc.gpsimd.tensor_tensor(out=parts[c, 0][:], in0=parts[c, 0][:], in1=parts[c, f][:], op=ALU.add)
+
+        def add_norm(c):
+            nc.gpsimd.tensor_tensor(
+                out=dist[SWEEPS - 1][:, c, :], in0=parts[c, 0][:], in1=x_norm[:], op=ALU.add
+            )
+
+        dist_steps = [(split_features, ())]
+        dist_steps.extend([(square_feature, (f,)) for f in range(NF)])
+        dist_steps.extend([(add_square, (f,)) for f in range(1, NF)])
+        for c in range(FIRST_SUMMED_CHUNK, NT):
+            dist_steps.extend([(product, (c, f)) for f in range(NF)])
+            dist_steps.extend([(add_product, (c, f)) for f in range(1, NF)])
+            dist_steps.append((add_norm, (c,)))
 
         t_bank = {}
         qT = {}
@@ -514,7 +506,7 @@ def tile_rbfbias_kernel(tc, q, k, v, qs_s, ks_s, alpha, beta, out):
         def normalise(u, lo, hi):
             b, half, h = place(u)
             if lo == 0:
-                o_sb[u] = work3.tile([P, GROUP, D], F32, name="osb", tag="osb")
+                o_sb[u] = work2.tile([P, GROUP, D], F32, name="osb", tag="osb")
             nc.vector.tensor_tensor(
                 out=o_sb[u][:, lo:hi, :],
                 in0=o_bank[u][:, lo:hi, :],
@@ -546,17 +538,22 @@ def tile_rbfbias_kernel(tc, q, k, v, qs_s, ks_s, alpha, beta, out):
             return head_of(u) if (u >= 0 and place(u)[1] == 0) else -1
 
         def on_scalar(tile):
-            return tile % GROUP == 0 and place(tile // GROUP)[1] == 0
+            return tile % GROUP == 0
 
         def bias_period(pair):
             return 2 * pair - 4 if pair < CATCH_UP else 2 * pair - 6
+
+        bank_periods = list(range(NT)) + [n for n in range(H * GROUP, NTILES) if n % GROUP in (0, 3)]
+        banks = [(1, c) for c in range(NT)] + [(2, c) for c in range(NT)]
+        banks += [(SWEEPS - 1, c) for c in range(FIRST_SUMMED_CHUNK)]
+        bank_of_period = dict(zip(bank_periods, banks))
 
         for n in range(-4, NTILES - 2):
             rank = (n - 2) % GROUP
             if is_tile(n + 3):
                 scores(n + 3)
-            if 0 <= n < NT:
-                fill_dist_bank(n)
+            if n in bank_of_period:
+                fill_dist_bank(*bank_of_period[n])
             if is_tile(n):
                 softmax_exp(n)
             if is_tile(n - 1):
@@ -590,7 +587,7 @@ def tile_rbfbias_kernel(tc, q, k, v, qs_s, ks_s, alpha, beta, out):
                 quantise_group(group_ending_at(n - 3))
             if rank == 0 and is_tile(n - 2) and not on_scalar(n - 2):
                 group_e(n - 2, False)
-            steps = 0 if n < 0 else 1 + n % 2
+            steps = 0 if n < 0 else 2 if n < 4 else 1 if n % GROUP in (0, 1) else 0
             for step, args in dist_steps[0:steps]:
                 step(*args)
             dist_steps = dist_steps[steps:]
@@ -606,14 +603,26 @@ def tile_rbfbias_kernel(tc, q, k, v, qs_s, ks_s, alpha, beta, out):
                 for c_pair in range(NT // 2):
                     dist_of_pair(1, c_pair, ps_t, "t", False)
                 clear_query_features(1)
-                query_features(1)
+                query_features(0, 1)
             if n == -3:
-                new_dist(1)
-                transpose_query_features(1)
-            if 0 <= n < NT:
-                empty_dist_bank(n)
+                transpose_query_features(0, 1)
+            if n in bank_of_period:
+                empty_dist_bank(*bank_of_period[n])
             if n == -2:
+                square_positions(1)
                 key_scalars()
+            if n == 11:
+                key_features(1)
+            if n == 15:
+                transpose_key_features(1)
+            if n == 19:
+                query_features(1, 0)
+            if n == 20:
+                query_features(1, 1)
+            if n == 23:
+                transpose_query_features(1, 0)
+            if n == 24:
+                transpose_query_features(1, 1)
 
         before, last = NGROUPS - 2, NGROUPS - 1
         t0 = last * GROUP

@@ -34,6 +34,7 @@ NGROUPS = NTILES // GROUP
 CATCH_UP = 7
 RAWB = 3
 HEADS_KEPT = 9
+FIRST_STEP = 24
 FIRST_SUMMED_CHUNK = 1
 
 
@@ -48,8 +49,8 @@ def tile_rbfbias_kernel(tc, q, k, v, qs_s, ks_s, alpha, beta, out):
         work2 = ctx.enter_context(tc.tile_pool(name="work2", bufs=2))
         work3 = ctx.enter_context(tc.tile_pool(name="work3", bufs=3))
         work4 = ctx.enter_context(tc.tile_pool(name="work4", bufs=4))
-        dists = ctx.enter_context(tc.tile_pool(name="dists", bufs=SWEEPS))
-        work5 = ctx.enter_context(tc.tile_pool(name="work5", bufs=5))
+        dists = ctx.enter_context(tc.tile_pool(name="dists", bufs=SWEEPS - 1))
+        work6 = ctx.enter_context(tc.tile_pool(name="work6", bufs=6))
         ps_w = ctx.enter_context(tc.psum_pool(name="ps_w", bufs=4))
         ps_t = ctx.enter_context(tc.psum_pool(name="ps_t", bufs=4))
         ctx.enter_context(tc.manual_schedule())
@@ -230,7 +231,7 @@ def tile_rbfbias_kernel(tc, q, k, v, qs_s, ks_s, alpha, beta, out):
         def empty_dist_bank(sweep, c):
             nc.vector.tensor_copy(out=dist[sweep][:, c, :], in_=dist_bank[sweep, c][:])
 
-        for sweep in range(SWEEPS):
+        for sweep in range(SWEEPS - 1):
             new_dist(sweep)
         for c_pair in range(NT // 2):
             dist_of_pair(0, c_pair, ps_w, "w", c_pair % 2 == 1)
@@ -405,8 +406,8 @@ def tile_rbfbias_kernel(tc, q, k, v, qs_s, ks_s, alpha, beta, out):
         def row_max(tile, g):
             h = (tile // GROUP) % H
             if g == 0:
-                minus_z[tile] = work5.tile([P, S], F32, name="zt", tag="zt")
-                minus_max_half[tile] = work5.tile([P, PASSES], F32, name="nb0", tag="nb0")
+                minus_z[tile] = work6.tile([P, S], F32, name="zt", tag="zt")
+                minus_max_half[tile] = work6.tile([P, PASSES], F32, name="nb0", tag="nb0")
             nc.vector.tensor_scalar(
                 out=minus_z[tile][:, g * BANK : (g + 1) * BANK],
                 in0=w_banks[tile][g][:],
@@ -417,7 +418,7 @@ def tile_rbfbias_kernel(tc, q, k, v, qs_s, ks_s, alpha, beta, out):
                 accum_out=minus_max_half[tile][:, g : g + 1],
             )
             if g == PASSES - 1:
-                minus_max[tile] = work4.tile([P, 1], F32, name="nb", tag="nb")
+                minus_max[tile] = work6.tile([P, 1], F32, name="nb", tag="nb")
                 nc.gpsimd.tensor_scalar(
                     out=minus_max[tile][:],
                     in0=minus_max_half[tile][:, 0:1],
@@ -541,17 +542,17 @@ def tile_rbfbias_kernel(tc, q, k, v, qs_s, ks_s, alpha, beta, out):
             return tile % GROUP == 0
 
         def bias_period(pair):
-            return 2 * pair - 4 if pair < CATCH_UP else 2 * pair - 6
+            return 2 * pair - 5 if pair < CATCH_UP else 2 * pair - 7
 
         bank_periods = list(range(NT)) + [n for n in range(H * GROUP, NTILES) if n % GROUP in (0, 3)]
         banks = [(1, c) for c in range(NT)] + [(2, c) for c in range(NT)]
         banks += [(SWEEPS - 1, c) for c in range(FIRST_SUMMED_CHUNK)]
         bank_of_period = dict(zip(bank_periods, banks))
 
-        for n in range(-4, NTILES - 2):
+        for n in range(-5, NTILES - 2):
             rank = (n - 2) % GROUP
-            if is_tile(n + 3):
-                scores(n + 3)
+            if is_tile(n + 4):
+                scores(n + 4)
             if n in bank_of_period:
                 fill_dist_bank(*bank_of_period[n])
             if is_tile(n):
@@ -560,18 +561,18 @@ def tile_rbfbias_kernel(tc, q, k, v, qs_s, ks_s, alpha, beta, out):
                 transpose_e(n - 1)
             if group_ending_at(n - 5) >= 0:
                 multiply_group(group_ending_at(n - 5))
-            if is_tile(n + 2):
-                row_max(n + 2, 0)
-            if n + 2 == NTILES - 1:
-                row_max(n + 2, 1)
+            if is_tile(n + 3):
+                row_max(n + 3, 0)
+            if n + 3 == NTILES - 1:
+                row_max(n + 3, 1)
             if rank != 0 and is_tile(n - 2) and n - 2 < NTILES - 2 and not on_scalar(n - 2):
                 group_e(n - 2, False)
             if group_ending_at(n - 6) >= 0:
                 normalise(group_ending_at(n - 6), 0, GROUP)
             if group_ending_at(n - 5) >= 0:
                 invert_sums(group_ending_at(n - 5))
-            if head_starting_at(n + 4) >= 0:
-                copy_kT(head_starting_at(n + 4))
+            if head_starting_at(n + 8) >= 0:
+                copy_kT(head_starting_at(n + 8))
             for pair in range(NTILES // 2):
                 if bias_period(pair) == n:
                     bias_exp(pair)
@@ -579,15 +580,17 @@ def tile_rbfbias_kernel(tc, q, k, v, qs_s, ks_s, alpha, beta, out):
                 group_e(n - 2, True)
             if group_starting_at(n + 6) >= 0:
                 copy_qT(group_starting_at(n + 6))
-            if is_tile(n + 2) and n + 2 < NTILES - 1:
-                row_max(n + 2, 1)
+            if is_tile(n + 3) and n + 3 < NTILES - 1:
+                row_max(n + 3, 1)
             if n == 3 or head_starting_at(n - 3) >= 0:
                 quantise_v(0 if n == 3 else head_starting_at(n - 3))
             if group_ending_at(n - 3) >= 0:
                 quantise_group(group_ending_at(n - 3))
             if rank == 0 and is_tile(n - 2) and not on_scalar(n - 2):
                 group_e(n - 2, False)
-            steps = 0 if n < 0 else 2 if n < 4 else 1 if n % GROUP in (0, 1) else 0
+            if n == FIRST_STEP:
+                new_dist(SWEEPS - 1)
+            steps = 0 if n % GROUP == 2 or n < FIRST_STEP else 1
             for step, args in dist_steps[0:steps]:
                 step(*args)
             dist_steps = dist_steps[steps:]
@@ -595,16 +598,16 @@ def tile_rbfbias_kernel(tc, q, k, v, qs_s, ks_s, alpha, beta, out):
                 group_v(head_starting_at(n + 1))
             if group_starting_at(n + 7) >= 0:
                 transpose_q(group_starting_at(n + 7))
-            if head_starting_at(n + 5) >= 0:
-                transpose_k(head_starting_at(n + 5))
+            if head_starting_at(n + 9) >= 0:
+                transpose_k(head_starting_at(n + 9))
             if n % GROUP == 0 and n >= 0 and n // GROUP + RAWB < NGROUPS:
                 load(n // GROUP + RAWB)
-            if n == -4:
+            if n == -5:
                 for c_pair in range(NT // 2):
                     dist_of_pair(1, c_pair, ps_t, "t", False)
                 clear_query_features(1)
                 query_features(0, 1)
-            if n == -3:
+            if n == -4:
                 transpose_query_features(0, 1)
             if n in bank_of_period:
                 empty_dist_bank(*bank_of_period[n])

@@ -116,6 +116,8 @@ def tile_rbfbias_kernel(tc, q, k, v, qs_s, ks_s, alpha, beta, out):
         ident_f = const.tile([P, P], F32, name="ident_f")
         masks.make_identity(nc, ident_f[:])
 
+        tiny = const.tile([P, 1], F32, name="tiny")
+        nc.vector.memset(tiny[:], 2.0 ** -60)
         feat_k = const.tile([P, NT, P], BF16, name="feat_k")
         feat_q = [const.tile([P, GROUP, P], BF16, name="feat_q%d" % half) for half in range(HALVES)]
         nc.vector.memset(feat_k[:], 0.0)
@@ -149,39 +151,40 @@ def tile_rbfbias_kernel(tc, q, k, v, qs_s, ks_s, alpha, beta, out):
 
         clear_query_features(0)
         square_positions(0)
-        key_features(0)
         query_features(0, 0)
+        key_features(0)
+        clear_query_features(1)
 
-        alpha_f = const.tile([P, H], F32, name="al")
-        nc.vector.tensor_copy(out=alpha_f[:], in_=alpha_bf[:])
-        sign = const.tile([P, H], F32, name="sgn")
-        nc.vector.tensor_scalar(
-            out=sign[:], in0=alpha_f[:], scalar1=0.0, scalar2=2.0, op0=ALU.is_ge, op1=ALU.mult
-        )
-        nc.vector.tensor_scalar(out=sign[:], in0=sign[:], scalar1=-1.0, scalar2=None, op0=ALU.add)
-        height = const.tile([P, H], F32, name="absa")
-        nc.vector.tensor_tensor(out=height[:], in0=alpha_f[:], in1=sign[:], op=ALU.mult)
-        nc.vector.tensor_scalar(
-            out=height[:], in0=height[:], scalar1=math.sqrt(D), scalar2=2.0 ** -60, op0=ALU.mult, op1=ALU.max
-        )
         ln_height = const.tile([P, H], F32, name="lna")
-        nc.scalar.activation(out=ln_height[:], in_=height[:], func=ACTF.Ln)
+        height = const.tile([P, H], F32, name="absa")
+        nc.scalar.activation(out=height[:], in_=alpha_bf[:], func=ACTF.Abs, scale=math.sqrt(D))
+        nc.scalar.activation(out=ln_height[:], in_=height[:], func=ACTF.Ln, bias=tiny[:])
         table_change = const.tile([P, 1], F32, name="warm")
         nc.scalar.activation(out=table_change[:], in_=ln_height[:, 0:1], func=ACTF.Exp)
         minus_beta = const.tile([P, H], F32, name="nbeta")
         nc.vector.tensor_scalar(out=minus_beta[:], in0=beta_bf[:], scalar1=-1.0, scalar2=None, op0=ALU.mult)
+        sign = const.tile([P, H], F32, name="sgn")
         to_minus_z = const.tile([P, H], F32, name="scneg")
-        nc.vector.tensor_scalar(out=to_minus_z[:], in0=sign[:], scalar1=-scale, scalar2=None, op0=ALU.mult)
+
+        def signs():
+            nc.vector.tensor_scalar(
+                out=sign[:], in0=alpha_bf[:], scalar1=0.0, scalar2=2.0, op0=ALU.is_ge, op1=ALU.mult
+            )
+            nc.vector.tensor_scalar(out=sign[:], in0=sign[:], scalar1=-1.0, scalar2=None, op0=ALU.add)
+            nc.vector.tensor_scalar(out=to_minus_z[:], in0=sign[:], scalar1=-scale, scalar2=None, op0=ALU.mult)
 
         feat_kT = {}
         feat_qT = {}
 
-        def transpose_key_features(b):
-            feat_kT[b] = const.tile([P, NT * P], BF16, name="feat_kT%d" % b)
-            bank = ps_t.tile([P, NT, P], BF16, name="fb", tag="t")
-            for c in range(NT):
-                nc.tensor.transpose(out=bank[:, c, :], in_=feat_k[:, c, :], identity=ident_bf[:])
-            nc.vector.tensor_copy(out=feat_kT[b][:], in_=bank[:].rearrange("p t c -> p (t c)"))
+        def transpose_key_features(b, g):
+            if g == 0:
+                feat_kT[b] = const.tile([P, NT * P], BF16, name="feat_kT%d" % b)
+            bank = ps_t.tile([P, PACK, P], BF16, name="fb", tag="t")
+            for j in range(PACK):
+                nc.tensor.transpose(out=bank[:, j, :], in_=feat_k[:, g * PACK + j, :], identity=ident_bf[:])
+            nc.vector.tensor_copy(
+                out=feat_kT[b][:, g * BANK : (g + 1) * BANK], in_=bank[:].rearrange("p t c -> p (t c)")
+            )
 
         def transpose_query_features(b, half):
             feat_qT[b, half] = const.tile([P, GROUP * P], BF16, name="feat_qT%d_%d" % (b, half))
@@ -190,30 +193,29 @@ def tile_rbfbias_kernel(tc, q, k, v, qs_s, ks_s, alpha, beta, out):
                 nc.tensor.transpose(out=bank[:, t, :], in_=feat_q[half][:, t, :], identity=ident_bf[:])
             nc.vector.tensor_copy(out=feat_qT[b, half][:], in_=bank[:].rearrange("p t c -> p (t c)"))
 
-        transpose_key_features(0)
         transpose_query_features(0, 0)
+        for g in range(PASSES):
+            transpose_key_features(0, g)
 
         dist = {}
 
         def new_dist(sweep):
             dist[sweep] = dists.tile([P, NT, BANK], F32, name="dT", tag="dT")
 
-        def dist_of_pair(pair, c_pair, pool, tag, on_scalar):
-            bank = pool.tile([P, 2, 2 * P], F32, name="dps", tag=tag)
-            for i in range(2):
-                c = 2 * c_pair + i
+        def dist_of_tile(t, g, pool, tag):
+            bank = pool.tile([P, PACK, P], F32, name="dps", tag=tag)
+            for j in range(PACK):
+                c = g * PACK + j
                 nc.tensor.matmul(
-                    out=bank[:, i, :],
+                    out=bank[:, j, :],
                     lhsT=feat_kT[0][:, c * P : (c + 1) * P],
-                    rhs=feat_qT[0, 0][:, pair * 2 * P : (pair + 1) * 2 * P],
+                    rhs=feat_qT[0, 0][:, t * P : (t + 1) * P],
                     start=True,
                     stop=True,
                 )
-            dst = dist[0][:, 2 * c_pair : 2 * c_pair + 2, pair * 2 * P : (pair + 1) * 2 * P]
-            if on_scalar:
-                nc.scalar.copy(out=dst, in_=bank[:])
-            else:
-                nc.vector.tensor_copy(out=dst, in_=bank[:])
+            nc.vector.tensor_copy(
+                out=dist[0][:, g * PACK : (g + 1) * PACK, t * P : (t + 1) * P], in_=bank[:]
+            )
 
         dist_bank = {}
 
@@ -233,8 +235,6 @@ def tile_rbfbias_kernel(tc, q, k, v, qs_s, ks_s, alpha, beta, out):
 
         for sweep in range(SWEEPS - 1):
             new_dist(sweep)
-        for c_pair in range(NT // 2):
-            dist_of_pair(0, c_pair, ps_w, "w", c_pair % 2 == 1)
 
         key_norm = const.tile([P, NT], F32, name="y2")
         minus_2y = const.tile([P, NT * NF], F32, name="m2y")
@@ -369,7 +369,7 @@ def tile_rbfbias_kernel(tc, q, k, v, qs_s, ks_s, alpha, beta, out):
             sweep, h = u // H, u % H
             first = (pair * 2 % GROUP) * P
             bias[pair] = work3.tile([P, NT, 2 * P], F32, name="et", tag="et")
-            cuts = 2 if pair == 0 else 1
+            cuts = 2 if pair * 2 < GROUP else 1
             width = 2 * P // cuts
             for cut in range(cuts):
                 nc.scalar.activation(
@@ -519,11 +519,17 @@ def tile_rbfbias_kernel(tc, q, k, v, qs_s, ks_s, alpha, beta, out):
                 in_=o_sb[u][:, lo:hi, :],
             )
 
-        transpose_q(0)
-        copy_qT(0)
+        for t in range(2):
+            for g in range(PASSES):
+                dist_of_tile(t, g, ps_w, "w")
+        signs()
         transpose_k(0)
         copy_kT(0)
-        group_v(0)
+        transpose_q(0)
+        copy_qT(0)
+        for t in range(2, GROUP):
+            for g in range(PASSES):
+                dist_of_tile(t, g, ps_t, "t")
 
         def is_tile(x):
             return 0 <= x < NTILES
@@ -539,7 +545,8 @@ def tile_rbfbias_kernel(tc, q, k, v, qs_s, ks_s, alpha, beta, out):
             return head_of(u) if (u >= 0 and place(u)[1] == 0) else -1
 
         def on_scalar(tile):
-            return tile % GROUP == 0
+            u, rank = tile // GROUP, tile % GROUP
+            return rank == 0 and (u < NGROUPS - H or u % 2 == 0)
 
         def bias_period(pair):
             return 2 * pair - 5 if pair < CATCH_UP else 2 * pair - 7
@@ -594,8 +601,8 @@ def tile_rbfbias_kernel(tc, q, k, v, qs_s, ks_s, alpha, beta, out):
             for step, args in dist_steps[0:steps]:
                 step(*args)
             dist_steps = dist_steps[steps:]
-            if head_starting_at(n + 1) >= 0:
-                group_v(head_starting_at(n + 1))
+            if n == 0 or head_starting_at(n + 1) >= 0:
+                group_v(0 if n == 0 else head_starting_at(n + 1))
             if group_starting_at(n + 7) >= 0:
                 transpose_q(group_starting_at(n + 7))
             if head_starting_at(n + 9) >= 0:
@@ -603,9 +610,6 @@ def tile_rbfbias_kernel(tc, q, k, v, qs_s, ks_s, alpha, beta, out):
             if n % GROUP == 0 and n >= 0 and n // GROUP + RAWB < NGROUPS:
                 load(n // GROUP + RAWB)
             if n == -5:
-                for c_pair in range(NT // 2):
-                    dist_of_pair(1, c_pair, ps_t, "t", False)
-                clear_query_features(1)
                 query_features(0, 1)
             if n == -4:
                 transpose_query_features(0, 1)
@@ -617,7 +621,8 @@ def tile_rbfbias_kernel(tc, q, k, v, qs_s, ks_s, alpha, beta, out):
             if n == 11:
                 key_features(1)
             if n == 15:
-                transpose_key_features(1)
+                for g in range(PASSES):
+                    transpose_key_features(1, g)
             if n == 19:
                 query_features(1, 0)
             if n == 20:
@@ -631,20 +636,25 @@ def tile_rbfbias_kernel(tc, q, k, v, qs_s, ks_s, alpha, beta, out):
         t0 = last * GROUP
         softmax_exp(t0 + 2)
         transpose_e(t0 + 1)
-        group_e(t0, True)
+        group_e(t0, False)
         softmax_exp(t0 + 3)
         transpose_e(t0 + 2)
-        group_e(t0 + 1, True)
-        transpose_e(t0 + 3)
-        group_e(t0 + 2, True)
-        group_e(t0 + 3, True)
         quantise_group(before)
         multiply_group(before)
-        for rank in range(GROUP):
-            quantise_tile(t0 + rank)
-            multiply_tile(t0 + rank)
+        group_e(t0 + 1, False)
+        quantise_tile(t0)
+        quantise_tile(t0 + 1)
+        group_e(t0 + 2, True)
+        transpose_e(t0 + 3)
+        group_e(t0 + 3, True)
+        multiply_tile(t0)
+        multiply_tile(t0 + 1)
         invert_sums(before)
         normalise(before, 0, GROUP)
         invert_sums(last)
+        quantise_tile(t0 + 2)
+        multiply_tile(t0 + 2)
         normalise(last, 0, 2)
+        quantise_tile(t0 + 3)
+        multiply_tile(t0 + 3)
         normalise(last, 2, GROUP)

@@ -116,6 +116,8 @@ def tile_rbfbias_kernel(tc, q, k, v, qs_s, ks_s, alpha, beta, out):
         ident_f = const.tile([P, P], F32, name="ident_f")
         masks.make_identity(nc, ident_f[:])
 
+        minus_one = const.tile([P, GROUP], F32, name="m1")
+        nc.vector.memset(minus_one[:], -1.0)
         tiny = const.tile([P, 1], F32, name="tiny")
         nc.vector.memset(tiny[:], 2.0 ** -60)
         feat_k = const.tile([P, NT, P], BF16, name="feat_k")
@@ -213,9 +215,11 @@ def tile_rbfbias_kernel(tc, q, k, v, qs_s, ks_s, alpha, beta, out):
                     start=True,
                     stop=True,
                 )
-            nc.vector.tensor_copy(
-                out=dist[0][:, g * PACK : (g + 1) * PACK, t * P : (t + 1) * P], in_=bank[:]
-            )
+            dst = dist[0][:, g * PACK : (g + 1) * PACK, t * P : (t + 1) * P]
+            if t > 0 and g > 0:
+                nc.scalar.copy(out=dst, in_=bank[:])
+            else:
+                nc.vector.tensor_copy(out=dst, in_=bank[:])
 
         dist_bank = {}
 
@@ -482,7 +486,10 @@ def tile_rbfbias_kernel(tc, q, k, v, qs_s, ks_s, alpha, beta, out):
 
         def invert_sums(u):
             inv_sums[u] = small.tile([P, GROUP], F32, name="rinv", tag="rinv")
-            nc.vector.reciprocal(out=inv_sums[u][:], in_=row_sums[u][:])
+            if u == NGROUPS - 1:
+                nc.vector.reciprocal(out=inv_sums[u][:], in_=row_sums[u][:])
+                return
+            nc.gpsimd.tensor_tensor(out=inv_sums[u][:], in0=row_sums[u][:], in1=minus_one[:], op=ALU.pow)
 
         def multiply_tile(tile):
             u, rank = tile // GROUP, tile % GROUP
@@ -546,7 +553,7 @@ def tile_rbfbias_kernel(tc, q, k, v, qs_s, ks_s, alpha, beta, out):
 
         def on_scalar(tile):
             u, rank = tile // GROUP, tile % GROUP
-            return rank == 0 and (u < NGROUPS - H or u % 2 == 0)
+            return rank == 0 or (rank == 2 and place(u)[1] == 0 and u % 2 == 0)
 
         def bias_period(pair):
             return 2 * pair - 5 if pair < CATCH_UP else 2 * pair - 7
@@ -576,8 +583,8 @@ def tile_rbfbias_kernel(tc, q, k, v, qs_s, ks_s, alpha, beta, out):
                 group_e(n - 2, False)
             if group_ending_at(n - 6) >= 0:
                 normalise(group_ending_at(n - 6), 0, GROUP)
-            if group_ending_at(n - 5) >= 0:
-                invert_sums(group_ending_at(n - 5))
+            if group_ending_at(n - 4) >= 0:
+                invert_sums(group_ending_at(n - 4))
             if head_starting_at(n + 8) >= 0:
                 copy_kT(head_starting_at(n + 8))
             for pair in range(NTILES // 2):

@@ -204,7 +204,8 @@ def tile_rbfbias_kernel(tc, q, k, v, qs_s, ks_s, alpha, beta, out):
         def new_dist(sweep):
             dist[sweep] = dists.tile([P, NT, BANK], F32, name="dT", tag="dT")
 
-        def dist_of_tile(t, g, pool, tag):
+        def dist_of_tile(t, g):
+            pool, tag = (ps_w, "w") if t < 2 else (ps_t, "t")
             bank = pool.tile([P, PACK, P], F32, name="dps", tag=tag)
             for j in range(PACK):
                 c = g * PACK + j
@@ -368,21 +369,18 @@ def tile_rbfbias_kernel(tc, q, k, v, qs_s, ks_s, alpha, beta, out):
                 in_=v_grouped[bh][:].rearrange("p g d j -> p (g d j)"),
             )
 
-        def bias_exp(pair):
-            u = pair * 2 // GROUP
+        def bias_exp(first, last):
+            u, pair = first // GROUP, first // 2
             sweep, h = u // H, u % H
-            first = (pair * 2 % GROUP) * P
-            bias[pair] = work3.tile([P, NT, 2 * P], F32, name="et", tag="et")
-            cuts = 2 if pair * 2 < GROUP else 1
-            width = 2 * P // cuts
-            for cut in range(cuts):
-                nc.scalar.activation(
-                    out=bias[pair][:, :, cut * width : (cut + 1) * width],
-                    in_=dist[sweep][:, :, first + cut * width : first + (cut + 1) * width],
-                    func=ACTF.Exp,
-                    scale=minus_beta[:, h : h + 1],
-                    bias=ln_height[:, h : h + 1],
-                )
+            if first % 2 == 0:
+                bias[pair] = work3.tile([P, NT, 2 * P], F32, name="et", tag="et")
+            nc.scalar.activation(
+                out=bias[pair][:, :, (first - 2 * pair) * P : (last - 2 * pair) * P],
+                in_=dist[sweep][:, :, (first - GROUP * u) * P : (last - GROUP * u) * P],
+                func=ACTF.Exp,
+                scale=minus_beta[:, h : h + 1],
+                bias=ln_height[:, h : h + 1],
+            )
 
         def scores(tile):
             u, rank = tile // GROUP, tile % GROUP
@@ -526,17 +524,16 @@ def tile_rbfbias_kernel(tc, q, k, v, qs_s, ks_s, alpha, beta, out):
                 in_=o_sb[u][:, lo:hi, :],
             )
 
-        for t in range(2):
+        for t in range(GROUP):
             for g in range(PASSES):
-                dist_of_tile(t, g, ps_w, "w")
-        signs()
-        transpose_k(0)
-        copy_kT(0)
-        transpose_q(0)
-        copy_qT(0)
-        for t in range(2, GROUP):
-            for g in range(PASSES):
-                dist_of_tile(t, g, ps_t, "t")
+                dist_of_tile(t, g)
+            bias_exp(t, t + 1)
+            if t == 1:
+                signs()
+                transpose_k(0)
+                copy_kT(0)
+                transpose_q(0)
+                copy_qT(0)
 
         def is_tile(x):
             return 0 <= x < NTILES
@@ -587,9 +584,9 @@ def tile_rbfbias_kernel(tc, q, k, v, qs_s, ks_s, alpha, beta, out):
                 invert_sums(group_ending_at(n - 4))
             if head_starting_at(n + 8) >= 0:
                 copy_kT(head_starting_at(n + 8))
-            for pair in range(NTILES // 2):
+            for pair in range(GROUP // 2, NTILES // 2):
                 if bias_period(pair) == n:
-                    bias_exp(pair)
+                    bias_exp(2 * pair, 2 * pair + 2)
             if is_tile(n - 2) and n - 2 < NTILES - 2 and on_scalar(n - 2):
                 group_e(n - 2, True)
             if group_starting_at(n + 6) >= 0:

@@ -34,7 +34,7 @@ NGROUPS = NTILES // GROUP
 CATCH_UP = 7
 RAWB = 3
 HEADS_KEPT = 9
-FIRST_STEP = 24
+FIRST_STEP = 20
 FIRST_SUMMED_CHUNK = 1
 
 
@@ -46,6 +46,7 @@ def tile_rbfbias_kernel(tc, q, k, v, qs_s, ks_s, alpha, beta, out):
         small = ctx.enter_context(tc.tile_pool(name="small", bufs=4))
         raw = ctx.enter_context(tc.tile_pool(name="raw", bufs=RAWB))
         kept = ctx.enter_context(tc.tile_pool(name="kept", bufs=HEADS_KEPT))
+        kept_v = ctx.enter_context(tc.tile_pool(name="kept_v", bufs=H // 2 + 1))
         work2 = ctx.enter_context(tc.tile_pool(name="work2", bufs=2))
         work3 = ctx.enter_context(tc.tile_pool(name="work3", bufs=3))
         work4 = ctx.enter_context(tc.tile_pool(name="work4", bufs=4))
@@ -121,9 +122,11 @@ def tile_rbfbias_kernel(tc, q, k, v, qs_s, ks_s, alpha, beta, out):
         tiny = const.tile([P, 1], F32, name="tiny")
         nc.vector.memset(tiny[:], 2.0 ** -60)
         feat_k = const.tile([P, NT, P], BF16, name="feat_k")
-        feat_q = [const.tile([P, GROUP, P], BF16, name="feat_q%d" % half) for half in range(HALVES)]
+        feat_q = const.tile([P, GROUP, P], BF16, name="feat_q")
         nc.vector.memset(feat_k[:], 0.0)
         nc.vector.memset(feat_k[:, :, 3:9], 1.0)
+        nc.vector.memset(feat_q[:], 0.0)
+        nc.vector.memset(feat_q[:, :, 9:15], 1.0)
         squares = [const.tile([P, 2, NT, NF], F32, name="sq%d" % b) for b in range(B)]
 
         def by_tile(b):
@@ -131,10 +134,6 @@ def tile_rbfbias_kernel(tc, q, k, v, qs_s, ks_s, alpha, beta, out):
 
         def square_positions(b):
             nc.vector.tensor_tensor(out=squares[b][:], in0=by_tile(b), in1=by_tile(b), op=ALU.mult)
-
-        def clear_query_features(half):
-            nc.vector.memset(feat_q[half][:], 0.0)
-            nc.vector.memset(feat_q[half][:, :, 9:15], 1.0)
 
         def key_features(b):
             sq = squares[b][:, 1]
@@ -144,21 +143,21 @@ def tile_rbfbias_kernel(tc, q, k, v, qs_s, ks_s, alpha, beta, out):
 
         def query_features(b, half):
             tiles = slice(half * GROUP, (half + 1) * GROUP)
-            sq, feat = squares[b][:, 0, tiles], feat_q[half]
-            nc.vector.tensor_copy(out=feat[:, :, 3:6], in_=sq)
+            sq = squares[b][:, 0, tiles]
+            nc.vector.tensor_copy(out=feat_q[:, :, 3:6], in_=sq)
             nc.vector.tensor_scalar(
-                out=feat[:, :, 0:3], in0=by_tile(b)[:, 0, tiles], scalar1=-2.0, scalar2=None, op0=ALU.mult
+                out=feat_q[:, :, 0:3], in0=by_tile(b)[:, 0, tiles], scalar1=-2.0, scalar2=None, op0=ALU.mult
             )
-            nc.vector.tensor_tensor(out=feat[:, :, 6:9], in0=sq, in1=feat[:, :, 3:6], op=ALU.subtract)
+            nc.vector.tensor_tensor(out=feat_q[:, :, 6:9], in0=sq, in1=feat_q[:, :, 3:6], op=ALU.subtract)
 
-        clear_query_features(0)
         square_positions(0)
         query_features(0, 0)
         key_features(0)
-        clear_query_features(1)
 
         ln_height = const.tile([P, H], F32, name="lna")
         height = const.tile([P, H], F32, name="absa")
+        table_load = const.tile([P, 1], F32, name="load")
+        nc.scalar.activation(out=table_load[:], in_=tiny[:], func=ACTF.Ln)
         nc.scalar.activation(out=height[:], in_=alpha_bf[:], func=ACTF.Abs, scale=math.sqrt(D))
         nc.scalar.activation(out=ln_height[:], in_=height[:], func=ACTF.Ln, bias=tiny[:])
         table_change = const.tile([P, 1], F32, name="warm")
@@ -184,15 +183,17 @@ def tile_rbfbias_kernel(tc, q, k, v, qs_s, ks_s, alpha, beta, out):
             bank = ps_t.tile([P, PACK, P], BF16, name="fb", tag="t")
             for j in range(PACK):
                 nc.tensor.transpose(out=bank[:, j, :], in_=feat_k[:, g * PACK + j, :], identity=ident_bf[:])
-            nc.vector.tensor_copy(
-                out=feat_kT[b][:, g * BANK : (g + 1) * BANK], in_=bank[:].rearrange("p t c -> p (t c)")
-            )
+            dst, src = feat_kT[b][:, g * BANK : (g + 1) * BANK], bank[:].rearrange("p t c -> p (t c)")
+            if b == 0 and g > 0:
+                nc.scalar.copy(out=dst, in_=src)
+            else:
+                nc.vector.tensor_copy(out=dst, in_=src)
 
         def transpose_query_features(b, half):
             feat_qT[b, half] = const.tile([P, GROUP * P], BF16, name="feat_qT%d_%d" % (b, half))
             bank = ps_t.tile([P, GROUP, P], BF16, name="fb", tag="t")
             for t in range(GROUP):
-                nc.tensor.transpose(out=bank[:, t, :], in_=feat_q[half][:, t, :], identity=ident_bf[:])
+                nc.tensor.transpose(out=bank[:, t, :], in_=feat_q[:, t, :], identity=ident_bf[:])
             nc.vector.tensor_copy(out=feat_qT[b, half][:], in_=bank[:].rearrange("p t c -> p (t c)"))
 
         transpose_query_features(0, 0)
@@ -350,9 +351,10 @@ def tile_rbfbias_kernel(tc, q, k, v, qs_s, ks_s, alpha, beta, out):
             nc.vector.tensor_copy(out=kT[bh][:], in_=t_bank["k", bh][:].rearrange("p t c -> p (t c)"))
 
         def group_v(bh):
-            v_grouped[bh] = work2.tile([P, PASSES, D, PACK], BF16, name="vg", tag="vg", align_bytes=64)
+            if bh % 2 == 0:
+                v_grouped[bh // 2] = work2.tile([P, 2, PASSES, D, PACK], BF16, name="vg", tag="vg", align_bytes=64)
             nc.gpsimd.tensor_scalar(
-                out=v_grouped[bh][:],
+                out=v_grouped[bh // 2][:, bh % 2],
                 in0=v_raw[bh][:].rearrange("p g j d -> p g d j"),
                 scalar1=1.0,
                 scalar2=0.0,
@@ -360,13 +362,13 @@ def tile_rbfbias_kernel(tc, q, k, v, qs_s, ks_s, alpha, beta, out):
                 op1=ALU.add,
             )
 
-        def quantise_v(bh):
-            v_codes[bh] = kept.tile([P, PASSES * D], U32, name="vc", tag="vc", align_bytes=64)
-            v_scales[bh] = kept.tile([P, PASSES * D], U8, name="vs", tag="vs", align_bytes=64)
+        def quantise_v(pair):
+            v_codes[pair] = kept_v.tile([P, 2 * PASSES * D], U32, name="vc", tag="vc", align_bytes=64)
+            v_scales[pair] = kept_v.tile([P, 2 * PASSES * D], U8, name="vs", tag="vs", align_bytes=64)
             nc.vector.quantize_mx(
-                out=v_codes[bh][:].bitcast(FP8X4),
-                scales=v_scales[bh][:],
-                in_=v_grouped[bh][:].rearrange("p g d j -> p (g d j)"),
+                out=v_codes[pair][:].bitcast(FP8X4),
+                scales=v_scales[pair][:],
+                in_=v_grouped[pair][:].rearrange("p h g d j -> p (h g d j)"),
             )
 
         def bias_exp(first, last):
@@ -492,6 +494,7 @@ def tile_rbfbias_kernel(tc, q, k, v, qs_s, ks_s, alpha, beta, out):
         def multiply_tile(tile):
             u, rank = tile // GROUP, tile % GROUP
             bh = head_of(u)
+            first = bh % 2 * PASSES * D
             if rank == 0:
                 o_bank[u] = ps_t.tile([P, GROUP, D], F32, name="ob", tag="t")
             for g in range(PASSES):
@@ -499,8 +502,8 @@ def tile_rbfbias_kernel(tc, q, k, v, qs_s, ks_s, alpha, beta, out):
                     out=o_bank[u][:, rank, :],
                     lhsT=e_codes[u][:, rank, g * P : (g + 1) * P].bitcast(FP8X4),
                     lhsT_scale=e_scales[u][:, rank, g * P : (g + 1) * P],
-                    rhs=v_codes[bh][:, g * D : (g + 1) * D].bitcast(FP8X4),
-                    rhs_scale=v_scales[bh][:, g * D : (g + 1) * D],
+                    rhs=v_codes[bh // 2][:, first + g * D : first + (g + 1) * D].bitcast(FP8X4),
+                    rhs_scale=v_scales[bh // 2][:, first + g * D : first + (g + 1) * D],
                     start=(g == 0),
                     stop=(g == PASSES - 1),
                 )
@@ -593,13 +596,14 @@ def tile_rbfbias_kernel(tc, q, k, v, qs_s, ks_s, alpha, beta, out):
                 copy_qT(group_starting_at(n + 6))
             if is_tile(n + 3) and n + 3 < NTILES - 1:
                 row_max(n + 3, 1)
-            if n == 3 or head_starting_at(n - 3) >= 0:
-                quantise_v(0 if n == 3 else head_starting_at(n - 3))
+            prepared = head_starting_at(n - 3)
+            if prepared >= 0 and prepared % 2 == 1:
+                quantise_v(prepared // 2)
             if group_ending_at(n - 3) >= 0:
                 quantise_group(group_ending_at(n - 3))
             if rank == 0 and is_tile(n - 2) and not on_scalar(n - 2):
                 group_e(n - 2, False)
-            if n == FIRST_STEP:
+            if n == FIRST_STEP + GROUP:
                 new_dist(SWEEPS - 1)
             steps = 0 if n % GROUP == 2 or n < FIRST_STEP else 1
             for step, args in dist_steps[0:steps]:
@@ -627,13 +631,13 @@ def tile_rbfbias_kernel(tc, q, k, v, qs_s, ks_s, alpha, beta, out):
             if n == 15:
                 for g in range(PASSES):
                     transpose_key_features(1, g)
-            if n == 19:
+            if n == 16:
                 query_features(1, 0)
+            if n == 19:
+                transpose_query_features(1, 0)
             if n == 20:
                 query_features(1, 1)
             if n == 23:
-                transpose_query_features(1, 0)
-            if n == 24:
                 transpose_query_features(1, 1)
 
         before, last = NGROUPS - 2, NGROUPS - 1

import math
from contextlib import ExitStack

import concourse.masks as masks
import concourse.mybir as mybir

FLOPS = 2 * 2 * 16 * 1024 * 1024 * 128

F32 = mybir.dt.float32
BF16 = mybir.dt.bfloat16
U32 = mybir.dt.uint32
U8 = mybir.dt.uint8
FP8X4 = mybir.dt.float8_e4m3fn_x4
ALU = mybir.AluOpType
ACTF = mybir.ActivationFunctionType
AX = mybir.AxisListType

P = 128
B = 2
H = 8
S = 1024
D = 128
NF = 3
NT = 8
BANK = 512
PACK = 4
PASSES = 2
WORD_BLOCKS = 4
GROUP = 4
HALVES = NT // GROUP
SWEEPS = B * HALVES
NTILES = B * H * NT
NGROUPS = NTILES // GROUP
CATCH_UP = 7
RAWB = 3
HEADS_KEPT = 9
FIRST_STEP = 20
FIRST_SUMMED_CHUNK = 1


def tile_rbfbias_kernel(tc, q, k, v, qs_s, ks_s, alpha, beta, out):
    nc = tc.nc
    scale = 1.0 / math.sqrt(D)
    with ExitStack() as ctx:
        const = ctx.enter_context(tc.tile_pool(name="const", bufs=1))
        small = ctx.enter_context(tc.tile_pool(name="small", bufs=4))
        raw = ctx.enter_context(tc.tile_pool(name="raw", bufs=RAWB))
        kept = ctx.enter_context(tc.tile_pool(name="kept", bufs=HEADS_KEPT))
        kept_v = ctx.enter_context(tc.tile_pool(name="kept_v", bufs=H // 2 + 1))
        work2 = ctx.enter_context(tc.tile_pool(name="work2", bufs=2))
        work3 = ctx.enter_context(tc.tile_pool(name="work3", bufs=3))
        work4 = ctx.enter_context(tc.tile_pool(name="work4", bufs=4))
        dists = ctx.enter_context(tc.tile_pool(name="dists", bufs=SWEEPS - 1))
        work6 = ctx.enter_context(tc.tile_pool(name="work6", bufs=6))
        ps_w = ctx.enter_context(tc.psum_pool(name="ps_w", bufs=4))
        ps_t = ctx.enter_context(tc.psum_pool(name="ps_t", bufs=4))
        ctx.enter_context(tc.manual_schedule())

        pos = [const.tile([P, 2, 32], BF16, name="pos%d" % b) for b in range(B)]

        def load_positions(b):
            nc.sync.dma_start(
                out=pos[b][:, 1, 0 : NT * NF].rearrange("p (g j f) -> p g j f", g=PASSES, f=NF),
                in_=ks_s[b].rearrange("(g p j) f -> p g j f", g=PASSES, j=PACK),
            )
            nc.sync.dma_start(
                out=pos[b][:, 0, 0 : NT * NF].rearrange("p (t f) -> p t f", f=NF),
                in_=qs_s[b].rearrange("(p t) f -> p t f", t=NT),
            )

        load_positions(0)
        alpha_bf = const.tile([P, H], BF16, name="al_bf")
        beta_bf = const.tile([P, H], BF16, name="be_bf")
        nc.sync.dma_start(out=alpha_bf[:], in_=alpha.rearrange("h o -> (h o)").partition_broadcast(P))
        nc.sync.dma_start(out=beta_bf[:], in_=beta.rearrange("h o -> (h o)").partition_broadcast(P))

        def place(u):
            return u // (HALVES * H), (u // H) % HALVES, u % H

        def head_of(u):
            b, half, h = place(u)
            return b * H + h

        q_raw = {}
        k_raw = {}
        v_raw = {}

        def load(u):
            b, half, h = place(u)
            bh = head_of(u)
            q_raw[u] = raw.tile([P, GROUP, D], BF16, name="qr", tag="qr")
            nc.sync.dma_start(
                out=q_raw[u][:],
                in_=q[b, h].rearrange("(p t) d -> p t d", t=NT)[:, half * GROUP : (half + 1) * GROUP, :],
            )
            if half > 0:
                return
            k_raw[bh] = raw.tile([P, PASSES, PACK, D], BF16, name="kr", tag="kr")
            nc.sync.dma_start(
                out=k_raw[bh][:], in_=k[b, h].rearrange("(g p j) d -> p g j d", g=PASSES, j=PACK)
            )
            v_raw[bh] = raw.tile([P, PASSES, PACK, D], BF16, name="vr", tag="vr")
            nc.sync.dma_start(
                out=v_raw[bh][:], in_=v[b, h].rearrange("(g p j) d -> p g j d", g=PASSES, j=PACK)
            )

        load(0)
        load(1)
        x_row = const.tile([P, S * NF], BF16, name="xrow")
        nc.sync.dma_start(out=x_row[:], in_=qs_s[1].rearrange("k f -> (k f)").partition_broadcast(P))
        load_positions(1)
        for u in range(2, RAWB):
            load(u)

        ident_bf = const.tile([P, P], BF16, name="ident_bf")
        masks.make_identity(nc, ident_bf[:])
        ident_f = const.tile([P, P], F32, name="ident_f")
        masks.make_identity(nc, ident_f[:])

        minus_one = const.tile([P, GROUP], F32, name="m1")
        nc.vector.memset(minus_one[:], -1.0)
        tiny = const.tile([P, 1], F32, name="tiny")
        nc.vector.memset(tiny[:], 2.0 ** -60)
        feat_k = const.tile([P, NT, P], BF16, name="feat_k")
        feat_q = const.tile([P, GROUP, P], BF16, name="feat_q")
        nc.vector.memset(feat_k[:], 0.0)
        nc.vector.memset(feat_k[:, :, 3:9], 1.0)
        nc.vector.memset(feat_q[:], 0.0)
        nc.vector.memset(feat_q[:, :, 9:15], 1.0)
        squares = [const.tile([P, 2, NT, NF], F32, name="sq%d" % b) for b in range(B)]

        def by_tile(b):
            return pos[b][:, :, 0 : NT * NF].rearrange("p w (t f) -> p w t f", f=NF)

        def square_positions(b):
            nc.vector.tensor_tensor(out=squares[b][:], in0=by_tile(b), in1=by_tile(b), op=ALU.mult)

        def key_features(b):
            sq = squares[b][:, 1]
            nc.vector.tensor_copy(out=feat_k[:, :, 9:12], in_=sq)
            nc.vector.tensor_copy(out=feat_k[:, :, 0:3], in_=by_tile(b)[:, 1])
            nc.vector.tensor_tensor(out=feat_k[:, :, 12:15], in0=sq, in1=feat_k[:, :, 9:12], op=ALU.subtract)

        def query_features(b, half):
            tiles = slice(half * GROUP, (half + 1) * GROUP)
            sq = squares[b][:, 0, tiles]
            nc.vector.tensor_copy(out=feat_q[:, :, 3:6], in_=sq)
            nc.vector.tensor_scalar(
                out=feat_q[:, :, 0:3], in0=by_tile(b)[:, 0, tiles], scalar1=-2.0, scalar2=None, op0=ALU.mult
            )
            nc.vector.tensor_tensor(out=feat_q[:, :, 6:9], in0=sq, in1=feat_q[:, :, 3:6], op=ALU.subtract)

        square_positions(0)
        query_features(0, 0)
        key_features(0)

        ln_height = const.tile([P, H], F32, name="lna")
        height = const.tile([P, H], F32, name="absa")
        table_load = const.tile([P, 1], F32, name="load")
        nc.scalar.activation(out=table_load[:], in_=tiny[:], func=ACTF.Ln)
        nc.scalar.activation(out=height[:], in_=alpha_bf[:], func=ACTF.Abs, scale=math.sqrt(D))
        nc.scalar.activation(out=ln_height[:], in_=height[:], func=ACTF.Ln, bias=tiny[:])
        table_change = const.tile([P, 1], F32, name="warm")
        nc.scalar.activation(out=table_change[:], in_=ln_height[:, 0:1], func=ACTF.Exp)
        minus_beta = const.tile([P, H], F32, name="nbeta")
        nc.vector.tensor_scalar(out=minus_beta[:], in0=beta_bf[:], scalar1=-1.0, scalar2=None, op0=ALU.mult)
        sign = const.tile([P, H], F32, name="sgn")
        to_minus_z = const.tile([P, H], F32, name="scneg")

        def signs():
            nc.vector.tensor_scalar(
                out=sign[:], in0=alpha_bf[:], scalar1=0.0, scalar2=2.0, op0=ALU.is_ge, op1=ALU.mult
            )
            nc.vector.tensor_scalar(out=sign[:], in0=sign[:], scalar1=-1.0, scalar2=None, op0=ALU.add)
            nc.vector.tensor_scalar(out=to_minus_z[:], in0=sign[:], scalar1=-scale, scalar2=None, op0=ALU.mult)

        feat_kT = {}
        feat_qT = {}

        def transpose_key_features(b, g):
            if g == 0:
                feat_kT[b] = const.tile([P, NT * P], BF16, name="feat_kT%d" % b)
            bank = ps_t.tile([P, PACK, P], BF16, name="fb", tag="t")
            for j in range(PACK):
                nc.tensor.transpose(out=bank[:, j, :], in_=feat_k[:, g * PACK + j, :], identity=ident_bf[:])
            dst, src = feat_kT[b][:, g * BANK : (g + 1) * BANK], bank[:].rearrange("p t c -> p (t c)")
            if b == 0 and g > 0:
                nc.scalar.copy(out=dst, in_=src)
            else:
                nc.vector.tensor_copy(out=dst, in_=src)

        def transpose_query_features(b, half):
            feat_qT[b, half] = const.tile([P, GROUP * P], BF16, name="feat_qT%d_%d" % (b, half))
            bank = ps_t.tile([P, GROUP, P], BF16, name="fb", tag="t")
            for t in range(GROUP):
                nc.tensor.transpose(out=bank[:, t, :], in_=feat_q[:, t, :], identity=ident_bf[:])
            nc.vector.tensor_copy(out=feat_qT[b, half][:], in_=bank[:].rearrange("p t c -> p (t c)"))

        transpose_query_features(0, 0)
        for g in range(PASSES):
            transpose_key_features(0, g)

        dist = {}

        def new_dist(sweep):
            dist[sweep] = dists.tile([P, NT, BANK], F32, name="dT", tag="dT")

        def dist_of_tile(t, g):
            pool, tag = (ps_w, "w") if t < 2 else (ps_t, "t")
            bank = pool.tile([P, PACK, P], F32, name="dps", tag=tag)
            for j in range(PACK):
                c = g * PACK + j
                nc.tensor.matmul(
                    out=bank[:, j, :],
                    lhsT=feat_kT[0][:, c * P : (c + 1) * P],
                    rhs=feat_qT[0, 0][:, t * P : (t + 1) * P],
                    start=True,
                    stop=True,
                )
            dst = dist[0][:, g * PACK : (g + 1) * PACK, t * P : (t + 1) * P]
            if t > 0 and g > 0:
                nc.scalar.copy(out=dst, in_=bank[:])
            else:
                nc.vector.tensor_copy(out=dst, in_=bank[:])

        dist_bank = {}

        def fill_dist_bank(sweep, c):
            b, half = sweep // HALVES, sweep % HALVES
            dist_bank[sweep, c] = ps_t.tile([P, BANK], F32, name="dps", tag="t")
            nc.tensor.matmul(
                out=dist_bank[sweep, c][:],
                lhsT=feat_kT[b][:, c * P : (c + 1) * P],
                rhs=feat_qT[b, half][:],
                start=True,
                stop=True,
            )

        def empty_dist_bank(sweep, c):
            nc.vector.tensor_copy(out=dist[sweep][:, c, :], in_=dist_bank[sweep, c][:])

        for sweep in range(SWEEPS - 1):
            new_dist(sweep)

        key_norm = const.tile([P, NT], F32, name="y2")
        minus_2y = const.tile([P, NT * NF], F32, name="m2y")

        def key_scalars():
            nc.vector.tensor_reduce(out=key_norm[:], in_=squares[1][:, 1], axis=AX.X, op=ALU.add)
            nc.vector.tensor_scalar(
                out=minus_2y[:], in0=pos[1][:, 1, 0 : NT * NF], scalar1=-2.0, scalar2=None, op0=ALU.mult
            )

        x_planes = const.tile([P, NF, BANK], BF16, name="xp")
        x_norm = const.tile([P, BANK], F32, name="xn")
        parts = {}

        def split_features():
            nc.gpsimd.tensor_scalar(
                out=x_planes[:].rearrange("x f (t p) -> x f t p", t=GROUP),
                in0=x_row[:].rearrange("x (p t f) -> x f t p", t=NT, f=NF)[:, :, NT - GROUP : NT, :],
                scalar1=1.0,
                scalar2=0.0,
                op0=ALU.mult,
                op1=ALU.add,
            )

        def square_feature(f):
            if f == 0:
                out = x_norm
            else:
                parts["x", f] = out = work2.tile([P, BANK], F32, name="dp", tag="dp")
            nc.gpsimd.tensor_tensor(out=out[:], in0=x_planes[:, f], in1=x_planes[:, f], op=ALU.mult)

        def add_square(f):
            nc.gpsimd.tensor_tensor(out=x_norm[:], in0=x_norm[:], in1=parts["x", f][:], op=ALU.add)

        def product(c, f):
            parts[c, f] = work3.tile([P, BANK], F32, name="ds", tag="ds")
            nc.gpsimd.tensor_scalar(
                out=parts[c, f][:],
                in0=x_planes[:, f],
                scalar1=minus_2y[:, c * NF + f : c * NF + f + 1],
                scalar2=(key_norm[:, c : c + 1] if f == 0 else 0.0),
                op0=ALU.mult,
                op1=ALU.add,
            )

        def add_product(c, f):
            nc.gpsimd.tensor_tensor(out=parts[c, 0][:], in0=parts[c, 0][:], in1=parts[c, f][:], op=ALU.add)

        def add_norm(c):
            nc.gpsimd.tensor_tensor(
                out=dist[SWEEPS - 1][:, c, :], in0=parts[c, 0][:], in1=x_norm[:], op=ALU.add
            )

        dist_steps = [(split_features, ())]
        dist_steps.extend([(square_feature, (f,)) for f in range(NF)])
        dist_steps.extend([(add_square, (f,)) for f in range(1, NF)])
        for c in range(FIRST_SUMMED_CHUNK, NT):
            dist_steps.extend([(product, (c, f)) for f in range(NF)])
            dist_steps.extend([(add_product, (c, f)) for f in range(1, NF)])
            dist_steps.append((add_norm, (c,)))

        t_bank = {}
        qT = {}
        kT = {}
        v_grouped = {}
        v_codes = {}
        v_scales = {}
        bias = {}
        w_banks = {}
        minus_z = {}
        minus_max_half = {}
        minus_max = {}
        row_sums = {}
        e_sb = {}
        eT_bank = {}
        e_grouped = {}
        e_codes = {}
        e_scales = {}
        inv_sums = {}
        o_bank = {}
        o_sb = {}

        def transpose_q(u):
            t_bank[u] = ps_t.tile([P, GROUP, P], BF16, name="tq", tag="t")
            for t in range(GROUP):
                nc.tensor.transpose(out=t_bank[u][:, t, :], in_=q_raw[u][:, t, :], identity=ident_bf[:])

        def copy_qT(u):
            h = u % H
            qT[u] = work3.tile([P, GROUP * P], BF16, name="qT", tag="qT")
            nc.vector.tensor_scalar(
                out=qT[u][:],
                in0=t_bank[u][:].rearrange("p t c -> p (t c)"),
                scalar1=sign[:, h : h + 1],
                scalar2=None,
                op0=ALU.mult,
            )

        def transpose_k(bh):
            t_bank["k", bh] = ps_t.tile([P, NT, P], BF16, name="tq", tag="t")
            for c in range(NT):
                nc.tensor.transpose(
                    out=t_bank["k", bh][:, c, :], in_=k_raw[bh][:, c // PACK, c % PACK, :], identity=ident_bf[:]
                )

        def copy_kT(bh):
            kT[bh] = kept.tile([P, NT * P], BF16, name="kT", tag="kT")
            nc.vector.tensor_copy(out=kT[bh][:], in_=t_bank["k", bh][:].rearrange("p t c -> p (t c)"))

        def group_v(bh):
            if bh % 2 == 0:
                v_grouped[bh // 2] = work2.tile([P, 2, PASSES, D, PACK], BF16, name="vg", tag="vg", align_bytes=64)
            nc.gpsimd.tensor_scalar(
                out=v_grouped[bh // 2][:, bh % 2],
                in0=v_raw[bh][:].rearrange("p g j d -> p g d j"),
                scalar1=1.0,
                scalar2=0.0,
                op0=ALU.mult,
                op1=ALU.add,
            )

        def quantise_v(pair):
            v_codes[pair] = kept_v.tile([P, 2 * PASSES * D], U32, name="vc", tag="vc", align_bytes=64)
            v_scales[pair] = kept_v.tile([P, 2 * PASSES * D], U8, name="vs", tag="vs", align_bytes=64)
            nc.vector.quantize_mx(
                out=v_codes[pair][:].bitcast(FP8X4),
                scales=v_scales[pair][:],
                in_=v_grouped[pair][:].rearrange("p h g d j -> p (h g d j)"),
            )

        def bias_exp(first, last):
            u, pair = first // GROUP, first // 2
            sweep, h = u // H, u % H
            if first % 2 == 0:
                bias[pair] = work3.tile([P, NT, 2 * P], F32, name="et", tag="et")
            nc.scalar.activation(
                out=bias[pair][:, :, (first - 2 * pair) * P : (last - 2 * pair) * P],
                in_=dist[sweep][:, :, (first - GROUP * u) * P : (last - GROUP * u) * P],
                func=ACTF.Exp,
                scale=minus_beta[:, h : h + 1],
                bias=ln_height[:, h : h + 1],
            )

        def scores(tile):
            u, rank = tile // GROUP, tile % GROUP
            w_banks[tile] = []
            for g in range(PASSES):
                bank = ps_w.tile([P, BANK], F32, name="wg", tag="w")
                nc.tensor.matmul(
                    out=bank[:],
                    lhsT=qT[u][:, rank * P : (rank + 1) * P],
                    rhs=kT[head_of(u)][:, g * BANK : (g + 1) * BANK],
                    start=True,
                    stop=False,
                )
                w_banks[tile].append(bank)
                for j in range(PACK):
                    nc.tensor.matmul(
                        out=w_banks[tile][g][:, j * P : (j + 1) * P],
                        lhsT=bias[tile // 2][:, g * PACK + j, (tile % 2) * P : (tile % 2 + 1) * P],
                        rhs=ident_f[:],
                        is_transpose=True,
                        start=False,
                        stop=(j == PACK - 1),
                    )

        def row_max(tile, g):
            h = (tile // GROUP) % H
            if g == 0:
                minus_z[tile] = work6.tile([P, S], F32, name="zt", tag="zt")
                minus_max_half[tile] = work6.tile([P, PASSES], F32, name="nb0", tag="nb0")
            nc.vector.tensor_scalar(
                out=minus_z[tile][:, g * BANK : (g + 1) * BANK],
                in0=w_banks[tile][g][:],
                scalar1=to_minus_z[:, h : h + 1],
                scalar2=None,
                op0=ALU.mult,
                op1=ALU.min,
                accum_out=minus_max_half[tile][:, g : g + 1],
            )
            if g == PASSES - 1:
                minus_max[tile] = work6.tile([P, 1], F32, name="nb", tag="nb")
                nc.gpsimd.tensor_scalar(
                    out=minus_max[tile][:],
                    in0=minus_max_half[tile][:, 0:1],
                    scalar1=minus_max_half[tile][:, 1:2],
                    scalar2=None,
                    op0=ALU.min,
                )

        def softmax_exp(tile):
            u, rank = tile // GROUP, tile % GROUP
            if rank == 0:
                row_sums[u] = small.tile([P, GROUP], F32, name="rs", tag="rs")
            e_sb[tile] = work4.tile([P, S], BF16, name="ee", tag="ee")
            nc.scalar.activation(
                out=e_sb[tile][:].rearrange("q (a p e) -> q a p e", a=WORD_BLOCKS, e=2),
                in_=minus_z[tile][:].rearrange("q (a e p) -> q a p e", a=WORD_BLOCKS, e=2),
                func=ACTF.Exp,
                scale=-1.0,
                bias=minus_max[tile][:],
                accum_out=row_sums[u][:, rank : rank + 1],
            )

        def transpose_e(tile):
            eT_bank[tile] = ps_t.tile([P, WORD_BLOCKS, P], F32, name="eT", tag="t")
            words = e_sb[tile][:].bitcast(F32)
            for a in range(WORD_BLOCKS):
                nc.tensor.transpose(
                    out=eT_bank[tile][:, a, :], in_=words[:, a * P : (a + 1) * P], identity=ident_f[:]
                )

        def group_e(tile, on_scalar):
            u, rank = tile // GROUP, tile % GROUP
            if rank == 0:
                e_grouped[u] = work2.tile([P, GROUP, PASSES, P, PACK], BF16, name="g4", tag="g4", align_bytes=64)
            dst = e_grouped[u][:, rank].bitcast(F32)
            src = eT_bank[tile][:].rearrange("p (g u) q -> p g q u", u=2)
            if on_scalar:
                nc.scalar.copy(out=dst, in_=src)
            else:
                nc.vector.tensor_copy(out=dst, in_=src)

        def quantise_group(u):
            e_codes[u] = work2.tile([P, GROUP, PASSES * P], U32, name="ec", tag="ec", align_bytes=64)
            e_scales[u] = work2.tile([P, GROUP, PASSES * P], U8, name="es", tag="es", align_bytes=64)
            nc.vector.quantize_mx(
                out=e_codes[u][:].rearrange("p i w -> p (i w)").bitcast(FP8X4),
                scales=e_scales[u][:].rearrange("p i w -> p (i w)"),
                in_=e_grouped[u][:].rearrange("p i g c j -> p (i g c j)"),
            )

        def quantise_tile(tile):
            u, rank = tile // GROUP, tile % GROUP
            if rank == 0:
                e_codes[u] = work2.tile([P, GROUP, PASSES * P], U32, name="ec", tag="ec", align_bytes=64)
                e_scales[u] = work2.tile([P, GROUP, PASSES * P], U8, name="es", tag="es", align_bytes=64)
            nc.vector.quantize_mx(
                out=e_codes[u][:, rank, :].bitcast(FP8X4),
                scales=e_scales[u][:, rank, :],
                in_=e_grouped[u][:, rank].rearrange("p g c j -> p (g c j)"),
            )

        def invert_sums(u):
            inv_sums[u] = small.tile([P, GROUP], F32, name="rinv", tag="rinv")
            if u == NGROUPS - 1:
                nc.vector.reciprocal(out=inv_sums[u][:], in_=row_sums[u][:])
                return
            nc.gpsimd.tensor_tensor(out=inv_sums[u][:], in0=row_sums[u][:], in1=minus_one[:], op=ALU.pow)

        def multiply_tile(tile):
            u, rank = tile // GROUP, tile % GROUP
            bh = head_of(u)
            first = bh % 2 * PASSES * D
            if rank == 0:
                o_bank[u] = ps_t.tile([P, GROUP, D], F32, name="ob", tag="t")
            for g in range(PASSES):
                nc.tensor.matmul_mx(
                    out=o_bank[u][:, rank, :],
                    lhsT=e_codes[u][:, rank, g * P : (g + 1) * P].bitcast(FP8X4),
                    lhsT_scale=e_scales[u][:, rank, g * P : (g + 1) * P],
                    rhs=v_codes[bh // 2][:, first + g * D : first + (g + 1) * D].bitcast(FP8X4),
                    rhs_scale=v_scales[bh // 2][:, first + g * D : first + (g + 1) * D],
                    start=(g == 0),
                    stop=(g == PASSES - 1),
                )

        def multiply_group(u):
            for rank in range(GROUP):
                multiply_tile(u * GROUP + rank)

        def normalise(u, lo, hi):
            b, half, h = place(u)
            if lo == 0:
                o_sb[u] = work2.tile([P, GROUP, D], F32, name="osb", tag="osb")
            nc.vector.tensor_tensor(
                out=o_sb[u][:, lo:hi, :],
                in0=o_bank[u][:, lo:hi, :],
                in1=inv_sums[u][:, lo:hi].unsqueeze(2).to_broadcast([P, hi - lo, D]),
                op=ALU.mult,
            )
            nc.sync.dma_start(
                out=out[b, h].rearrange("(p t) d -> p t d", t=NT)[:, half * GROUP + lo : half * GROUP + hi, :],
                in_=o_sb[u][:, lo:hi, :],
            )

        for t in range(GROUP):
            for g in range(PASSES):
                dist_of_tile(t, g)
            bias_exp(t, t + 1)
            if t == 1:
                signs()
                transpose_k(0)
                copy_kT(0)
                transpose_q(0)
                copy_qT(0)

        def is_tile(x):
            return 0 <= x < NTILES

        def group_ending_at(x):
            return x // GROUP if (x % GROUP == GROUP - 1 and is_tile(x)) else -1

        def group_starting_at(x):
            return x // GROUP if (x % GROUP == 0 and GROUP <= x < NTILES) else -1

        def head_starting_at(x):
            u = group_starting_at(x)
            return head_of(u) if (u >= 0 and place(u)[1] == 0) else -1

        def on_scalar(tile):
            u, rank = tile // GROUP, tile % GROUP
            return rank == 0 or (rank == 2 and place(u)[1] == 0 and u % 2 == 0)

        def bias_period(pair):
            return 2 * pair - 5 if pair < CATCH_UP else 2 * pair - 7

        bank_periods = list(range(NT)) + [n for n in range(H * GROUP, NTILES) if n % GROUP in (0, 3)]
        banks = [(1, c) for c in range(NT)] + [(2, c) for c in range(NT)]
        banks += [(SWEEPS - 1, c) for c in range(FIRST_SUMMED_CHUNK)]
        bank_of_period = dict(zip(bank_periods, banks))

        for n in range(-5, NTILES - 2):
            rank = (n - 2) % GROUP
            if is_tile(n + 4):
                scores(n + 4)
            if n in bank_of_period:
                fill_dist_bank(*bank_of_period[n])
            if is_tile(n):
                softmax_exp(n)
            if is_tile(n - 1):
                transpose_e(n - 1)
            if group_ending_at(n - 5) >= 0:
                multiply_group(group_ending_at(n - 5))
            if is_tile(n + 3):
                row_max(n + 3, 0)
            if n + 3 == NTILES - 1:
                row_max(n + 3, 1)
            if rank != 0 and is_tile(n - 2) and n - 2 < NTILES - 2 and not on_scalar(n - 2):
                group_e(n - 2, False)
            if group_ending_at(n - 6) >= 0:
                normalise(group_ending_at(n - 6), 0, GROUP)
            if group_ending_at(n - 4) >= 0:
                invert_sums(group_ending_at(n - 4))
            if head_starting_at(n + 8) >= 0:
                copy_kT(head_starting_at(n + 8))
            for pair in range(GROUP // 2, NTILES // 2):
                if bias_period(pair) == n:
                    bias_exp(2 * pair, 2 * pair + 2)
            if is_tile(n - 2) and n - 2 < NTILES - 2 and on_scalar(n - 2):
                group_e(n - 2, True)
            if group_starting_at(n + 6) >= 0:
                copy_qT(group_starting_at(n + 6))
            if is_tile(n + 3) and n + 3 < NTILES - 1:
                row_max(n + 3, 1)
            prepared = head_starting_at(n - 3)
            if prepared >= 0 and prepared % 2 == 1:
                quantise_v(prepared // 2)
            if group_ending_at(n - 3) >= 0:
                quantise_group(group_ending_at(n - 3))
            if rank == 0 and is_tile(n - 2) and not on_scalar(n - 2):
                group_e(n - 2, False)
            if n == FIRST_STEP + GROUP:
                new_dist(SWEEPS - 1)
            steps = 0 if n % GROUP == 2 or n < FIRST_STEP else 1
            for step, args in dist_steps[0:steps]:
                step(*args)
            dist_steps = dist_steps[steps:]
            if n == 0 or head_starting_at(n + 1) >= 0:
                group_v(0 if n == 0 else head_starting_at(n + 1))
            if group_starting_at(n + 7) >= 0:
                transpose_q(group_starting_at(n + 7))
            if head_starting_at(n + 9) >= 0:
                transpose_k(head_starting_at(n + 9))
            if n % GROUP == 0 and n >= 0 and n // GROUP + RAWB < NGROUPS:
                load(n // GROUP + RAWB)
            if n == -5:
                query_features(0, 1)
            if n == -4:
                transpose_query_features(0, 1)
            if n in bank_of_period:
                empty_dist_bank(*bank_of_period[n])
            if n == -2:
                square_positions(1)
                key_scalars()
            if n == 11:
                key_features(1)
            if n == 15:
                for g in range(PASSES):
                    transpose_key_features(1, g)
            if n == 16:
                query_features(1, 0)
            if n == 19:
                transpose_query_features(1, 0)
            if n == 20:
                query_features(1, 1)
            if n == 23:
                transpose_query_features(1, 1)

        before, last = NGROUPS - 2, NGROUPS - 1
        t0 = last * GROUP
        softmax_exp(t0 + 2)
        transpose_e(t0 + 1)
        group_e(t0, False)
        softmax_exp(t0 + 3)
        transpose_e(t0 + 2)
        quantise_group(before)
        multiply_group(before)
        group_e(t0 + 1, False)
        quantise_tile(t0)
        quantise_tile(t0 + 1)
        group_e(t0 + 2, True)
        transpose_e(t0 + 3)
        group_e(t0 + 3, True)
        multiply_tile(t0)
        multiply_tile(t0 + 1)
        invert_sums(before)
        normalise(before, 0, GROUP)
        invert_sums(last)
        quantise_tile(t0 + 2)
        multiply_tile(t0 + 2)
        normalise(last, 0, 2)
        quantise_tile(t0 + 3)
        multiply_tile(t0 + 3)
        normalise(last, 2, GROUP)
